import numpy as np
import ml_dtypes


def mxq(x, axis, fmt="e4m3"):
    dtype, down = {"e4m3": (ml_dtypes.float8_e4m3fn, 7), "e5m2": (ml_dtypes.float8_e5m2, 14)}[fmt]
    v = np.moveaxis(np.asarray(x, np.float32).astype(ml_dtypes.bfloat16).astype(np.float64), axis, -1)
    blocks = v.reshape(v.shape[:-1] + (-1, 32))
    amax = np.abs(blocks).max(-1, keepdims=True)
    byte = np.maximum(np.where(amax > 0, np.frexp(amax)[1] - 1 + 127, 0) - down, 1)
    scale = np.exp2(byte - 127.0)
    codes = (blocks / scale).astype(np.float32).astype(dtype).astype(np.float64)
    return np.moveaxis((codes * scale).reshape(v.shape), -1, axis)


WIDE = False


def mx_kscale(k):
    if not WIDE:
        return np.ones(k)
    levels = np.array([10, -10, 5, -5, 0])
    a = np.random.permutation(np.resize(levels, k // 512 * 4)).reshape(k // 512, 4)
    idx = np.arange(k)
    return np.exp2(a[idx // 512, idx % 128 // 32])


BF16 = ml_dtypes.bfloat16


def bf(x):
    return np.asarray(x, np.float32).astype(BF16)


def f64(x):
    return np.asarray(x).astype(np.float64)


B, J, C, K, H, M = 8, 128, 512, 4, 8, 256
DH = C // H
S_G2A, S_A2G = 0.5, 0.8


def setup_inputs():
    s = mx_kscale(C)
    return {'attn_o': bf(np.random.standard_normal((B, H, J, DH)) * 0.6 * s.reshape(H, 1, DH)),
            'xg1': bf(np.random.standard_normal((B, J, C)) * 0.7 * s),
            'x': bf(np.random.standard_normal((B, J, C))),
            'adj': bf(np.random.uniform(size=(K, J, J)) / np.sqrt(K * J)),
            'proj_w': bf(np.random.standard_normal((C, C)) / np.sqrt(C) / s),
            'proj_b': bf(0.1 * np.random.standard_normal(C)),
            'gcn2_w': bf(np.random.standard_normal((K * C, C)) * 1.5 / np.sqrt(C) / s),
            'gcn2_b': bf(np.random.standard_normal(K * C) * 0.6 / np.sqrt(J))}


def reference(attn_o, xg1, x, adj, proj_w, proj_b, gcn2_w, gcn2_b):
    o = f64(attn_o)
    g1 = f64(xg1)
    attn2gcn = o.transpose(0, 2, 1, 3).reshape(B, J, C)
    fh = (g1 * S_G2A).reshape(B, J, H, DH).transpose(0, 2, 1, 3)
    v = (o + fh).transpose(0, 2, 1, 3).reshape(B, J, C)
    xa = (mxq(v, 2, 'e4m3') @ mxq(f64(proj_w), 1, 'e4m3').T) + f64(proj_b)
    u = g1 + attn2gcn * S_A2G
    y = (mxq(u, 2, 'e4m3') @ mxq(f64(gcn2_w), 1, 'e4m3').T) + f64(gcn2_b)
    yk = y.reshape(B, J, K, C).transpose(0, 2, 1, 3).reshape(B, K * J, C)
    a = f64(adj).reshape(K * J, J)
    xg2 = mxq(a, 0, 'e4m3').T @ mxq(yk, 1, 'e4m3')
    return f64(x) + xg2 + xa

@@ -1,0 +1,236 @@
+from contextlib import ExitStack
+
+import concourse.mybir as mybir
+from concourse.masks import make_identity
+
+F32 = mybir.dt.float32
+BF16 = mybir.dt.bfloat16
+U32 = mybir.dt.uint32
+U8 = mybir.dt.uint8
+FP8X4 = mybir.dt.float8_e4m3fn_x4
+ADD = mybir.AluOpType.add
+MULT = mybir.AluOpType.mult
+
+P = 128
+PACK = 4
+B = 8
+C = 512
+KINDS = 4
+HEADS = 8
+HEAD_DIM = 64
+HALVES = 2
+PAIR = 2
+S_G2A = 0.5
+S_A2G = 0.8
+
+FLOPS = 2 * B * P * C * (C + KINDS * C) + 2 * B * P * (KINDS * P) * C
+
+
+def channels_to_partitions(nc, psum, ident, src_words, dst_words, first_block):
+    turned = psum.tile([P, PAIR, HALVES, P], F32, tag="turn")
+    for i in range(PAIR):
+        for h in range(HALVES):
+            nc.tensor.transpose(
+                turned[:, i, h, :],
+                src_words[:, first_block + i, h * P : (h + 1) * P],
+                ident[:],
+            )
+    nc.scalar.copy(
+        out=dst_words[:, first_block : first_block + PAIR, :, :],
+        in_=turned[:].rearrange("q i h r -> q i r h"),
+    )
+
+
+def tile_block_pb_kernel(
+    tc, attn_o, xg1, x, adj, proj_w, proj_b, gcn2_w, gcn2_b, out
+):
+    nc = tc.nc
+    with ExitStack() as ctx:
+        keep = ctx.enter_context(tc.tile_pool(name="keep", bufs=1))
+        work = ctx.enter_context(tc.tile_pool(name="work", bufs=3))
+        psum_turn = ctx.enter_context(tc.psum_pool(name="psum_turn", bufs=2))
+        psum_y = ctx.enter_context(tc.psum_pool(name="psum_y", bufs=4))
+        psum_out = ctx.enter_context(tc.psum_pool(name="psum_out", bufs=2))
+
+        ident_f32 = keep.tile([P, P], F32)
+        make_identity(nc, ident_f32[:])
+        ident_bf16 = keep.tile([P, P], BF16)
+        make_identity(nc, ident_bf16[:])
+
+        a_rows = keep.tile([P, B * C], BF16)
+        g_rows = keep.tile([P, B * C], BF16)
+        x_rows = keep.tile([P, B, C], BF16)
+        wg_rows = keep.tile([P, KINDS * KINDS * C], BF16)
+        wp_rows = keep.tile([P, KINDS * C], BF16)
+        adj_rows = keep.tile([P, KINDS, P], BF16)
+        bias_g = keep.tile([P, KINDS, C], BF16)
+        bias_p = keep.tile([P, C], BF16)
+
+        def load_streams(b0):
+            batches = slice(b0, b0 + PAIR)
+            nc.sync.dma_start(
+                out=a_rows[:].rearrange("j (bh d) -> j bh d", d=HEAD_DIM)[
+                    :, b0 * HEADS : (b0 + PAIR) * HEADS, :
+                ],
+                in_=attn_o.rearrange("b h j d -> (b h) j d")[
+                    b0 * HEADS : (b0 + PAIR) * HEADS
+                ].rearrange("bh j d -> j bh d"),
+            )
+            nc.sync.dma_start(
+                out=g_rows[:].rearrange("j (b c) -> j b c", c=C)[:, batches, :],
+                in_=xg1[batches].rearrange("b j c -> j b c"),
+            )
+
+        load_streams(0)
+        wg_dram = gcn2_w.rearrange("(k cb p) c -> cb p k c", k=KINDS, cb=KINDS)
+        wg_blocks = wg_rows[:].rearrange("p (cb k c) -> p cb k c", cb=KINDS, k=KINDS)
+        for cb in range(KINDS):
+            nc.sync.dma_start(out=wg_blocks[:, cb, :, :], in_=wg_dram[cb])
+        nc.sync.dma_start(
+            out=bias_g[:].rearrange("p k c -> p (k c)"), in_=gcn2_b.partition_broadcast(P)
+        )
+        nc.sync.dma_start(
+            out=wp_rows[:].rearrange("p (ob c) -> p ob c", c=C),
+            in_=proj_w.rearrange("(ob p) c -> p ob c", p=P),
+        )
+        nc.sync.dma_start(out=adj_rows[:], in_=adj.rearrange("k j w -> j k w"))
+        nc.sync.dma_start(out=bias_p[:], in_=proj_b.partition_broadcast(P))
+        for b0 in range(PAIR, B, PAIR):
+            load_streams(b0)
+            nc.sync.dma_start(
+                out=x_rows[:, b0 - PAIR : b0, :],
+                in_=x[b0 - PAIR : b0].rearrange("b j c -> j b c"),
+            )
+        nc.sync.dma_start(
+            out=x_rows[:, B - PAIR : B, :], in_=x[B - PAIR : B].rearrange("b j c -> j b c")
+        )
+
+        a_turned = keep.tile([P, B * P * PACK], BF16)
+        g_turned = keep.tile([P, B * P * PACK], BF16)
+        u_bf16 = keep.tile([P, B * P * PACK], BF16, align_bytes=64)
+        v_bf16 = keep.tile([P, B * P * PACK], BF16, align_bytes=64)
+        wg_turned = keep.tile([P, KINDS * C * PACK], BF16, align_bytes=64)
+        wp_turned = keep.tile([P, C * PACK], BF16, align_bytes=64)
+        adj_grouped = keep.tile([P, P, KINDS], BF16, align_bytes=64)
+
+        u_codes = keep.tile([P, B * P], U32, align_bytes=64)
+        u_scales = keep.tile([P, B * P], U8, align_bytes=64)
+        v_codes = keep.tile([P, B * P], U32, align_bytes=64)
+        v_scales = keep.tile([P, B * P], U8, align_bytes=64)
+        wg_codes = keep.tile([P, KINDS * C], U32, align_bytes=64)
+        wg_scales = keep.tile([P, KINDS * C], U8, align_bytes=64)
+        wp_codes = keep.tile([P, C], U32, align_bytes=64)
+        wp_scales = keep.tile([P, C], U8, align_bytes=64)
+        adj_codes = keep.tile([P, P], U32, align_bytes=64)
+        adj_scales = keep.tile([P, P], U8, align_bytes=64)
+        x_plus_bias = keep.tile([P, B, C], F32)
+
+        def as_row_words(rows):
+            return rows[:].bitcast(F32).rearrange("p (n w) -> p n w", w=C // 2)
+
+        def as_turned_words(turned):
+            return turned[:].bitcast(F32).rearrange("q (n r h) -> q n r h", r=P, h=HALVES)
+
+        def quantise(values, codes, scales):
+            nc.vector.quantize_mx(out=codes.bitcast(FP8X4), scales=scales, in_=values)
+
+        def mix_streams(b0):
+            channels_to_partitions(
+                nc, psum_turn, ident_f32, as_row_words(a_rows), as_turned_words(a_turned), b0
+            )
+            channels_to_partitions(
+                nc, psum_turn, ident_f32, as_row_words(g_rows), as_turned_words(g_turned), b0
+            )
+            values = slice(b0 * P * PACK, (b0 + PAIR) * P * PACK)
+            words = slice(b0 * P, (b0 + PAIR) * P)
+            nc.vector.scalar_tensor_tensor(
+                out=u_bf16[:, values], in0=a_turned[:, values], scalar=S_A2G,
+                in1=g_turned[:, values], op0=MULT, op1=ADD,
+            )
+            nc.vector.scalar_tensor_tensor(
+                out=v_bf16[:, values], in0=g_turned[:, values], scalar=S_G2A,
+                in1=a_turned[:, values], op0=MULT, op1=ADD,
+            )
+            quantise(u_bf16[:, values], u_codes[:, words], u_scales[:, words])
+            quantise(v_bf16[:, values], v_codes[:, words], v_scales[:, words])
+
+        mix_streams(0)
+
+        for cb in range(KINDS):
+            for k0 in range(0, KINDS, PAIR):
+                channels_to_partitions(
+                    nc, psum_turn, ident_f32, as_row_words(wg_rows),
+                    as_turned_words(wg_turned), cb * KINDS + k0,
+                )
+            quantise(
+                wg_turned[:, cb * C * PACK : (cb + 1) * C * PACK],
+                wg_codes[:, cb * C : (cb + 1) * C],
+                wg_scales[:, cb * C : (cb + 1) * C],
+            )
+        for ob in range(0, KINDS, PAIR):
+            channels_to_partitions(
+                nc, psum_turn, ident_f32, as_row_words(wp_rows), as_turned_words(wp_turned), ob
+            )
+        quantise(wp_turned[:], wp_codes[:], wp_scales[:])
+
+        nc.scalar.copy(out=adj_grouped[:], in_=adj_rows[:].rearrange("j k w -> j w k"))
+        quantise(adj_grouped[:].rearrange("j w k -> j (w k)"), adj_codes[:], adj_scales[:])
+
+        def residual(b):
+            summed = psum_turn.tile([P, C], F32, tag="turn")
+            nc.tensor.matmul(out=summed[:], lhsT=ident_bf16[:], rhs=x_rows[:, b, :], start=True, stop=False)
+            nc.tensor.matmul(out=summed[:], lhsT=ident_bf16[:], rhs=bias_p[:], start=False, stop=True)
+            nc.scalar.copy(out=x_plus_bias[:, b, :], in_=summed[:])
+
+        def graph_and_projection(b):
+            joints = slice(b * P, (b + 1) * P)
+            y_grouped = work.tile([P, KINDS, P, KINDS], BF16, align_bytes=64)
+            y_codes = work.tile([P, C], U32, align_bytes=64)
+            y_scales = work.tile([P, C], U8, align_bytes=64)
+            for cb in range(KINDS):
+                y_bank = psum_y.tile([P, KINDS, P], F32)
+                nc.tensor.matmul_mx(
+                    out=y_bank[:].rearrange("j k c -> j (k c)"),
+                    lhsT=u_codes[:, joints].bitcast(FP8X4),
+                    lhsT_scale=u_scales[:, joints],
+                    rhs=wg_codes[:, cb * C : (cb + 1) * C].bitcast(FP8X4),
+                    rhs_scale=wg_scales[:, cb * C : (cb + 1) * C],
+                    start=True,
+                    stop=True,
+                )
+                nc.vector.tensor_tensor(
+                    out=y_grouped[:, cb, :, :],
+                    in0=y_bank[:].rearrange("j k c -> j c k"),
+                    in1=bias_g[:, :, cb * P : (cb + 1) * P].rearrange("j k c -> j c k"),
+                    op=ADD,
+                )
+            quantise(y_grouped[:].rearrange("j cb c k -> j (cb c k)"), y_codes[:], y_scales[:])
+            total = psum_out.tile([P, C], F32)
+            nc.tensor.matmul_mx(
+                out=total[:],
+                lhsT=v_codes[:, joints].bitcast(FP8X4),
+                lhsT_scale=v_scales[:, joints],
+                rhs=wp_codes[:].bitcast(FP8X4),
+                rhs_scale=wp_scales[:],
+                start=True,
+                stop=False,
+            )
+            nc.tensor.matmul_mx(
+                out=total[:],
+                lhsT=adj_codes[:].bitcast(FP8X4),
+                lhsT_scale=adj_scales[:],
+                rhs=y_codes[:].bitcast(FP8X4),
+                rhs_scale=y_scales[:],
+                start=False,
+                stop=True,
+            )
+            result = work.tile([P, C], F32)
+            nc.vector.tensor_tensor(out=result[:], in0=total[:], in1=x_plus_bias[:, b, :], op=ADD)
+            nc.sync.dma_start(out=out[b], in_=result[:])
+
+        for b0 in range(0, B, PAIR):
+            if b0 + PAIR < B:
+                mix_streams(b0 + PAIR)
+            for b in range(b0, b0 + PAIR):
+                residual(b)
+                graph_and_projection(b)

@@ -20,25 +20,11 @@ HEADS = 8
 HEAD_DIM = 64
 HALVES = 2
 PAIR = 2
+BANKS = 8
 S_G2A = 0.5
 S_A2G = 0.8
 
 FLOPS = 2 * B * P * C * (C + KINDS * C) + 2 * B * P * (KINDS * P) * C
-
-
-def channels_to_partitions(nc, psum, ident, src_words, dst_words, first_block):
-    turned = psum.tile([P, PAIR, HALVES, P], F32, tag="turn")
-    for i in range(PAIR):
-        for h in range(HALVES):
-            nc.tensor.transpose(
-                turned[:, i, h, :],
-                src_words[:, first_block + i, h * P : (h + 1) * P],
-                ident[:],
-            )
-    nc.scalar.copy(
-        out=dst_words[:, first_block : first_block + PAIR, :, :],
-        in_=turned[:].rearrange("q i h r -> q i r h"),
-    )
 
 
 def tile_block_pb_kernel(
@@ -46,101 +32,114 @@ def tile_block_pb_kernel(
 ):
     nc = tc.nc
     with ExitStack() as ctx:
+        ctx.enter_context(tc.manual_schedule())
         keep = ctx.enter_context(tc.tile_pool(name="keep", bufs=1))
         work = ctx.enter_context(tc.tile_pool(name="work", bufs=3))
-        psum_turn = ctx.enter_context(tc.psum_pool(name="psum_turn", bufs=2))
-        psum_y = ctx.enter_context(tc.psum_pool(name="psum_y", bufs=4))
-        psum_out = ctx.enter_context(tc.psum_pool(name="psum_out", bufs=2))
+        psum = ctx.enter_context(tc.psum_pool(name="psum", bufs=BANKS))
 
         ident_f32 = keep.tile([P, P], F32)
         make_identity(nc, ident_f32[:])
         ident_bf16 = keep.tile([P, P], BF16)
         make_identity(nc, ident_bf16[:])
 
+        bias_rows = keep.tile([P, P], BF16)
         a_rows = keep.tile([P, B * C], BF16)
         g_rows = keep.tile([P, B * C], BF16)
-        x_rows = keep.tile([P, B, C], BF16)
         wg_rows = keep.tile([P, KINDS * KINDS * C], BF16)
         wp_rows = keep.tile([P, KINDS * C], BF16)
         adj_rows = keep.tile([P, KINDS, P], BF16)
-        bias_g = keep.tile([P, KINDS, C], BF16)
-        bias_p = keep.tile([P, C], BF16)
+        x_rows = keep.tile([P, B, C], BF16)
 
-        def load_streams(b0):
-            batches = slice(b0, b0 + PAIR)
+        nc.vector.memset(bias_rows[:], 0.0)
+        nc.sync.dma_start(
+            out=bias_rows[0 : KINDS * KINDS, :], in_=gcn2_b.rearrange("(n c) -> n c", c=P)
+        )
+        nc.sync.dma_start(
+            out=bias_rows[KINDS * KINDS : KINDS * KINDS + KINDS, :],
+            in_=proj_b.rearrange("(n c) -> n c", c=P),
+        )
+        a_dram = attn_o.rearrange("b h j d -> (b h) j d")
+        for b0 in range(0, B, PAIR):
+            heads = slice(b0 * HEADS, (b0 + PAIR) * HEADS)
             nc.sync.dma_start(
-                out=a_rows[:].rearrange("j (bh d) -> j bh d", d=HEAD_DIM)[
-                    :, b0 * HEADS : (b0 + PAIR) * HEADS, :
-                ],
-                in_=attn_o.rearrange("b h j d -> (b h) j d")[
-                    b0 * HEADS : (b0 + PAIR) * HEADS
-                ].rearrange("bh j d -> j bh d"),
+                out=a_rows[:].rearrange("j (bh d) -> j bh d", d=HEAD_DIM)[:, heads, :],
+                in_=a_dram[heads].rearrange("bh j d -> j bh d"),
             )
             nc.sync.dma_start(
-                out=g_rows[:].rearrange("j (b c) -> j b c", c=C)[:, batches, :],
-                in_=xg1[batches].rearrange("b j c -> j b c"),
+                out=g_rows[:].rearrange("j (b c) -> j b c", c=C)[:, b0 : b0 + PAIR, :],
+                in_=xg1[b0 : b0 + PAIR].rearrange("b j c -> j b c"),
             )
-
-        load_streams(0)
         wg_dram = gcn2_w.rearrange("(k cb p) c -> cb p k c", k=KINDS, cb=KINDS)
         wg_blocks = wg_rows[:].rearrange("p (cb k c) -> p cb k c", cb=KINDS, k=KINDS)
         for cb in range(KINDS):
             nc.sync.dma_start(out=wg_blocks[:, cb, :, :], in_=wg_dram[cb])
         nc.sync.dma_start(
-            out=bias_g[:].rearrange("p k c -> p (k c)"), in_=gcn2_b.partition_broadcast(P)
-        )
-        nc.sync.dma_start(
             out=wp_rows[:].rearrange("p (ob c) -> p ob c", c=C),
             in_=proj_w.rearrange("(ob p) c -> p ob c", p=P),
         )
         nc.sync.dma_start(out=adj_rows[:], in_=adj.rearrange("k j w -> j k w"))
-        nc.sync.dma_start(out=bias_p[:], in_=proj_b.partition_broadcast(P))
-        for b0 in range(PAIR, B, PAIR):
-            load_streams(b0)
+        for b0 in range(0, B, PAIR):
             nc.sync.dma_start(
-                out=x_rows[:, b0 - PAIR : b0, :],
-                in_=x[b0 - PAIR : b0].rearrange("b j c -> j b c"),
+                out=x_rows[:, b0 : b0 + PAIR, :],
+                in_=x[b0 : b0 + PAIR].rearrange("b j c -> j b c"),
             )
-        nc.sync.dma_start(
-            out=x_rows[:, B - PAIR : B, :], in_=x[B - PAIR : B].rearrange("b j c -> j b c")
-        )
+
+        bias_g = keep.tile([P, KINDS, P, KINDS], BF16)
+        bias_p = keep.tile([P, KINDS, P], BF16)
+        bias_cols = keep.tile([P, P], BF16)
+        stood_up = psum.tile([P, P], BF16, tag="bank")
+        nc.tensor.transpose(stood_up[:], bias_rows[:], ident_bf16[:])
+        nc.scalar.copy(out=bias_cols[:], in_=stood_up[:])
+
+        def spread_row(dst, n):
+            nc.tensor.transpose(dst, bias_cols[:, n : n + 1].to_broadcast([P, P]), ident_bf16[:])
+
+        for cb0 in range(0, KINDS, PAIR):
+            spread_g = psum.tile([P, PAIR, KINDS, P], BF16, tag="bank")
+            for i in range(PAIR):
+                for k in range(KINDS):
+                    spread_row(spread_g[:, i, k, :], k * KINDS + cb0 + i)
+            nc.vector.tensor_copy(
+                out=bias_g[:, cb0 : cb0 + PAIR, :, :],
+                in_=spread_g[:].rearrange("p i k c -> p i c k"),
+            )
+        spread_p = psum.tile([P, KINDS, P], BF16, tag="bank")
+        for n in range(KINDS):
+            spread_row(spread_p[:, n, :], KINDS * KINDS + n)
+        nc.scalar.copy(out=bias_p[:], in_=spread_p[:])
+
+        def channels_to_partitions(rows, turned, first_block):
+            row_words = rows[:].bitcast(F32).rearrange("p (n w) -> p n w", w=C // 2)
+            turned_words = turned[:].bitcast(F32).rearrange(
+                "q (n r h) -> q n r h", r=P, h=HALVES
+            )
+            bank = psum.tile([P, PAIR, HALVES, P], F32, tag="bank")
+            for i in range(PAIR):
+                for h in range(HALVES):
+                    nc.tensor.transpose(
+                        bank[:, i, h, :],
+                        row_words[:, first_block + i, h * P : (h + 1) * P],
+                        ident_f32[:],
+                    )
+            nc.scalar.copy(
+                out=turned_words[:, first_block : first_block + PAIR, :, :],
+                in_=bank[:].rearrange("q i h r -> q i r h"),
+            )
+
+        def quantise(values, codes, scales):
+            nc.vector.quantize_mx(out=codes.bitcast(FP8X4), scales=scales, in_=values)
 
         a_turned = keep.tile([P, B * P * PACK], BF16)
         g_turned = keep.tile([P, B * P * PACK], BF16)
         u_bf16 = keep.tile([P, B * P * PACK], BF16, align_bytes=64)
         v_bf16 = keep.tile([P, B * P * PACK], BF16, align_bytes=64)
-        wg_turned = keep.tile([P, KINDS * C * PACK], BF16, align_bytes=64)
-        wp_turned = keep.tile([P, C * PACK], BF16, align_bytes=64)
-        adj_grouped = keep.tile([P, P, KINDS], BF16, align_bytes=64)
-
         u_codes = keep.tile([P, B * P], U32, align_bytes=64)
         u_scales = keep.tile([P, B * P], U8, align_bytes=64)
         v_codes = keep.tile([P, B * P], U32, align_bytes=64)
         v_scales = keep.tile([P, B * P], U8, align_bytes=64)
-        wg_codes = keep.tile([P, KINDS * C], U32, align_bytes=64)
-        wg_scales = keep.tile([P, KINDS * C], U8, align_bytes=64)
-        wp_codes = keep.tile([P, C], U32, align_bytes=64)
-        wp_scales = keep.tile([P, C], U8, align_bytes=64)
-        adj_codes = keep.tile([P, P], U32, align_bytes=64)
-        adj_scales = keep.tile([P, P], U8, align_bytes=64)
-        x_plus_bias = keep.tile([P, B, C], F32)
-
-        def as_row_words(rows):
-            return rows[:].bitcast(F32).rearrange("p (n w) -> p n w", w=C // 2)
-
-        def as_turned_words(turned):
-            return turned[:].bitcast(F32).rearrange("q (n r h) -> q n r h", r=P, h=HALVES)
-
-        def quantise(values, codes, scales):
-            nc.vector.quantize_mx(out=codes.bitcast(FP8X4), scales=scales, in_=values)
-
-        def mix_streams(b0):
-            channels_to_partitions(
-                nc, psum_turn, ident_f32, as_row_words(a_rows), as_turned_words(a_turned), b0
-            )
-            channels_to_partitions(
-                nc, psum_turn, ident_f32, as_row_words(g_rows), as_turned_words(g_turned), b0
-            )
+        for b0 in range(0, B, PAIR):
+            channels_to_partitions(a_rows, a_turned, b0)
+            channels_to_partitions(g_rows, g_turned, b0)
             values = slice(b0 * P * PACK, (b0 + PAIR) * P * PACK)
             words = slice(b0 * P, (b0 + PAIR) * P)
             nc.vector.scalar_tensor_tensor(
@@ -154,41 +153,36 @@ def tile_block_pb_kernel(
             quantise(u_bf16[:, values], u_codes[:, words], u_scales[:, words])
             quantise(v_bf16[:, values], v_codes[:, words], v_scales[:, words])
 
-        mix_streams(0)
-
+        wg_turned = keep.tile([P, KINDS * C * PACK], BF16, align_bytes=64)
+        wg_codes = keep.tile([P, KINDS * C], U32, align_bytes=64)
+        wg_scales = keep.tile([P, KINDS * C], U8, align_bytes=64)
         for cb in range(KINDS):
             for k0 in range(0, KINDS, PAIR):
-                channels_to_partitions(
-                    nc, psum_turn, ident_f32, as_row_words(wg_rows),
-                    as_turned_words(wg_turned), cb * KINDS + k0,
-                )
+                channels_to_partitions(wg_rows, wg_turned, cb * KINDS + k0)
             quantise(
                 wg_turned[:, cb * C * PACK : (cb + 1) * C * PACK],
                 wg_codes[:, cb * C : (cb + 1) * C],
                 wg_scales[:, cb * C : (cb + 1) * C],
             )
+
+        wp_turned = keep.tile([P, C * PACK], BF16, align_bytes=64)
+        wp_codes = keep.tile([P, C], U32, align_bytes=64)
+        wp_scales = keep.tile([P, C], U8, align_bytes=64)
         for ob in range(0, KINDS, PAIR):
-            channels_to_partitions(
-                nc, psum_turn, ident_f32, as_row_words(wp_rows), as_turned_words(wp_turned), ob
-            )
+            channels_to_partitions(wp_rows, wp_turned, ob)
         quantise(wp_turned[:], wp_codes[:], wp_scales[:])
 
+        adj_grouped = keep.tile([P, P, KINDS], BF16, align_bytes=64)
+        adj_codes = keep.tile([P, P], U32, align_bytes=64)
+        adj_scales = keep.tile([P, P], U8, align_bytes=64)
         nc.scalar.copy(out=adj_grouped[:], in_=adj_rows[:].rearrange("j k w -> j w k"))
         quantise(adj_grouped[:].rearrange("j w k -> j (w k)"), adj_codes[:], adj_scales[:])
 
-        def residual(b):
-            summed = psum_turn.tile([P, C], F32, tag="turn")
-            nc.tensor.matmul(out=summed[:], lhsT=ident_bf16[:], rhs=x_rows[:, b, :], start=True, stop=False)
-            nc.tensor.matmul(out=summed[:], lhsT=ident_bf16[:], rhs=bias_p[:], start=False, stop=True)
-            nc.scalar.copy(out=x_plus_bias[:, b, :], in_=summed[:])
-
-        def graph_and_projection(b):
+        def graph_product(b):
             joints = slice(b * P, (b + 1) * P)
             y_grouped = work.tile([P, KINDS, P, KINDS], BF16, align_bytes=64)
-            y_codes = work.tile([P, C], U32, align_bytes=64)
-            y_scales = work.tile([P, C], U8, align_bytes=64)
             for cb in range(KINDS):
-                y_bank = psum_y.tile([P, KINDS, P], F32)
+                y_bank = psum.tile([P, KINDS, P], F32, tag="bank")
                 nc.tensor.matmul_mx(
                     out=y_bank[:].rearrange("j k c -> j (k c)"),
                     lhsT=u_codes[:, joints].bitcast(FP8X4),
@@ -201,11 +195,30 @@ def tile_block_pb_kernel(
                 nc.vector.tensor_tensor(
                     out=y_grouped[:, cb, :, :],
                     in0=y_bank[:].rearrange("j k c -> j c k"),
-                    in1=bias_g[:, :, cb * P : (cb + 1) * P].rearrange("j k c -> j c k"),
+                    in1=bias_g[:, cb, :, :],
                     op=ADD,
                 )
+            return y_grouped
+
+        def quantise_y(y_grouped):
+            y_codes = work.tile([P, C], U32, align_bytes=64)
+            y_scales = work.tile([P, C], U8, align_bytes=64)
             quantise(y_grouped[:].rearrange("j cb c k -> j (cb c k)"), y_codes[:], y_scales[:])
-            total = psum_out.tile([P, C], F32)
+            return y_codes, y_scales
+
+        def finish(b, y_codes, y_scales):
+            joints = slice(b * P, (b + 1) * P)
+            residual_bank = psum.tile([P, C], F32, tag="bank")
+            nc.tensor.matmul(
+                out=residual_bank[:], lhsT=ident_bf16[:], rhs=x_rows[:, b, :], start=True, stop=False
+            )
+            nc.tensor.matmul(
+                out=residual_bank[:], lhsT=ident_bf16[:],
+                rhs=bias_p[:].rearrange("p n c -> p (n c)"), start=False, stop=True,
+            )
+            residual = work.tile([P, C], F32)
+            nc.scalar.copy(out=residual[:], in_=residual_bank[:])
+            total = psum.tile([P, C], F32, tag="bank")
             nc.tensor.matmul_mx(
                 out=total[:],
                 lhsT=v_codes[:, joints].bitcast(FP8X4),
@@ -225,12 +238,12 @@ def tile_block_pb_kernel(
                 stop=True,
             )
             result = work.tile([P, C], F32)
-            nc.vector.tensor_tensor(out=result[:], in0=total[:], in1=x_plus_bias[:, b, :], op=ADD)
+            nc.vector.tensor_tensor(out=result[:], in0=total[:], in1=residual[:], op=ADD)
             nc.sync.dma_start(out=out[b], in_=result[:])
 
-        for b0 in range(0, B, PAIR):
-            if b0 + PAIR < B:
-                mix_streams(b0 + PAIR)
-            for b in range(b0, b0 + PAIR):
-                residual(b)
-                graph_and_projection(b)
+        quantised = quantise_y(graph_product(0))
+        for b in range(1, B):
+            y_grouped = graph_product(b)
+            finish(b - 1, quantised[0], quantised[1])
+            quantised = quantise_y(y_grouped)
+        finish(B - 1, quantised[0], quantised[1])

@@ -20,6 +20,8 @@ HEADS = 8
 HEAD_DIM = 64
 HALVES = 2
 PAIR = 2
+ROUNDS = B // PAIR
+AHEAD = 2
 BANKS = 8
 S_G2A = 0.5
 S_A2G = 0.8
@@ -34,7 +36,8 @@ def tile_block_pb_kernel(
     with ExitStack() as ctx:
         ctx.enter_context(tc.manual_schedule())
         keep = ctx.enter_context(tc.tile_pool(name="keep", bufs=1))
-        work = ctx.enter_context(tc.tile_pool(name="work", bufs=3))
+        rounds = ctx.enter_context(tc.tile_pool(name="rounds", bufs=2))
+        ends = ctx.enter_context(tc.tile_pool(name="ends", bufs=2 * PAIR))
         psum = ctx.enter_context(tc.psum_pool(name="psum", bufs=BANKS))
 
         ident_f32 = keep.tile([P, P], F32)
@@ -50,6 +53,26 @@ def tile_block_pb_kernel(
         adj_rows = keep.tile([P, KINDS, P], BF16)
         x_rows = keep.tile([P, B, C], BF16)
 
+        a_dram = attn_o.rearrange("b h j d -> (b h) j d")
+
+        def load_streams(r):
+            heads = slice(r * PAIR * HEADS, (r + 1) * PAIR * HEADS)
+            batches = slice(r * PAIR, (r + 1) * PAIR)
+            nc.sync.dma_start(
+                out=a_rows[:].rearrange("j (bh d) -> j bh d", d=HEAD_DIM)[:, heads, :],
+                in_=a_dram[heads].rearrange("bh j d -> j bh d"),
+            )
+            nc.sync.dma_start(
+                out=g_rows[:].rearrange("j (b c) -> j b c", c=C)[:, batches, :],
+                in_=xg1[batches].rearrange("b j c -> j b c"),
+            )
+
+        def load_residual(r):
+            batches = slice(r * PAIR, (r + 1) * PAIR)
+            nc.sync.dma_start(
+                out=x_rows[:, batches, :], in_=x[batches].rearrange("b j c -> j b c")
+            )
+
         nc.vector.memset(bias_rows[:], 0.0)
         nc.sync.dma_start(
             out=bias_rows[0 : KINDS * KINDS, :], in_=gcn2_b.rearrange("(n c) -> n c", c=P)
@@ -58,17 +81,8 @@ def tile_block_pb_kernel(
             out=bias_rows[KINDS * KINDS : KINDS * KINDS + KINDS, :],
             in_=proj_b.rearrange("(n c) -> n c", c=P),
         )
-        a_dram = attn_o.rearrange("b h j d -> (b h) j d")
-        for b0 in range(0, B, PAIR):
-            heads = slice(b0 * HEADS, (b0 + PAIR) * HEADS)
-            nc.sync.dma_start(
-                out=a_rows[:].rearrange("j (bh d) -> j bh d", d=HEAD_DIM)[:, heads, :],
-                in_=a_dram[heads].rearrange("bh j d -> j bh d"),
-            )
-            nc.sync.dma_start(
-                out=g_rows[:].rearrange("j (b c) -> j b c", c=C)[:, b0 : b0 + PAIR, :],
-                in_=xg1[b0 : b0 + PAIR].rearrange("b j c -> j b c"),
-            )
+        for r in range(AHEAD):
+            load_streams(r)
         wg_dram = gcn2_w.rearrange("(k cb p) c -> cb p k c", k=KINDS, cb=KINDS)
         wg_blocks = wg_rows[:].rearrange("p (cb k c) -> p cb k c", cb=KINDS, k=KINDS)
         for cb in range(KINDS):
@@ -78,11 +92,11 @@ def tile_block_pb_kernel(
             in_=proj_w.rearrange("(ob p) c -> p ob c", p=P),
         )
         nc.sync.dma_start(out=adj_rows[:], in_=adj.rearrange("k j w -> j k w"))
-        for b0 in range(0, B, PAIR):
-            nc.sync.dma_start(
-                out=x_rows[:, b0 : b0 + PAIR, :],
-                in_=x[b0 : b0 + PAIR].rearrange("b j c -> j b c"),
-            )
+        for r in range(AHEAD, ROUNDS):
+            load_streams(r)
+            load_residual(r - AHEAD)
+        for r in range(ROUNDS - AHEAD, ROUNDS):
+            load_residual(r)
 
         bias_g = keep.tile([P, KINDS, P, KINDS], BF16)
         bias_p = keep.tile([P, KINDS, P], BF16)
@@ -106,7 +120,7 @@ def tile_block_pb_kernel(
         spread_p = psum.tile([P, KINDS, P], BF16, tag="bank")
         for n in range(KINDS):
             spread_row(spread_p[:, n, :], KINDS * KINDS + n)
-        nc.scalar.copy(out=bias_p[:], in_=spread_p[:])
+        nc.vector.tensor_copy(out=bias_p[:], in_=spread_p[:])
 
         def channels_to_partitions(rows, turned, first_block):
             row_words = rows[:].bitcast(F32).rearrange("p (n w) -> p n w", w=C // 2)
@@ -131,27 +145,37 @@ def tile_block_pb_kernel(
 
         a_turned = keep.tile([P, B * P * PACK], BF16)
         g_turned = keep.tile([P, B * P * PACK], BF16)
+        g_halved = keep.tile([P, B * P * PACK], BF16)
         u_bf16 = keep.tile([P, B * P * PACK], BF16, align_bytes=64)
         v_bf16 = keep.tile([P, B * P * PACK], BF16, align_bytes=64)
         u_codes = keep.tile([P, B * P], U32, align_bytes=64)
         u_scales = keep.tile([P, B * P], U8, align_bytes=64)
         v_codes = keep.tile([P, B * P], U32, align_bytes=64)
         v_scales = keep.tile([P, B * P], U8, align_bytes=64)
-        for b0 in range(0, B, PAIR):
-            channels_to_partitions(a_rows, a_turned, b0)
-            channels_to_partitions(g_rows, g_turned, b0)
-            values = slice(b0 * P * PACK, (b0 + PAIR) * P * PACK)
-            words = slice(b0 * P, (b0 + PAIR) * P)
+
+        def turn_streams(r):
+            channels_to_partitions(a_rows, a_turned, r * PAIR)
+            channels_to_partitions(g_rows, g_turned, r * PAIR)
+            values = slice(r * PAIR * P * PACK, (r + 1) * PAIR * P * PACK)
+            nc.scalar.mul(out=g_halved[:, values], in_=g_turned[:, values], mul=S_G2A)
+
+        def mix_streams(r):
+            values = slice(r * PAIR * P * PACK, (r + 1) * PAIR * P * PACK)
+            words = slice(r * PAIR * P, (r + 1) * PAIR * P)
             nc.vector.scalar_tensor_tensor(
                 out=u_bf16[:, values], in0=a_turned[:, values], scalar=S_A2G,
                 in1=g_turned[:, values], op0=MULT, op1=ADD,
             )
-            nc.vector.scalar_tensor_tensor(
-                out=v_bf16[:, values], in0=g_turned[:, values], scalar=S_G2A,
-                in1=a_turned[:, values], op0=MULT, op1=ADD,
+            nc.vector.tensor_tensor(
+                out=v_bf16[:, values], in0=a_turned[:, values], in1=g_halved[:, values], op=ADD
             )
             quantise(u_bf16[:, values], u_codes[:, words], u_scales[:, words])
             quantise(v_bf16[:, values], v_codes[:, words], v_scales[:, words])
+
+        for r in range(AHEAD):
+            turn_streams(r)
+        for r in range(AHEAD):
+            mix_streams(r)
 
         wg_turned = keep.tile([P, KINDS * C * PACK], BF16, align_bytes=64)
         wg_codes = keep.tile([P, KINDS * C], U32, align_bytes=64)
@@ -168,19 +192,19 @@ def tile_block_pb_kernel(
         wp_turned = keep.tile([P, C * PACK], BF16, align_bytes=64)
         wp_codes = keep.tile([P, C], U32, align_bytes=64)
         wp_scales = keep.tile([P, C], U8, align_bytes=64)
-        for ob in range(0, KINDS, PAIR):
-            channels_to_partitions(wp_rows, wp_turned, ob)
-        quantise(wp_turned[:], wp_codes[:], wp_scales[:])
-
         adj_grouped = keep.tile([P, P, KINDS], BF16, align_bytes=64)
         adj_codes = keep.tile([P, P], U32, align_bytes=64)
         adj_scales = keep.tile([P, P], U8, align_bytes=64)
-        nc.scalar.copy(out=adj_grouped[:], in_=adj_rows[:].rearrange("j k w -> j w k"))
-        quantise(adj_grouped[:].rearrange("j w k -> j (w k)"), adj_codes[:], adj_scales[:])
 
-        def graph_product(b):
+        def prepare_projection():
+            for ob in range(0, KINDS, PAIR):
+                channels_to_partitions(wp_rows, wp_turned, ob)
+            nc.scalar.copy(out=adj_grouped[:], in_=adj_rows[:].rearrange("j k w -> j w k"))
+            quantise(wp_turned[:], wp_codes[:], wp_scales[:])
+            quantise(adj_grouped[:].rearrange("j w k -> j (w k)"), adj_codes[:], adj_scales[:])
+
+        def graph_product(b, y_part):
             joints = slice(b * P, (b + 1) * P)
-            y_grouped = work.tile([P, KINDS, P, KINDS], BF16, align_bytes=64)
             for cb in range(KINDS):
                 y_bank = psum.tile([P, KINDS, P], F32, tag="bank")
                 nc.tensor.matmul_mx(
@@ -193,57 +217,69 @@ def tile_block_pb_kernel(
                     stop=True,
                 )
                 nc.vector.tensor_tensor(
-                    out=y_grouped[:, cb, :, :],
+                    out=y_part[:, cb, :, :],
                     in0=y_bank[:].rearrange("j k c -> j c k"),
                     in1=bias_g[:, cb, :, :],
                     op=ADD,
                 )
-            return y_grouped
 
-        def quantise_y(y_grouped):
-            y_codes = work.tile([P, C], U32, align_bytes=64)
-            y_scales = work.tile([P, C], U8, align_bytes=64)
-            quantise(y_grouped[:].rearrange("j cb c k -> j (cb c k)"), y_codes[:], y_scales[:])
-            return y_codes, y_scales
+        def finish_round(r, y_codes, y_scales, adder):
+            residuals = []
+            totals = []
+            for b in range(r * PAIR, (r + 1) * PAIR):
+                residual_bank = psum.tile([P, C], F32, tag="bank")
+                nc.tensor.matmul(
+                    out=residual_bank[:], lhsT=ident_bf16[:], rhs=x_rows[:, b, :],
+                    start=True, stop=False,
+                )
+                nc.tensor.matmul(
+                    out=residual_bank[:], lhsT=ident_bf16[:],
+                    rhs=bias_p[:].rearrange("p n c -> p (n c)"), start=False, stop=True,
+                )
+                residual = ends.tile([P, C], F32)
+                nc.scalar.copy(out=residual[:], in_=residual_bank[:])
+                residuals.append(residual)
+            for b in range(r * PAIR, (r + 1) * PAIR):
+                total = psum.tile([P, C], F32, tag="bank")
+                nc.tensor.matmul_mx(
+                    out=total[:],
+                    lhsT=v_codes[:, b * P : (b + 1) * P].bitcast(FP8X4),
+                    lhsT_scale=v_scales[:, b * P : (b + 1) * P],
+                    rhs=wp_codes[:].bitcast(FP8X4),
+                    rhs_scale=wp_scales[:],
+                    start=True,
+                    stop=False,
+                )
+                totals.append(total)
+            for i in range(PAIR):
+                nc.tensor.matmul_mx(
+                    out=totals[i][:],
+                    lhsT=adj_codes[:].bitcast(FP8X4),
+                    lhsT_scale=adj_scales[:],
+                    rhs=y_codes[:, i * C : (i + 1) * C].bitcast(FP8X4),
+                    rhs_scale=y_scales[:, i * C : (i + 1) * C],
+                    start=False,
+                    stop=True,
+                )
+                products = ends.tile([P, C], F32)
+                nc.scalar.copy(out=products[:], in_=totals[i][:])
+                result = ends.tile([P, C], F32)
+                adder.tensor_tensor(out=result[:], in0=products[:], in1=residuals[i][:], op=ADD)
+                nc.sync.dma_start(out=out[r * PAIR + i], in_=result[:])
 
-        def finish(b, y_codes, y_scales):
-            joints = slice(b * P, (b + 1) * P)
-            residual_bank = psum.tile([P, C], F32, tag="bank")
-            nc.tensor.matmul(
-                out=residual_bank[:], lhsT=ident_bf16[:], rhs=x_rows[:, b, :], start=True, stop=False
-            )
-            nc.tensor.matmul(
-                out=residual_bank[:], lhsT=ident_bf16[:],
-                rhs=bias_p[:].rearrange("p n c -> p (n c)"), start=False, stop=True,
-            )
-            residual = work.tile([P, C], F32)
-            nc.scalar.copy(out=residual[:], in_=residual_bank[:])
-            total = psum.tile([P, C], F32, tag="bank")
-            nc.tensor.matmul_mx(
-                out=total[:],
-                lhsT=v_codes[:, joints].bitcast(FP8X4),
-                lhsT_scale=v_scales[:, joints],
-                rhs=wp_codes[:].bitcast(FP8X4),
-                rhs_scale=wp_scales[:],
-                start=True,
-                stop=False,
-            )
-            nc.tensor.matmul_mx(
-                out=total[:],
-                lhsT=adj_codes[:].bitcast(FP8X4),
-                lhsT_scale=adj_scales[:],
-                rhs=y_codes[:].bitcast(FP8X4),
-                rhs_scale=y_scales[:],
-                start=False,
-                stop=True,
-            )
-            result = work.tile([P, C], F32)
-            nc.vector.tensor_tensor(out=result[:], in0=total[:], in1=residual[:], op=ADD)
-            nc.sync.dma_start(out=out[b], in_=result[:])
-
-        quantised = quantise_y(graph_product(0))
-        for b in range(1, B):
-            y_grouped = graph_product(b)
-            finish(b - 1, quantised[0], quantised[1])
-            quantised = quantise_y(y_grouped)
-        finish(B - 1, quantised[0], quantised[1])
+        for r in range(ROUNDS):
+            y_grouped = rounds.tile([P, PAIR, KINDS, P, KINDS], BF16, align_bytes=64)
+            graph_product(r * PAIR, y_grouped[:, 0])
+            if r == 0:
+                prepare_projection()
+            else:
+                finish_round(r - 1, y_codes, y_scales, nc.gpsimd)
+            graph_product(r * PAIR + 1, y_grouped[:, 1])
+            if r + AHEAD < ROUNDS:
+                turn_streams(r + AHEAD)
+            y_codes = rounds.tile([P, PAIR * C], U32, align_bytes=64)
+            y_scales = rounds.tile([P, PAIR * C], U8, align_bytes=64)
+            quantise(y_grouped[:].rearrange("j i cb c k -> j (i cb c k)"), y_codes[:], y_scales[:])
+            if r + AHEAD < ROUNDS:
+                mix_streams(r + AHEAD)
+        finish_round(ROUNDS - 1, y_codes, y_scales, nc.vector)

@@ -20,9 +20,8 @@ HEADS = 8
 HEAD_DIM = 64
 HALVES = 2
 PAIR = 2
-ROUNDS = B // PAIR
-AHEAD = 2
 BANKS = 8
+STREAMS = 2
 S_G2A = 0.5
 S_A2G = 0.8
 
@@ -36,8 +35,7 @@ def tile_block_pb_kernel(
     with ExitStack() as ctx:
         ctx.enter_context(tc.manual_schedule())
         keep = ctx.enter_context(tc.tile_pool(name="keep", bufs=1))
-        rounds = ctx.enter_context(tc.tile_pool(name="rounds", bufs=2))
-        ends = ctx.enter_context(tc.tile_pool(name="ends", bufs=2 * PAIR))
+        flow = ctx.enter_context(tc.tile_pool(name="flow", bufs=3))
         psum = ctx.enter_context(tc.psum_pool(name="psum", bufs=BANKS))
 
         ident_f32 = keep.tile([P, P], F32)
@@ -53,24 +51,23 @@ def tile_block_pb_kernel(
         adj_rows = keep.tile([P, KINDS, P], BF16)
         x_rows = keep.tile([P, B, C], BF16)
 
-        a_dram = attn_o.rearrange("b h j d -> (b h) j d")
+        wg_dram = gcn2_w.rearrange("(k cb p) c -> cb p k c", k=KINDS, cb=KINDS)
+        wg_blocks = wg_rows[:].rearrange("p (cb k c) -> p cb k c", cb=KINDS, k=KINDS)
 
-        def load_streams(r):
-            heads = slice(r * PAIR * HEADS, (r + 1) * PAIR * HEADS)
-            batches = slice(r * PAIR, (r + 1) * PAIR)
+        def load_streams(b):
             nc.sync.dma_start(
-                out=a_rows[:].rearrange("j (bh d) -> j bh d", d=HEAD_DIM)[:, heads, :],
-                in_=a_dram[heads].rearrange("bh j d -> j bh d"),
+                out=a_rows[:, b * C : (b + 1) * C].rearrange("j (h d) -> j h d", d=HEAD_DIM),
+                in_=attn_o[b].rearrange("h j d -> j h d"),
             )
-            nc.sync.dma_start(
-                out=g_rows[:].rearrange("j (b c) -> j b c", c=C)[:, batches, :],
-                in_=xg1[batches].rearrange("b j c -> j b c"),
-            )
+            nc.sync.dma_start(out=g_rows[:, b * C : (b + 1) * C], in_=xg1[b])
 
-        def load_residual(r):
-            batches = slice(r * PAIR, (r + 1) * PAIR)
+        def load_weights(cb):
+            nc.sync.dma_start(out=wg_blocks[:, cb, :, :], in_=wg_dram[cb])
+
+        def load_residuals(b0):
             nc.sync.dma_start(
-                out=x_rows[:, batches, :], in_=x[batches].rearrange("b j c -> j b c")
+                out=x_rows[:, b0 : b0 + PAIR, :],
+                in_=x[b0 : b0 + PAIR].rearrange("b j c -> j b c"),
             )
 
         nc.vector.memset(bias_rows[:], 0.0)
@@ -81,22 +78,23 @@ def tile_block_pb_kernel(
             out=bias_rows[KINDS * KINDS : KINDS * KINDS + KINDS, :],
             in_=proj_b.rearrange("(n c) -> n c", c=P),
         )
-        for r in range(AHEAD):
-            load_streams(r)
-        wg_dram = gcn2_w.rearrange("(k cb p) c -> cb p k c", k=KINDS, cb=KINDS)
-        wg_blocks = wg_rows[:].rearrange("p (cb k c) -> p cb k c", cb=KINDS, k=KINDS)
-        for cb in range(KINDS):
-            nc.sync.dma_start(out=wg_blocks[:, cb, :, :], in_=wg_dram[cb])
+        load_weights(0)
+        load_streams(0)
+        load_streams(1)
+        for cb in range(1, KINDS):
+            load_weights(cb)
+        load_streams(2)
         nc.sync.dma_start(
             out=wp_rows[:].rearrange("p (ob c) -> p ob c", c=C),
             in_=proj_w.rearrange("(ob p) c -> p ob c", p=P),
         )
         nc.sync.dma_start(out=adj_rows[:], in_=adj.rearrange("k j w -> j k w"))
-        for r in range(AHEAD, ROUNDS):
-            load_streams(r)
-            load_residual(r - AHEAD)
-        for r in range(ROUNDS - AHEAD, ROUNDS):
-            load_residual(r)
+        for b in range(PAIR + 1, B):
+            load_streams(b)
+            if b % PAIR == 0:
+                load_residuals(b - 2 * PAIR)
+        load_residuals(B - 2 * PAIR)
+        load_residuals(B - PAIR)
 
         bias_g = keep.tile([P, KINDS, P, KINDS], BF16)
         bias_p = keep.tile([P, KINDS, P], BF16)
@@ -108,87 +106,72 @@ def tile_block_pb_kernel(
         def spread_row(dst, n):
             nc.tensor.transpose(dst, bias_cols[:, n : n + 1].to_broadcast([P, P]), ident_bf16[:])
 
-        for cb0 in range(0, KINDS, PAIR):
-            spread_g = psum.tile([P, PAIR, KINDS, P], BF16, tag="bank")
-            for i in range(PAIR):
-                for k in range(KINDS):
-                    spread_row(spread_g[:, i, k, :], k * KINDS + cb0 + i)
-            nc.vector.tensor_copy(
-                out=bias_g[:, cb0 : cb0 + PAIR, :, :],
-                in_=spread_g[:].rearrange("p i k c -> p i c k"),
-            )
-        spread_p = psum.tile([P, KINDS, P], BF16, tag="bank")
-        for n in range(KINDS):
-            spread_row(spread_p[:, n, :], KINDS * KINDS + n)
-        nc.vector.tensor_copy(out=bias_p[:], in_=spread_p[:])
+        def spread_graph_bias(cb, copier):
+            spread = psum.tile([P, KINDS, P], BF16, tag="bank")
+            for k in range(KINDS):
+                spread_row(spread[:, k, :], k * KINDS + cb)
+            copier(out=bias_g[:, cb, :, :], in_=spread[:].rearrange("p k c -> p c k"))
 
-        def channels_to_partitions(rows, turned, first_block):
-            row_words = rows[:].bitcast(F32).rearrange("p (n w) -> p n w", w=C // 2)
-            turned_words = turned[:].bitcast(F32).rearrange(
-                "q (n r h) -> q n r h", r=P, h=HALVES
-            )
-            bank = psum.tile([P, PAIR, HALVES, P], F32, tag="bank")
-            for i in range(PAIR):
-                for h in range(HALVES):
-                    nc.tensor.transpose(
-                        bank[:, i, h, :],
-                        row_words[:, first_block + i, h * P : (h + 1) * P],
-                        ident_f32[:],
-                    )
-            nc.scalar.copy(
-                out=turned_words[:, first_block : first_block + PAIR, :, :],
-                in_=bank[:].rearrange("q i h r -> q i r h"),
-            )
+        def spread_projection_bias():
+            spread = psum.tile([P, KINDS, P], BF16, tag="bank")
+            for n in range(KINDS):
+                spread_row(spread[:, n, :], KINDS * KINDS + n)
+            nc.scalar.copy(out=bias_p[:], in_=spread[:])
+
+        def turn_block(dst, rows, block):
+            words = rows[:].bitcast(F32).rearrange("p (n w) -> p n w", w=C // 2)
+            for h in range(HALVES):
+                nc.tensor.transpose(
+                    dst[:, h, :], words[:, block, h * P : (h + 1) * P], ident_f32[:]
+                )
 
         def quantise(values, codes, scales):
             nc.vector.quantize_mx(out=codes.bitcast(FP8X4), scales=scales, in_=values)
 
-        a_turned = keep.tile([P, B * P * PACK], BF16)
-        g_turned = keep.tile([P, B * P * PACK], BF16)
-        g_halved = keep.tile([P, B * P * PACK], BF16)
-        u_bf16 = keep.tile([P, B * P * PACK], BF16, align_bytes=64)
-        v_bf16 = keep.tile([P, B * P * PACK], BF16, align_bytes=64)
+        VALUES = P * PACK
+        g_turned = keep.tile([P, B * VALUES], BF16)
+        g_halved = keep.tile([P, B * VALUES], BF16)
+        u_bf16 = keep.tile([P, B * VALUES], BF16, align_bytes=64)
+        v_bf16 = keep.tile([P, B * VALUES], BF16, align_bytes=64)
         u_codes = keep.tile([P, B * P], U32, align_bytes=64)
         u_scales = keep.tile([P, B * P], U8, align_bytes=64)
         v_codes = keep.tile([P, B * P], U32, align_bytes=64)
         v_scales = keep.tile([P, B * P], U8, align_bytes=64)
 
-        def turn_streams(r):
-            channels_to_partitions(a_rows, a_turned, r * PAIR)
-            channels_to_partitions(g_rows, g_turned, r * PAIR)
-            values = slice(r * PAIR * P * PACK, (r + 1) * PAIR * P * PACK)
-            nc.scalar.mul(out=g_halved[:, values], in_=g_turned[:, values], mul=S_G2A)
+        turned_streams = {}
 
-        def mix_streams(r):
-            values = slice(r * PAIR * P * PACK, (r + 1) * PAIR * P * PACK)
-            words = slice(r * PAIR * P, (r + 1) * PAIR * P)
+        def turn_streams(b):
+            bank = psum.tile([P, STREAMS, P, HALVES], F32, tag="bank")
+            turn_block(bank[:, 0, :, :].rearrange("q r h -> q h r"), a_rows, b)
+            turn_block(bank[:, 1, :, :].rearrange("q r h -> q h r"), g_rows, b)
+            values = slice(b * VALUES, (b + 1) * VALUES)
+            banks = bank[:].rearrange("q s r h -> q (s r h)")
+            g_words = banks[:, P * HALVES : STREAMS * P * HALVES]
+            turned_streams[b] = banks[:, 0 : P * HALVES].bitcast(BF16)
+            nc.scalar.copy(
+                out=g_turned[:].bitcast(F32)[:, b * P * HALVES : (b + 1) * P * HALVES], in_=g_words
+            )
+            nc.scalar.mul(out=g_halved[:, values], in_=g_words.bitcast(BF16), mul=S_G2A)
+
+        def mix_streams(b):
+            values = slice(b * VALUES, (b + 1) * VALUES)
             nc.vector.scalar_tensor_tensor(
-                out=u_bf16[:, values], in0=a_turned[:, values], scalar=S_A2G,
+                out=u_bf16[:, values], in0=turned_streams[b], scalar=S_A2G,
                 in1=g_turned[:, values], op0=MULT, op1=ADD,
             )
             nc.vector.tensor_tensor(
-                out=v_bf16[:, values], in0=a_turned[:, values], in1=g_halved[:, values], op=ADD
+                out=v_bf16[:, values], in0=turned_streams[b], in1=g_halved[:, values], op=ADD
             )
+
+        def quantise_streams(b):
+            values = slice(b * VALUES, (b + 1) * VALUES)
+            words = slice(b * P, (b + 1) * P)
             quantise(u_bf16[:, values], u_codes[:, words], u_scales[:, words])
             quantise(v_bf16[:, values], v_codes[:, words], v_scales[:, words])
-
-        for r in range(AHEAD):
-            turn_streams(r)
-        for r in range(AHEAD):
-            mix_streams(r)
 
         wg_turned = keep.tile([P, KINDS * C * PACK], BF16, align_bytes=64)
         wg_codes = keep.tile([P, KINDS * C], U32, align_bytes=64)
         wg_scales = keep.tile([P, KINDS * C], U8, align_bytes=64)
-        for cb in range(KINDS):
-            for k0 in range(0, KINDS, PAIR):
-                channels_to_partitions(wg_rows, wg_turned, cb * KINDS + k0)
-            quantise(
-                wg_turned[:, cb * C * PACK : (cb + 1) * C * PACK],
-                wg_codes[:, cb * C : (cb + 1) * C],
-                wg_scales[:, cb * C : (cb + 1) * C],
-            )
-
         wp_turned = keep.tile([P, C * PACK], BF16, align_bytes=64)
         wp_codes = keep.tile([P, C], U32, align_bytes=64)
         wp_scales = keep.tile([P, C], U8, align_bytes=64)
@@ -196,90 +179,195 @@ def tile_block_pb_kernel(
         adj_codes = keep.tile([P, P], U32, align_bytes=64)
         adj_scales = keep.tile([P, P], U8, align_bytes=64)
 
-        def prepare_projection():
-            for ob in range(0, KINDS, PAIR):
-                channels_to_partitions(wp_rows, wp_turned, ob)
+        def turn_rows(rows, turned, first_block, copiers):
+            words = turned[:].bitcast(F32).rearrange("q (n r h) -> q n r h", r=P, h=HALVES)
+            for n, copier in zip(range(first_block, first_block + KINDS, PAIR), copiers):
+                bank = psum.tile([P, PAIR, HALVES, P], F32, tag="bank")
+                for i in range(PAIR):
+                    turn_block(bank[:, i, :, :], rows, n + i)
+                copier(
+                    out=words[:, n : n + PAIR, :, :], in_=bank[:].rearrange("q i h r -> q i r h")
+                )
+
+        def turn_graph_weights(cb, *copiers):
+            turn_rows(wg_rows, wg_turned, cb * KINDS, copiers or (nc.scalar.copy, nc.scalar.copy))
+
+        def quantise_graph_weights(cb):
+            quantise(
+                wg_turned[:, cb * C * PACK : (cb + 1) * C * PACK],
+                wg_codes[:, cb * C : (cb + 1) * C],
+                wg_scales[:, cb * C : (cb + 1) * C],
+            )
+
+        def turn_projection():
+            turn_rows(wp_rows, wp_turned, 0, (nc.scalar.copy, nc.scalar.copy))
             nc.scalar.copy(out=adj_grouped[:], in_=adj_rows[:].rearrange("j k w -> j w k"))
+
+        def quantise_projection():
             quantise(wp_turned[:], wp_codes[:], wp_scales[:])
             quantise(adj_grouped[:].rearrange("j w k -> j (w k)"), adj_codes[:], adj_scales[:])
 
-        def graph_product(b, y_part):
-            joints = slice(b * P, (b + 1) * P)
-            for cb in range(KINDS):
-                y_bank = psum.tile([P, KINDS, P], F32, tag="bank")
-                nc.tensor.matmul_mx(
-                    out=y_bank[:].rearrange("j k c -> j (k c)"),
-                    lhsT=u_codes[:, joints].bitcast(FP8X4),
-                    lhsT_scale=u_scales[:, joints],
-                    rhs=wg_codes[:, cb * C : (cb + 1) * C].bitcast(FP8X4),
-                    rhs_scale=wg_scales[:, cb * C : (cb + 1) * C],
-                    start=True,
-                    stop=True,
-                )
-                nc.vector.tensor_tensor(
-                    out=y_part[:, cb, :, :],
-                    in0=y_bank[:].rearrange("j k c -> j c k"),
-                    in1=bias_g[:, cb, :, :],
-                    op=ADD,
-                )
+        y_values = {}
+        y_codes = {}
+        y_scales = {}
 
-        def finish_round(r, y_codes, y_scales, adder):
-            residuals = []
-            totals = []
-            for b in range(r * PAIR, (r + 1) * PAIR):
-                residual_bank = psum.tile([P, C], F32, tag="bank")
-                nc.tensor.matmul(
-                    out=residual_bank[:], lhsT=ident_bf16[:], rhs=x_rows[:, b, :],
-                    start=True, stop=False,
-                )
-                nc.tensor.matmul(
-                    out=residual_bank[:], lhsT=ident_bf16[:],
-                    rhs=bias_p[:].rearrange("p n c -> p (n c)"), start=False, stop=True,
-                )
-                residual = ends.tile([P, C], F32)
-                nc.scalar.copy(out=residual[:], in_=residual_bank[:])
-                residuals.append(residual)
-            for b in range(r * PAIR, (r + 1) * PAIR):
-                total = psum.tile([P, C], F32, tag="bank")
-                nc.tensor.matmul_mx(
-                    out=total[:],
-                    lhsT=v_codes[:, b * P : (b + 1) * P].bitcast(FP8X4),
-                    lhsT_scale=v_scales[:, b * P : (b + 1) * P],
-                    rhs=wp_codes[:].bitcast(FP8X4),
-                    rhs_scale=wp_scales[:],
-                    start=True,
-                    stop=False,
-                )
-                totals.append(total)
-            for i in range(PAIR):
-                nc.tensor.matmul_mx(
-                    out=totals[i][:],
-                    lhsT=adj_codes[:].bitcast(FP8X4),
-                    lhsT_scale=adj_scales[:],
-                    rhs=y_codes[:, i * C : (i + 1) * C].bitcast(FP8X4),
-                    rhs_scale=y_scales[:, i * C : (i + 1) * C],
-                    start=False,
-                    stop=True,
-                )
-                products = ends.tile([P, C], F32)
-                nc.scalar.copy(out=products[:], in_=totals[i][:])
-                result = ends.tile([P, C], F32)
-                adder.tensor_tensor(out=result[:], in0=products[:], in1=residuals[i][:], op=ADD)
-                nc.sync.dma_start(out=out[r * PAIR + i], in_=result[:])
+        def open_batch(b):
+            y_values[b] = flow.tile([P, KINDS, P, KINDS], BF16, align_bytes=64, name="y_values")
+            y_codes[b] = flow.tile([P, C], U32, align_bytes=64, name="y_codes")
+            y_scales[b] = flow.tile([P, C], U8, align_bytes=64, name="y_scales")
 
-        for r in range(ROUNDS):
-            y_grouped = rounds.tile([P, PAIR, KINDS, P, KINDS], BF16, align_bytes=64)
-            graph_product(r * PAIR, y_grouped[:, 0])
-            if r == 0:
-                prepare_projection()
-            else:
-                finish_round(r - 1, y_codes, y_scales, nc.gpsimd)
-            graph_product(r * PAIR + 1, y_grouped[:, 1])
-            if r + AHEAD < ROUNDS:
-                turn_streams(r + AHEAD)
-            y_codes = rounds.tile([P, PAIR * C], U32, align_bytes=64)
-            y_scales = rounds.tile([P, PAIR * C], U8, align_bytes=64)
-            quantise(y_grouped[:].rearrange("j i cb c k -> j (i cb c k)"), y_codes[:], y_scales[:])
-            if r + AHEAD < ROUNDS:
-                mix_streams(r + AHEAD)
-        finish_round(ROUNDS - 1, y_codes, y_scales, nc.vector)
+        def graph_product(b, cb):
+            bank = psum.tile([P, KINDS, P], F32, tag="bank")
+            nc.tensor.matmul_mx(
+                out=bank[:].rearrange("j k c -> j (k c)"),
+                lhsT=u_codes[:, b * P : (b + 1) * P].bitcast(FP8X4),
+                lhsT_scale=u_scales[:, b * P : (b + 1) * P],
+                rhs=wg_codes[:, cb * C : (cb + 1) * C].bitcast(FP8X4),
+                rhs_scale=wg_scales[:, cb * C : (cb + 1) * C],
+                start=True,
+                stop=True,
+            )
+            return bank[:].rearrange("j k c -> j c k")
+
+        def y_by_vector(b, cb):
+            product = graph_product(b, cb)
+            nc.vector.tensor_tensor(
+                out=y_values[b][:, cb, :, :], in0=product, in1=bias_g[:, cb, :, :], op=ADD
+            )
+
+        def y_by_scalar_and_gpsimd(b, cb):
+            product = graph_product(b, cb)
+            copied = flow.tile([P, P, KINDS], F32, name="copied")
+            nc.scalar.copy(out=copied[:], in_=product)
+            nc.gpsimd.tensor_tensor(
+                out=y_values[b][:, cb, :, :], in0=copied[:], in1=bias_g[:, cb, :, :], op=ADD
+            )
+
+        def quantise_y(b, cb0=0, cb1=KINDS):
+            columns = slice(cb0 * P, cb1 * P)
+            quantise(
+                y_values[b][:, cb0:cb1, :, :].rearrange("j cb c k -> j (cb c k)"),
+                y_codes[b][:, columns],
+                y_scales[b][:, columns],
+            )
+
+        residuals = {}
+
+        def make_residual(b):
+            bank = psum.tile([P, C], F32, tag="bank")
+            nc.tensor.matmul(
+                out=bank[:], lhsT=ident_bf16[:], rhs=x_rows[:, b, :], start=True, stop=False
+            )
+            nc.tensor.matmul(
+                out=bank[:], lhsT=ident_bf16[:], rhs=bias_p[:].rearrange("p n c -> p (n c)"),
+                start=False, stop=True,
+            )
+            residuals[b] = flow.tile([P, C], F32, name="residual")
+            nc.scalar.copy(out=residuals[b][:], in_=bank[:])
+
+        def aggregate(b, columns):
+            total = psum.tile([P, C], F32, tag="bank")
+            nc.tensor.matmul_mx(
+                out=total[:, columns],
+                lhsT=v_codes[:, b * P : (b + 1) * P].bitcast(FP8X4),
+                lhsT_scale=v_scales[:, b * P : (b + 1) * P],
+                rhs=wp_codes[:, columns].bitcast(FP8X4),
+                rhs_scale=wp_scales[:, columns],
+                start=True,
+                stop=False,
+            )
+            nc.tensor.matmul_mx(
+                out=total[:, columns],
+                lhsT=adj_codes[:].bitcast(FP8X4),
+                lhsT_scale=adj_scales[:],
+                rhs=y_codes[b][:, columns].bitcast(FP8X4),
+                rhs_scale=y_scales[b][:, columns],
+                start=False,
+                stop=True,
+            )
+            return total
+
+        def finish_by_gpsimd(b):
+            total = aggregate(b, slice(0, C))
+            products = flow.tile([P, C], F32, name="products")
+            nc.scalar.copy(out=products[:], in_=total[:])
+            result = flow.tile([P, C], F32, name="result")
+            nc.gpsimd.tensor_tensor(out=result[:], in0=products[:], in1=residuals[b][:], op=ADD)
+            nc.sync.dma_start(out=out[b], in_=result[:])
+
+        def finish_by_vector(b, cb0, cb1):
+            columns = slice(cb0 * P, cb1 * P)
+            total = aggregate(b, columns)
+            result = flow.tile([P, C], F32, name="result")
+            nc.vector.tensor_tensor(
+                out=result[:, columns], in0=total[:, columns], in1=residuals[b][:, columns], op=ADD
+            )
+            nc.sync.dma_start(out=out[b][:, columns], in_=result[:, columns])
+
+        spread_graph_bias(0, nc.vector.tensor_copy)
+        spread_graph_bias(1, nc.vector.tensor_copy)
+        turn_graph_weights(0, nc.scalar.copy, nc.vector.tensor_copy)
+        turn_streams(0)
+        quantise_graph_weights(0)
+        mix_streams(0)
+        quantise_streams(0)
+        turn_streams(1)
+        for b in range(PAIR):
+            open_batch(b)
+        mix_streams(1)
+        y_by_vector(0, 0)
+        turn_graph_weights(1)
+        quantise_streams(1)
+        y_by_vector(1, 0)
+        turn_graph_weights(2)
+        quantise_graph_weights(1)
+        turn_graph_weights(3)
+        quantise_graph_weights(2)
+        y_by_vector(0, 1)
+        spread_graph_bias(2, nc.scalar.copy)
+        y_by_vector(1, 1)
+        turn_streams(2)
+        quantise_graph_weights(3)
+        y_by_vector(0, 2)
+        y_by_vector(1, 2)
+        spread_graph_bias(3, nc.scalar.copy)
+        turn_projection()
+        mix_streams(2)
+        y_by_vector(0, 3)
+        quantise_streams(2)
+        y_by_vector(1, 3)
+        turn_streams(3)
+        spread_projection_bias()
+        quantise_y(0)
+        open_batch(2)
+        y_by_scalar_and_gpsimd(2, 0)
+        quantise_projection()
+        make_residual(0)
+        mix_streams(3)
+        quantise_streams(3)
+
+        for b in range(PAIR, B):
+            y_by_vector(b, 1)
+            if b + 2 < B:
+                turn_streams(b + 2)
+            quantise_y(b - 1)
+            y_by_vector(b, 2)
+            if b + 2 < B:
+                mix_streams(b + 2)
+                quantise_streams(b + 2)
+            if b == B - 1:
+                make_residual(b)
+                quantise_y(b, 0, PAIR)
+            y_by_vector(b, 3)
+            if b + 1 < B:
+                open_batch(b + 1)
+                y_by_scalar_and_gpsimd(b + 1, 0)
+            if b == PAIR:
+                finish_by_gpsimd(b - 2)
+            make_residual(b - 1)
+            if b + 1 < B:
+                finish_by_gpsimd(b - 1)
+        finish_by_vector(B - 2, 0, KINDS)
+        quantise_y(B - 1, PAIR, KINDS)
+        finish_by_vector(B - 1, 0, PAIR)
+        finish_by_vector(B - 1, PAIR, KINDS)

@@ -35,7 +35,7 @@ def tile_block_pb_kernel(
     with ExitStack() as ctx:
         ctx.enter_context(tc.manual_schedule())
         keep = ctx.enter_context(tc.tile_pool(name="keep", bufs=1))
-        flow = ctx.enter_context(tc.tile_pool(name="flow", bufs=3))
+        flow = ctx.enter_context(tc.tile_pool(name="flow", bufs=4))
         psum = ctx.enter_context(tc.psum_pool(name="psum", bufs=BANKS))
 
         ident_f32 = keep.tile([P, P], F32)
@@ -312,20 +312,20 @@ def tile_block_pb_kernel(
         mix_streams(0)
         quantise_streams(0)
         turn_streams(1)
+        turn_graph_weights(1)
         for b in range(PAIR):
             open_batch(b)
         mix_streams(1)
-        y_by_vector(0, 0)
-        turn_graph_weights(1)
         quantise_streams(1)
+        y_by_vector(0, 0)
         y_by_vector(1, 0)
         turn_graph_weights(2)
         quantise_graph_weights(1)
         turn_graph_weights(3)
+        y_by_scalar_and_gpsimd(0, 1)
         quantise_graph_weights(2)
-        y_by_vector(0, 1)
         spread_graph_bias(2, nc.scalar.copy)
-        y_by_vector(1, 1)
+        y_by_scalar_and_gpsimd(1, 1)
         turn_streams(2)
         quantise_graph_weights(3)
         y_by_vector(0, 2)
@@ -357,7 +357,6 @@ def tile_block_pb_kernel(
                 quantise_streams(b + 2)
             if b == B - 1:
                 make_residual(b)
-                quantise_y(b, 0, PAIR)
             y_by_vector(b, 3)
             if b + 1 < B:
                 open_batch(b + 1)
@@ -368,6 +367,7 @@ def tile_block_pb_kernel(
             if b + 1 < B:
                 finish_by_gpsimd(b - 1)
         finish_by_vector(B - 2, 0, KINDS)
+        quantise_y(B - 1, 0, PAIR)
         quantise_y(B - 1, PAIR, KINDS)
         finish_by_vector(B - 1, 0, PAIR)
         finish_by_vector(B - 1, PAIR, KINDS)

@@ -20,6 +20,7 @@ HEADS = 8
 HEAD_DIM = 64
 HALVES = 2
 PAIR = 2
+G_ROWS = KINDS * KINDS // PAIR
 BANKS = 8
 STREAMS = 2
 S_G2A = 0.5
@@ -43,7 +44,7 @@ def tile_block_pb_kernel(
         ident_bf16 = keep.tile([P, P], BF16)
         make_identity(nc, ident_bf16[:])
 
-        bias_rows = keep.tile([P, P], BF16)
+        bias_rows = keep.tile([P, PAIR * P], BF16)
         a_rows = keep.tile([P, B * C], BF16)
         g_rows = keep.tile([P, B * C], BF16)
         wg_rows = keep.tile([P, KINDS * KINDS * C], BF16)
@@ -61,8 +62,8 @@ def tile_block_pb_kernel(
             )
             nc.sync.dma_start(out=g_rows[:, b * C : (b + 1) * C], in_=xg1[b])
 
-        def load_weights(cb):
-            nc.sync.dma_start(out=wg_blocks[:, cb, :, :], in_=wg_dram[cb])
+        def load_weights(cb, k0=0, k1=KINDS):
+            nc.sync.dma_start(out=wg_blocks[:, cb, k0:k1, :], in_=wg_dram[cb][:, k0:k1, :])
 
         def load_residuals(b0):
             nc.sync.dma_start(
@@ -72,13 +73,14 @@ def tile_block_pb_kernel(
 
         nc.vector.memset(bias_rows[:], 0.0)
         nc.sync.dma_start(
-            out=bias_rows[0 : KINDS * KINDS, :], in_=gcn2_b.rearrange("(n c) -> n c", c=P)
+            out=bias_rows[0:G_ROWS, :], in_=gcn2_b.rearrange("(n c) -> n c", c=PAIR * P)
         )
         nc.sync.dma_start(
-            out=bias_rows[KINDS * KINDS : KINDS * KINDS + KINDS, :],
-            in_=proj_b.rearrange("(n c) -> n c", c=P),
+            out=bias_rows[G_ROWS : G_ROWS + PAIR, :],
+            in_=proj_b.rearrange("(n c) -> n c", c=PAIR * P),
         )
-        load_weights(0)
+        load_weights(0, 0, PAIR)
+        load_weights(0, PAIR, KINDS)
         load_streams(0)
         load_streams(1)
         for cb in range(1, KINDS):
@@ -97,26 +99,32 @@ def tile_block_pb_kernel(
         load_residuals(B - PAIR)
 
         bias_g = keep.tile([P, KINDS, P, KINDS], BF16)
-        bias_p = keep.tile([P, KINDS, P], BF16)
-        bias_cols = keep.tile([P, P], BF16)
-        stood_up = psum.tile([P, P], BF16, tag="bank")
-        nc.tensor.transpose(stood_up[:], bias_rows[:], ident_bf16[:])
+        bias_p = keep.tile([P, C], BF16)
+        bias_cols = keep.tile([P, P], F32)
+        stood_up = psum.tile([P, P], F32, tag="bank")
+        nc.tensor.transpose(stood_up[:], bias_rows[:].bitcast(F32), ident_f32[:])
         nc.scalar.copy(out=bias_cols[:], in_=stood_up[:])
 
         def spread_row(dst, n):
-            nc.tensor.transpose(dst, bias_cols[:, n : n + 1].to_broadcast([P, P]), ident_bf16[:])
+            nc.tensor.transpose(dst, bias_cols[:, n : n + 1].to_broadcast([P, P]), ident_f32[:])
 
-        def spread_graph_bias(cb, copier):
-            spread = psum.tile([P, KINDS, P], BF16, tag="bank")
+        def spread_graph_bias(cb0, copier):
+            spread = psum.tile([P, KINDS, P], F32, tag="bank")
             for k in range(KINDS):
-                spread_row(spread[:, k, :], k * KINDS + cb)
-            copier(out=bias_g[:, cb, :, :], in_=spread[:].rearrange("p k c -> p c k"))
+                spread_row(spread[:, k, :], k * PAIR + cb0 // PAIR)
+            values = spread[:].rearrange("p k w -> p (k w)").bitcast(BF16)
+            copier(
+                out=bias_g[:, cb0 : cb0 + PAIR, :, :],
+                in_=values.rearrange("p (k i c) -> p i c k", k=KINDS, i=PAIR),
+            )
 
         def spread_projection_bias():
-            spread = psum.tile([P, KINDS, P], BF16, tag="bank")
-            for n in range(KINDS):
-                spread_row(spread[:, n, :], KINDS * KINDS + n)
-            nc.scalar.copy(out=bias_p[:], in_=spread[:])
+            spread = psum.tile([P, PAIR, P], F32, tag="bank")
+            for n in range(PAIR):
+                spread_row(spread[:, n, :], G_ROWS + n)
+            nc.scalar.copy(
+                out=bias_p[:].bitcast(F32), in_=spread[:].rearrange("p n w -> p (n w)")
+            )
 
         def turn_block(dst, rows, block):
             words = rows[:].bitcast(F32).rearrange("p (n w) -> p n w", w=C // 2)
@@ -131,12 +139,10 @@ def tile_block_pb_kernel(
         VALUES = P * PACK
         g_turned = keep.tile([P, B * VALUES], BF16)
         g_halved = keep.tile([P, B * VALUES], BF16)
-        u_bf16 = keep.tile([P, B * VALUES], BF16, align_bytes=64)
-        v_bf16 = keep.tile([P, B * VALUES], BF16, align_bytes=64)
-        u_codes = keep.tile([P, B * P], U32, align_bytes=64)
-        u_scales = keep.tile([P, B * P], U8, align_bytes=64)
-        v_codes = keep.tile([P, B * P], U32, align_bytes=64)
-        v_scales = keep.tile([P, B * P], U8, align_bytes=64)
+        mixed = keep.tile([P, B, STREAMS, VALUES], BF16, align_bytes=64)
+        mixed_codes = keep.tile([P, B, STREAMS, P], U32, align_bytes=64)
+        mixed_scales = keep.tile([P, B, STREAMS, P], U8, align_bytes=64)
+        U, V = 0, 1
 
         turned_streams = {}
 
@@ -156,18 +162,19 @@ def tile_block_pb_kernel(
         def mix_streams(b):
             values = slice(b * VALUES, (b + 1) * VALUES)
             nc.vector.scalar_tensor_tensor(
-                out=u_bf16[:, values], in0=turned_streams[b], scalar=S_A2G,
+                out=mixed[:, b, U, :], in0=turned_streams[b], scalar=S_A2G,
                 in1=g_turned[:, values], op0=MULT, op1=ADD,
             )
             nc.vector.tensor_tensor(
-                out=v_bf16[:, values], in0=turned_streams[b], in1=g_halved[:, values], op=ADD
+                out=mixed[:, b, V, :], in0=turned_streams[b], in1=g_halved[:, values], op=ADD
             )
 
         def quantise_streams(b):
-            values = slice(b * VALUES, (b + 1) * VALUES)
-            words = slice(b * P, (b + 1) * P)
-            quantise(u_bf16[:, values], u_codes[:, words], u_scales[:, words])
-            quantise(v_bf16[:, values], v_codes[:, words], v_scales[:, words])
+            quantise(
+                mixed[:, b, :, :].rearrange("q s v -> q (s v)"),
+                mixed_codes[:, b, :, :].rearrange("q s r -> q (s r)"),
+                mixed_scales[:, b, :, :].rearrange("q s r -> q (s r)"),
+            )
 
         wg_turned = keep.tile([P, KINDS * C * PACK], BF16, align_bytes=64)
         wg_codes = keep.tile([P, KINDS * C], U32, align_bytes=64)
@@ -220,8 +227,8 @@ def tile_block_pb_kernel(
             bank = psum.tile([P, KINDS, P], F32, tag="bank")
             nc.tensor.matmul_mx(
                 out=bank[:].rearrange("j k c -> j (k c)"),
-                lhsT=u_codes[:, b * P : (b + 1) * P].bitcast(FP8X4),
-                lhsT_scale=u_scales[:, b * P : (b + 1) * P],
+                lhsT=mixed_codes[:, b, U, :].bitcast(FP8X4),
+                lhsT_scale=mixed_scales[:, b, U, :],
                 rhs=wg_codes[:, cb * C : (cb + 1) * C].bitcast(FP8X4),
                 rhs_scale=wg_scales[:, cb * C : (cb + 1) * C],
                 start=True,
@@ -259,7 +266,7 @@ def tile_block_pb_kernel(
                 out=bank[:], lhsT=ident_bf16[:], rhs=x_rows[:, b, :], start=True, stop=False
             )
             nc.tensor.matmul(
-                out=bank[:], lhsT=ident_bf16[:], rhs=bias_p[:].rearrange("p n c -> p (n c)"),
+                out=bank[:], lhsT=ident_bf16[:], rhs=bias_p[:],
                 start=False, stop=True,
             )
             residuals[b] = flow.tile([P, C], F32, name="residual")
@@ -269,8 +276,8 @@ def tile_block_pb_kernel(
             total = psum.tile([P, C], F32, tag="bank")
             nc.tensor.matmul_mx(
                 out=total[:, columns],
-                lhsT=v_codes[:, b * P : (b + 1) * P].bitcast(FP8X4),
-                lhsT_scale=v_scales[:, b * P : (b + 1) * P],
+                lhsT=mixed_codes[:, b, V, :].bitcast(FP8X4),
+                lhsT_scale=mixed_scales[:, b, V, :],
                 rhs=wp_codes[:, columns].bitcast(FP8X4),
                 rhs_scale=wp_scales[:, columns],
                 start=True,
@@ -304,33 +311,31 @@ def tile_block_pb_kernel(
             )
             nc.sync.dma_start(out=out[b][:, columns], in_=result[:, columns])
 
-        spread_graph_bias(0, nc.vector.tensor_copy)
-        spread_graph_bias(1, nc.vector.tensor_copy)
         turn_graph_weights(0, nc.scalar.copy, nc.vector.tensor_copy)
         turn_streams(0)
         quantise_graph_weights(0)
         mix_streams(0)
-        quantise_streams(0)
         turn_streams(1)
+        spread_graph_bias(0, nc.scalar.copy)
+        quantise_streams(0)
         turn_graph_weights(1)
         for b in range(PAIR):
             open_batch(b)
         mix_streams(1)
         quantise_streams(1)
         y_by_vector(0, 0)
-        y_by_vector(1, 0)
         turn_graph_weights(2)
-        quantise_graph_weights(1)
-        turn_graph_weights(3)
-        y_by_scalar_and_gpsimd(0, 1)
-        quantise_graph_weights(2)
         spread_graph_bias(2, nc.scalar.copy)
-        y_by_scalar_and_gpsimd(1, 1)
+        quantise_graph_weights(1)
+        y_by_vector(1, 0)
+        y_by_vector(0, 1)
+        quantise_graph_weights(2)
+        turn_graph_weights(3)
+        y_by_vector(1, 1)
         turn_streams(2)
-        quantise_graph_weights(3)
         y_by_vector(0, 2)
-        y_by_vector(1, 2)
-        spread_graph_bias(3, nc.scalar.copy)
+        quantise_graph_weights(3)
+        y_by_scalar_and_gpsimd(1, 2)
         turn_projection()
         mix_streams(2)
         y_by_vector(0, 3)

@@ -71,6 +71,8 @@ def tile_block_pb_kernel(
                 in_=x[b0 : b0 + PAIR].rearrange("b j c -> j b c"),
             )
 
+        load_weights(0, 0, PAIR)
+        load_weights(0, PAIR, KINDS)
         nc.vector.memset(bias_rows[:], 0.0)
         nc.sync.dma_start(
             out=bias_rows[0:G_ROWS, :], in_=gcn2_b.rearrange("(n c) -> n c", c=PAIR * P)
@@ -79,8 +81,6 @@ def tile_block_pb_kernel(
             out=bias_rows[G_ROWS : G_ROWS + PAIR, :],
             in_=proj_b.rearrange("(n c) -> n c", c=PAIR * P),
         )
-        load_weights(0, 0, PAIR)
-        load_weights(0, PAIR, KINDS)
         load_streams(0)
         load_streams(1)
         for cb in range(1, KINDS):
@@ -101,9 +101,11 @@ def tile_block_pb_kernel(
         bias_g = keep.tile([P, KINDS, P, KINDS], BF16)
         bias_p = keep.tile([P, C], BF16)
         bias_cols = keep.tile([P, P], F32)
-        stood_up = psum.tile([P, P], F32, tag="bank")
-        nc.tensor.transpose(stood_up[:], bias_rows[:].bitcast(F32), ident_f32[:])
-        nc.scalar.copy(out=bias_cols[:], in_=stood_up[:])
+
+        def stand_biases_up():
+            stood_up = psum.tile([P, P], F32, tag="bank")
+            nc.tensor.transpose(stood_up[:], bias_rows[:].bitcast(F32), ident_f32[:])
+            nc.scalar.copy(out=bias_cols[:], in_=stood_up[:])
 
         def spread_row(dst, n):
             nc.tensor.transpose(dst, bias_cols[:, n : n + 1].to_broadcast([P, P]), ident_f32[:])
@@ -312,6 +314,7 @@ def tile_block_pb_kernel(
             nc.sync.dma_start(out=out[b][:, columns], in_=result[:, columns])
 
         turn_graph_weights(0, nc.scalar.copy, nc.vector.tensor_copy)
+        stand_biases_up()
         turn_streams(0)
         quantise_graph_weights(0)
         mix_streams(0)
@@ -348,10 +351,11 @@ def tile_block_pb_kernel(
         y_by_scalar_and_gpsimd(2, 0)
         quantise_projection()
         make_residual(0)
+        finish_by_gpsimd(0)
         mix_streams(3)
         quantise_streams(3)
 
-        for b in range(PAIR, B):
+        for b in range(PAIR, B - 1):
             y_by_vector(b, 1)
             if b + 2 < B:
                 turn_streams(b + 2)
@@ -360,19 +364,22 @@ def tile_block_pb_kernel(
             if b + 2 < B:
                 mix_streams(b + 2)
                 quantise_streams(b + 2)
-            if b == B - 1:
-                make_residual(b)
             y_by_vector(b, 3)
-            if b + 1 < B:
-                open_batch(b + 1)
-                y_by_scalar_and_gpsimd(b + 1, 0)
-            if b == PAIR:
-                finish_by_gpsimd(b - 2)
+            open_batch(b + 1)
+            y_by_scalar_and_gpsimd(b + 1, 0)
             make_residual(b - 1)
-            if b + 1 < B:
+            if b + 2 < B:
                 finish_by_gpsimd(b - 1)
-        finish_by_vector(B - 2, 0, KINDS)
-        quantise_y(B - 1, 0, PAIR)
-        quantise_y(B - 1, PAIR, KINDS)
-        finish_by_vector(B - 1, 0, PAIR)
-        finish_by_vector(B - 1, PAIR, KINDS)
+        b = B - 1
+        y_by_vector(b, 1)
+        quantise_y(b - 1)
+        finish_by_gpsimd(b - 2)
+        y_by_vector(b, 2)
+        make_residual(b)
+        make_residual(b - 1)
+        y_by_vector(b, 3)
+        finish_by_vector(b - 1, 0, KINDS)
+        quantise_y(b, 0, PAIR)
+        quantise_y(b, PAIR, KINDS)
+        finish_by_vector(b, 0, PAIR)
+        finish_by_vector(b, PAIR, KINDS)

@@ -313,7 +313,7 @@ def tile_block_pb_kernel(
             )
             nc.sync.dma_start(out=out[b][:, columns], in_=result[:, columns])
 
-        turn_graph_weights(0, nc.scalar.copy, nc.vector.tensor_copy)
+        turn_graph_weights(0)
         stand_biases_up()
         turn_streams(0)
         quantise_graph_weights(0)
@@ -344,25 +344,27 @@ def tile_block_pb_kernel(
         y_by_vector(0, 3)
         quantise_streams(2)
         y_by_vector(1, 3)
-        turn_streams(3)
         spread_projection_bias()
+        turn_streams(3)
+        quantise_projection()
         quantise_y(0)
         open_batch(2)
         y_by_scalar_and_gpsimd(2, 0)
-        quantise_projection()
         make_residual(0)
-        finish_by_gpsimd(0)
         mix_streams(3)
-        quantise_streams(3)
+        finish_by_gpsimd(0)
 
         for b in range(PAIR, B - 1):
             y_by_vector(b, 1)
+            if b == PAIR:
+                quantise_streams(b + 1)
             if b + 2 < B:
                 turn_streams(b + 2)
             quantise_y(b - 1)
-            y_by_vector(b, 2)
             if b + 2 < B:
                 mix_streams(b + 2)
+            y_by_vector(b, 2)
+            if b + 2 < B:
                 quantise_streams(b + 2)
             y_by_vector(b, 3)
             open_batch(b + 1)

@@ -56,11 +56,11 @@ def tile_block_pb_kernel(
         wg_blocks = wg_rows[:].rearrange("p (cb k c) -> p cb k c", cb=KINDS, k=KINDS)
 
         def load_streams(b):
+            nc.sync.dma_start(out=g_rows[:, b * C : (b + 1) * C], in_=xg1[b])
             nc.sync.dma_start(
                 out=a_rows[:, b * C : (b + 1) * C].rearrange("j (h d) -> j h d", d=HEAD_DIM),
                 in_=attn_o[b].rearrange("h j d -> j h d"),
             )
-            nc.sync.dma_start(out=g_rows[:, b * C : (b + 1) * C], in_=xg1[b])
 
         def load_weights(cb, k0=0, k1=KINDS):
             nc.sync.dma_start(out=wg_blocks[:, cb, k0:k1, :], in_=wg_dram[cb][:, k0:k1, :])
@@ -71,8 +71,8 @@ def tile_block_pb_kernel(
                 in_=x[b0 : b0 + PAIR].rearrange("b j c -> j b c"),
             )
 
-        load_weights(0, 0, PAIR)
-        load_weights(0, PAIR, KINDS)
+        for k in range(KINDS):
+            load_weights(0, k, k + 1)
         nc.vector.memset(bias_rows[:], 0.0)
         nc.sync.dma_start(
             out=bias_rows[0:G_ROWS, :], in_=gcn2_b.rearrange("(n c) -> n c", c=PAIR * P)
@@ -84,7 +84,8 @@ def tile_block_pb_kernel(
         load_streams(0)
         load_streams(1)
         for cb in range(1, KINDS):
-            load_weights(cb)
+            load_weights(cb, 0, PAIR)
+            load_weights(cb, PAIR, KINDS)
         load_streams(2)
         nc.sync.dma_start(
             out=wp_rows[:].rearrange("p (ob c) -> p ob c", c=C),
@@ -149,27 +150,35 @@ def tile_block_pb_kernel(
         turned_streams = {}
 
         def turn_streams(b):
-            bank = psum.tile([P, STREAMS, P, HALVES], F32, tag="bank")
-            turn_block(bank[:, 0, :, :].rearrange("q r h -> q h r"), a_rows, b)
-            turn_block(bank[:, 1, :, :].rearrange("q r h -> q h r"), g_rows, b)
             values = slice(b * VALUES, (b + 1) * VALUES)
-            banks = bank[:].rearrange("q s r h -> q (s r h)")
-            g_words = banks[:, P * HALVES : STREAMS * P * HALVES]
-            turned_streams[b] = banks[:, 0 : P * HALVES].bitcast(BF16)
+            bank = psum.tile([P, STREAMS, P, HALVES], F32, tag="bank")
+            a_bank = bank
+            if b < PAIR:
+                a_bank = psum.tile([P, STREAMS, P, HALVES], F32, tag="bank")
+            turn_block(bank[:, 1, :, :].rearrange("q r h -> q h r"), g_rows, b)
+            turn_block(a_bank[:, 0, :, :].rearrange("q r h -> q h r"), a_rows, b)
+            g_words = bank[:, 1, :, :].rearrange("q r h -> q (r h)")
             nc.scalar.copy(
                 out=g_turned[:].bitcast(F32)[:, b * P * HALVES : (b + 1) * P * HALVES], in_=g_words
             )
             nc.scalar.mul(out=g_halved[:, values], in_=g_words.bitcast(BF16), mul=S_G2A)
+            turned_streams[b] = a_bank[:, 0, :, :].rearrange("q r h -> q (r h)").bitcast(BF16)
 
-        def mix_streams(b):
-            values = slice(b * VALUES, (b + 1) * VALUES)
+        def mix_u(b):
             nc.vector.scalar_tensor_tensor(
                 out=mixed[:, b, U, :], in0=turned_streams[b], scalar=S_A2G,
-                in1=g_turned[:, values], op0=MULT, op1=ADD,
+                in1=g_turned[:, b * VALUES : (b + 1) * VALUES], op0=MULT, op1=ADD,
             )
+
+        def mix_v(b):
             nc.vector.tensor_tensor(
-                out=mixed[:, b, V, :], in0=turned_streams[b], in1=g_halved[:, values], op=ADD
+                out=mixed[:, b, V, :], in0=turned_streams[b],
+                in1=g_halved[:, b * VALUES : (b + 1) * VALUES], op=ADD,
             )
+
+        def mix_streams(b):
+            mix_u(b)
+            mix_v(b)
 
         def quantise_streams(b):
             quantise(
@@ -320,30 +329,31 @@ def tile_block_pb_kernel(
         mix_streams(0)
         turn_streams(1)
         spread_graph_bias(0, nc.scalar.copy)
+        mix_u(1)
         quantise_streams(0)
         turn_graph_weights(1)
         for b in range(PAIR):
             open_batch(b)
-        mix_streams(1)
+        mix_v(1)
         quantise_streams(1)
         y_by_vector(0, 0)
         turn_graph_weights(2)
-        spread_graph_bias(2, nc.scalar.copy)
         quantise_graph_weights(1)
         y_by_vector(1, 0)
-        y_by_vector(0, 1)
+        spread_graph_bias(2, nc.scalar.copy)
         quantise_graph_weights(2)
+        y_by_vector(0, 1)
         turn_graph_weights(3)
         y_by_vector(1, 1)
         turn_streams(2)
-        y_by_vector(0, 2)
+        y_by_scalar_and_gpsimd(0, 2)
         quantise_graph_weights(3)
-        y_by_scalar_and_gpsimd(1, 2)
+        y_by_vector(1, 2)
         turn_projection()
         mix_streams(2)
         y_by_vector(0, 3)
         quantise_streams(2)
-        y_by_vector(1, 3)
+        y_by_scalar_and_gpsimd(1, 3)
         spread_projection_bias()
         turn_streams(3)
         quantise_projection()

@@ -103,6 +103,18 @@ def tile_block_pb_kernel(
         bias_p = keep.tile([P, C], BF16)
         bias_cols = keep.tile([P, P], F32)
 
+        def warm_up():
+            unread = psum.tile([P, C], F32, tag="bank")
+            nc.tensor.matmul_mx(
+                out=unread[:],
+                lhsT=wg_codes[:, 0:P].bitcast(FP8X4),
+                lhsT_scale=wg_scales[:, 0:P],
+                rhs=wg_codes[:, 0:C].bitcast(FP8X4),
+                rhs_scale=wg_scales[:, 0:C],
+                start=True,
+                stop=True,
+            )
+
         def stand_biases_up():
             stood_up = psum.tile([P, P], F32, tag="bank")
             nc.tensor.transpose(stood_up[:], bias_rows[:].bitcast(F32), ident_f32[:])
@@ -336,6 +348,7 @@ def tile_block_pb_kernel(
             open_batch(b)
         mix_v(1)
         quantise_streams(1)
+        warm_up()
         y_by_vector(0, 0)
         turn_graph_weights(2)
         quantise_graph_weights(1)

@@ -16,15 +16,18 @@ PACK = 4
 B = 8
 C = 512
 KINDS = 4
-HEADS = 8
 HEAD_DIM = 64
 HALVES = 2
+JOINTS = P // HALVES
 PAIR = 2
-G_ROWS = KINDS * KINDS // PAIR
+CHUNKS = 8
+CHUNK = C // CHUNKS
 BANKS = 8
 STREAMS = 2
+U, V = 0, 1
 S_G2A = 0.5
 S_A2G = 0.8
+G_IN_U = 1.25
 
 FLOPS = 2 * B * P * C * (C + KINDS * C) + 2 * B * P * (KINDS * P) * C
 
@@ -39,14 +42,20 @@ def tile_block_pb_kernel(
         flow = ctx.enter_context(tc.tile_pool(name="flow", bufs=4))
         psum = ctx.enter_context(tc.psum_pool(name="psum", bufs=BANKS))
 
-        ident_f32 = keep.tile([P, P], F32)
-        make_identity(nc, ident_f32[:])
-        ident_bf16 = keep.tile([P, P], BF16)
-        make_identity(nc, ident_bf16[:])
-
         bias_rows = keep.tile([P, PAIR * P], BF16)
-        a_rows = keep.tile([P, B * C], BF16)
-        g_rows = keep.tile([P, B * C], BF16)
+        nc.vector.memset(bias_rows[:], 0.0)
+        ident = keep.tile([P, P], F32)
+        make_identity(nc, ident[:])
+
+        mixer = keep.tile([P, STREAMS, JOINTS], BF16)
+        for s, factor in ((U, G_IN_U), (V, S_G2A)):
+            nc.vector.scalar_tensor_tensor(
+                out=mixer[:, s, :], in0=ident[:, JOINTS:P], scalar=factor, in1=ident[:, 0:JOINTS],
+                op0=MULT, op1=ADD,
+            )
+
+        bias_raw = keep.tile([CHUNKS, KINDS, CHUNK], BF16)
+        streams = keep.tile([P, B, HALVES, C], BF16)
         wg_rows = keep.tile([P, KINDS * KINDS * C], BF16)
         wp_rows = keep.tile([P, KINDS * C], BF16)
         adj_rows = keep.tile([P, KINDS, P], BF16)
@@ -56,11 +65,15 @@ def tile_block_pb_kernel(
         wg_blocks = wg_rows[:].rearrange("p (cb k c) -> p cb k c", cb=KINDS, k=KINDS)
 
         def load_streams(b):
-            nc.sync.dma_start(out=g_rows[:, b * C : (b + 1) * C], in_=xg1[b])
             nc.sync.dma_start(
-                out=a_rows[:, b * C : (b + 1) * C].rearrange("j (h d) -> j h d", d=HEAD_DIM),
-                in_=attn_o[b].rearrange("h j d -> j h d"),
+                out=streams[JOINTS:P, b, :, :], in_=xg1[b].rearrange("(h i) c -> i h c", h=HALVES)
             )
+            a_dram = attn_o[b].rearrange("n (h i) d -> h i n d", h=HALVES)
+            for h in range(HALVES):
+                nc.sync.dma_start(
+                    out=streams[0:JOINTS, b, h, :].rearrange("i (n d) -> i n d", d=HEAD_DIM),
+                    in_=a_dram[h],
+                )
 
         def load_weights(cb, k0=0, k1=KINDS):
             nc.sync.dma_start(out=wg_blocks[:, cb, k0:k1, :], in_=wg_dram[cb][:, k0:k1, :])
@@ -71,21 +84,22 @@ def tile_block_pb_kernel(
                 in_=x[b0 : b0 + PAIR].rearrange("b j c -> j b c"),
             )
 
-        for k in range(KINDS):
-            load_weights(0, k, k + 1)
-        nc.vector.memset(bias_rows[:], 0.0)
+        load_streams(0)
         nc.sync.dma_start(
-            out=bias_rows[0:G_ROWS, :], in_=gcn2_b.rearrange("(n c) -> n c", c=PAIR * P)
+            out=bias_raw[:], in_=gcn2_b.rearrange("(k n c) -> n k c", k=KINDS, n=CHUNKS)
         )
         nc.sync.dma_start(
-            out=bias_rows[G_ROWS : G_ROWS + PAIR, :],
+            out=bias_rows[CHUNKS : CHUNKS + PAIR, :],
             in_=proj_b.rearrange("(n c) -> n c", c=PAIR * P),
         )
-        load_streams(0)
+        for k in range(KINDS):
+            load_weights(0, k, k + 1)
         load_streams(1)
         for cb in range(1, KINDS):
             load_weights(cb, 0, PAIR)
             load_weights(cb, PAIR, KINDS)
+            if cb == 2:
+                load_residuals(0)
         load_streams(2)
         nc.sync.dma_start(
             out=wp_rows[:].rearrange("p (ob c) -> p ob c", c=C),
@@ -94,107 +108,87 @@ def tile_block_pb_kernel(
         nc.sync.dma_start(out=adj_rows[:], in_=adj.rearrange("k j w -> j k w"))
         for b in range(PAIR + 1, B):
             load_streams(b)
-            if b % PAIR == 0:
-                load_residuals(b - 2 * PAIR)
-        load_residuals(B - 2 * PAIR)
-        load_residuals(B - PAIR)
+            if b % PAIR == 1:
+                load_residuals(b - 1)
 
         bias_g = keep.tile([P, KINDS, P, KINDS], BF16)
         bias_p = keep.tile([P, C], BF16)
         bias_cols = keep.tile([P, P], F32)
 
-        def warm_up():
-            unread = psum.tile([P, C], F32, tag="bank")
-            nc.tensor.matmul_mx(
-                out=unread[:],
-                lhsT=wg_codes[:, 0:P].bitcast(FP8X4),
-                lhsT_scale=wg_scales[:, 0:P],
-                rhs=wg_codes[:, 0:C].bitcast(FP8X4),
-                rhs_scale=wg_scales[:, 0:C],
-                start=True,
-                stop=True,
+        def interleave_graph_bias():
+            nc.vector.tensor_copy(
+                out=bias_rows[0:CHUNKS, :].rearrange("n (c k) -> n c k", k=KINDS),
+                in_=bias_raw[:].rearrange("n k c -> n c k"),
             )
 
         def stand_biases_up():
             stood_up = psum.tile([P, P], F32, tag="bank")
-            nc.tensor.transpose(stood_up[:], bias_rows[:].bitcast(F32), ident_f32[:])
+            nc.tensor.transpose(stood_up[:], bias_rows[:].bitcast(F32), ident[:])
             nc.scalar.copy(out=bias_cols[:], in_=stood_up[:])
 
-        def spread_row(dst, n):
-            nc.tensor.transpose(dst, bias_cols[:, n : n + 1].to_broadcast([P, P]), ident_f32[:])
-
-        def spread_graph_bias(cb0, copier):
+        def spread_rows(dst, row0, rows):
             spread = psum.tile([P, KINDS, P], F32, tag="bank")
-            for k in range(KINDS):
-                spread_row(spread[:, k, :], k * PAIR + cb0 // PAIR)
-            values = spread[:].rearrange("p k w -> p (k w)").bitcast(BF16)
-            copier(
-                out=bias_g[:, cb0 : cb0 + PAIR, :, :],
-                in_=values.rearrange("p (k i c) -> p i c k", k=KINDS, i=PAIR),
+            for n in range(rows):
+                nc.tensor.transpose(
+                    spread[:, n, :],
+                    bias_cols[:, row0 + n : row0 + n + 1].to_broadcast([P, P]),
+                    ident[:],
+                )
+            nc.scalar.copy(
+                out=dst.bitcast(F32), in_=spread[:, 0:rows, :].rearrange("p n w -> p (n w)")
+            )
+
+        def spread_graph_bias(cb0):
+            spread_rows(
+                bias_g[:, cb0 : cb0 + PAIR, :, :].rearrange("p i c k -> p (i c k)"),
+                cb0 * PAIR, PAIR * PAIR,
             )
 
         def spread_projection_bias():
-            spread = psum.tile([P, PAIR, P], F32, tag="bank")
-            for n in range(PAIR):
-                spread_row(spread[:, n, :], G_ROWS + n)
-            nc.scalar.copy(
-                out=bias_p[:].bitcast(F32), in_=spread[:].rearrange("p n w -> p (n w)")
-            )
-
-        def turn_block(dst, rows, block):
-            words = rows[:].bitcast(F32).rearrange("p (n w) -> p n w", w=C // 2)
-            for h in range(HALVES):
-                nc.tensor.transpose(
-                    dst[:, h, :], words[:, block, h * P : (h + 1) * P], ident_f32[:]
-                )
+            spread_rows(bias_p[:], CHUNKS, PAIR)
 
         def quantise(values, codes, scales):
             nc.vector.quantize_mx(out=codes.bitcast(FP8X4), scales=scales, in_=values)
 
-        VALUES = P * PACK
-        g_turned = keep.tile([P, B * VALUES], BF16)
-        g_halved = keep.tile([P, B * VALUES], BF16)
-        mixed = keep.tile([P, B, STREAMS, VALUES], BF16, align_bytes=64)
+        mixed = keep.tile([P, B, STREAMS, P, PACK], BF16, align_bytes=64)
         mixed_codes = keep.tile([P, B, STREAMS, P], U32, align_bytes=64)
         mixed_scales = keep.tile([P, B, STREAMS, P], U8, align_bytes=64)
-        U, V = 0, 1
 
-        turned_streams = {}
+        def round_by_scalar(dst, product, factor):
+            if factor == 1.0:
+                nc.scalar.copy(out=dst, in_=product)
+            else:
+                nc.scalar.mul(out=dst, in_=product, mul=factor)
 
-        def turn_streams(b):
-            values = slice(b * VALUES, (b + 1) * VALUES)
-            bank = psum.tile([P, STREAMS, P, HALVES], F32, tag="bank")
-            a_bank = bank
-            if b < PAIR:
-                a_bank = psum.tile([P, STREAMS, P, HALVES], F32, tag="bank")
-            turn_block(bank[:, 1, :, :].rearrange("q r h -> q h r"), g_rows, b)
-            turn_block(a_bank[:, 0, :, :].rearrange("q r h -> q h r"), a_rows, b)
-            g_words = bank[:, 1, :, :].rearrange("q r h -> q (r h)")
-            nc.scalar.copy(
-                out=g_turned[:].bitcast(F32)[:, b * P * HALVES : (b + 1) * P * HALVES], in_=g_words
-            )
-            nc.scalar.mul(out=g_halved[:, values], in_=g_words.bitcast(BF16), mul=S_G2A)
-            turned_streams[b] = a_bank[:, 0, :, :].rearrange("q r h -> q (r h)").bitcast(BF16)
+        def round_by_vector(dst, product, factor):
+            if factor == 1.0:
+                nc.vector.tensor_copy(out=dst, in_=product)
+            else:
+                nc.vector.tensor_scalar(out=dst, in0=product, scalar1=factor, scalar2=None, op0=MULT)
 
-        def mix_u(b):
-            nc.vector.scalar_tensor_tensor(
-                out=mixed[:, b, U, :], in0=turned_streams[b], scalar=S_A2G,
-                in1=g_turned[:, b * VALUES : (b + 1) * VALUES], op0=MULT, op1=ADD,
-            )
-
-        def mix_v(b):
-            nc.vector.tensor_tensor(
-                out=mixed[:, b, V, :], in0=turned_streams[b],
-                in1=g_halved[:, b * VALUES : (b + 1) * VALUES], op=ADD,
-            )
+        def mix_half(b, h, rounder=round_by_scalar):
+            bank = psum.tile([P, PACK, STREAMS, JOINTS], F32, tag="bank")
+            for t in range(PACK):
+                half, parity = divmod(t, PACK // HALVES)
+                first = half * (C // HALVES)
+                nc.tensor.matmul(
+                    out=bank[:, t, :, :].rearrange("q s i -> q (s i)"),
+                    lhsT=streams[:, b, h, first + parity : first + C // HALVES : 2],
+                    rhs=mixer[:].rearrange("p s i -> p (s i)"),
+                    start=True, stop=True,
+                )
+            joints = slice(h * JOINTS, (h + 1) * JOINTS)
+            products = bank[:].rearrange("q t s i -> q s i t")
+            for s, factor in ((U, S_A2G), (V, 1.0)):
+                rounder(mixed[:, b, s, joints, :], products[:, s, :, :], factor)
 
         def mix_streams(b):
-            mix_u(b)
-            mix_v(b)
+            for h in range(HALVES):
+                mix_half(b, h)
 
         def quantise_streams(b):
             quantise(
-                mixed[:, b, :, :].rearrange("q s v -> q (s v)"),
+                mixed[:, b, :, :, :].rearrange("q s j t -> q (s j t)"),
                 mixed_codes[:, b, :, :].rearrange("q s r -> q (s r)"),
                 mixed_scales[:, b, :, :].rearrange("q s r -> q (s r)"),
             )
@@ -210,11 +204,15 @@ def tile_block_pb_kernel(
         adj_scales = keep.tile([P, P], U8, align_bytes=64)
 
         def turn_rows(rows, turned, first_block, copiers):
+            row_words = rows[:].bitcast(F32).rearrange("p (n w) -> p n w", w=C // 2)
             words = turned[:].bitcast(F32).rearrange("q (n r h) -> q n r h", r=P, h=HALVES)
             for n, copier in zip(range(first_block, first_block + KINDS, PAIR), copiers):
                 bank = psum.tile([P, PAIR, HALVES, P], F32, tag="bank")
                 for i in range(PAIR):
-                    turn_block(bank[:, i, :, :], rows, n + i)
+                    for h in range(HALVES):
+                        nc.tensor.transpose(
+                            bank[:, i, h, :], row_words[:, n + i, h * P : (h + 1) * P], ident[:]
+                        )
                 copier(
                     out=words[:, n : n + PAIR, :, :], in_=bank[:].rearrange("q i h r -> q i r h")
                 )
@@ -246,7 +244,9 @@ def tile_block_pb_kernel(
             y_codes[b] = flow.tile([P, C], U32, align_bytes=64, name="y_codes")
             y_scales[b] = flow.tile([P, C], U8, align_bytes=64, name="y_scales")
 
-        def graph_product(b, cb):
+        products = {}
+
+        def multiply(b, cb):
             bank = psum.tile([P, KINDS, P], F32, tag="bank")
             nc.tensor.matmul_mx(
                 out=bank[:].rearrange("j k c -> j (k c)"),
@@ -257,18 +257,16 @@ def tile_block_pb_kernel(
                 start=True,
                 stop=True,
             )
-            return bank[:].rearrange("j k c -> j c k")
+            products[b, cb] = bank[:].rearrange("j k c -> j c k")
 
-        def y_by_vector(b, cb):
-            product = graph_product(b, cb)
+        def add_by_vector(b, cb):
             nc.vector.tensor_tensor(
-                out=y_values[b][:, cb, :, :], in0=product, in1=bias_g[:, cb, :, :], op=ADD
+                out=y_values[b][:, cb, :, :], in0=products[b, cb], in1=bias_g[:, cb, :, :], op=ADD
             )
 
-        def y_by_scalar_and_gpsimd(b, cb):
-            product = graph_product(b, cb)
+        def add_by_gpsimd(b, cb):
             copied = flow.tile([P, P, KINDS], F32, name="copied")
-            nc.scalar.copy(out=copied[:], in_=product)
+            nc.scalar.copy(out=copied[:], in_=products[b, cb])
             nc.gpsimd.tensor_tensor(
                 out=y_values[b][:, cb, :, :], in0=copied[:], in1=bias_g[:, cb, :, :], op=ADD
             )
@@ -281,21 +279,17 @@ def tile_block_pb_kernel(
                 y_scales[b][:, columns],
             )
 
-        residuals = {}
+        residuals = keep.tile([P, B, C], F32)
 
         def make_residual(b):
-            bank = psum.tile([P, C], F32, tag="bank")
-            nc.tensor.matmul(
-                out=bank[:], lhsT=ident_bf16[:], rhs=x_rows[:, b, :], start=True, stop=False
+            nc.gpsimd.tensor_tensor(
+                out=residuals[:, b, :], in0=x_rows[:, b, :], in1=bias_p[:], op=ADD
             )
-            nc.tensor.matmul(
-                out=bank[:], lhsT=ident_bf16[:], rhs=bias_p[:],
-                start=False, stop=True,
-            )
-            residuals[b] = flow.tile([P, C], F32, name="residual")
-            nc.scalar.copy(out=residuals[b][:], in_=bank[:])
 
-        def aggregate(b, columns):
+        totals = {}
+
+        def aggregate(b, cb0=0, cb1=KINDS):
+            columns = slice(cb0 * P, cb1 * P)
             total = psum.tile([P, C], F32, tag="bank")
             nc.tensor.matmul_mx(
                 out=total[:, columns],
@@ -315,96 +309,98 @@ def tile_block_pb_kernel(
                 start=False,
                 stop=True,
             )
-            return total
+            totals[b, cb0] = total
 
-        def finish_by_gpsimd(b):
-            total = aggregate(b, slice(0, C))
-            products = flow.tile([P, C], F32, name="products")
-            nc.scalar.copy(out=products[:], in_=total[:])
-            result = flow.tile([P, C], F32, name="result")
-            nc.gpsimd.tensor_tensor(out=result[:], in0=products[:], in1=residuals[b][:], op=ADD)
-            nc.sync.dma_start(out=out[b], in_=result[:])
-
-        def finish_by_vector(b, cb0, cb1):
+        def finish(b, cb0=0, cb1=KINDS):
             columns = slice(cb0 * P, cb1 * P)
-            total = aggregate(b, columns)
             result = flow.tile([P, C], F32, name="result")
             nc.vector.tensor_tensor(
-                out=result[:, columns], in0=total[:, columns], in1=residuals[b][:, columns], op=ADD
+                out=result[:, columns], in0=totals[b, cb0][:, columns],
+                in1=residuals[:, b, columns], op=ADD,
             )
             nc.sync.dma_start(out=out[b][:, columns], in_=result[:, columns])
 
-        turn_graph_weights(0)
-        stand_biases_up()
-        turn_streams(0)
-        quantise_graph_weights(0)
-        mix_streams(0)
-        turn_streams(1)
-        spread_graph_bias(0, nc.scalar.copy)
-        mix_u(1)
+        mix_half(0, 0)
+        mix_half(0, 1, round_by_vector)
+        interleave_graph_bias()
         quantise_streams(0)
-        turn_graph_weights(1)
+        turn_graph_weights(0, nc.scalar.copy, nc.vector.tensor_copy)
+        stand_biases_up()
+        mix_half(1, 0)
+        mix_half(1, 1, round_by_vector)
+        spread_graph_bias(0)
+        quantise_graph_weights(0)
+        turn_graph_weights(1, nc.scalar.copy, nc.vector.tensor_copy)
+        quantise_streams(1)
         for b in range(PAIR):
             open_batch(b)
-        mix_v(1)
-        quantise_streams(1)
-        warm_up()
-        y_by_vector(0, 0)
-        turn_graph_weights(2)
-        quantise_graph_weights(1)
-        y_by_vector(1, 0)
-        spread_graph_bias(2, nc.scalar.copy)
-        quantise_graph_weights(2)
-        y_by_vector(0, 1)
-        turn_graph_weights(3)
-        y_by_vector(1, 1)
-        turn_streams(2)
-        y_by_scalar_and_gpsimd(0, 2)
-        quantise_graph_weights(3)
-        y_by_vector(1, 2)
-        turn_projection()
-        mix_streams(2)
-        y_by_vector(0, 3)
-        quantise_streams(2)
-        y_by_scalar_and_gpsimd(1, 3)
+        multiply(0, 0)
         spread_projection_bias()
-        turn_streams(3)
-        quantise_projection()
-        quantise_y(0)
-        open_batch(2)
-        y_by_scalar_and_gpsimd(2, 0)
+        turn_graph_weights(2)
+        multiply(1, 0)
+        add_by_vector(0, 0)
+        quantise_graph_weights(1)
         make_residual(0)
+        make_residual(1)
+        add_by_vector(1, 0)
+        multiply(0, 1)
+        turn_graph_weights(3)
+        multiply(1, 1)
+        spread_graph_bias(2)
+        quantise_graph_weights(2)
+        add_by_vector(0, 1)
+        multiply(0, 2)
+        mix_streams(2)
+        add_by_vector(1, 1)
+        multiply(1, 2)
+        quantise_graph_weights(3)
+        add_by_gpsimd(0, 2)
+        multiply(0, 3)
+        multiply(1, 3)
+        add_by_vector(1, 2)
+        quantise_streams(2)
+        add_by_vector(0, 3)
+        turn_projection()
+        add_by_vector(1, 3)
+        open_batch(2)
+        multiply(2, 0)
+        multiply(2, 1)
+        add_by_gpsimd(2, 0)
         mix_streams(3)
-        finish_by_gpsimd(0)
+        quantise_y(0)
+        multiply(2, 2)
+        multiply(2, 3)
+        quantise_projection()
+        add_by_vector(2, 1)
+        aggregate(0)
+        make_residual(2)
+        quantise_streams(3)
+        make_residual(3)
+        finish(0)
 
-        for b in range(PAIR, B - 1):
-            y_by_vector(b, 1)
-            if b == PAIR:
-                quantise_streams(b + 1)
-            if b + 2 < B:
-                turn_streams(b + 2)
+        for b in range(PAIR, B):
+            add_by_vector(b, 2)
+            if b + 1 < B:
+                open_batch(b + 1)
+                multiply(b + 1, 0)
+                multiply(b + 1, 1)
+                add_by_gpsimd(b + 1, 0)
             quantise_y(b - 1)
             if b + 2 < B:
                 mix_streams(b + 2)
-            y_by_vector(b, 2)
+            add_by_vector(b, 3)
+            aggregate(b - 1)
+            if b + 1 < B:
+                multiply(b + 1, 2)
+                multiply(b + 1, 3)
+                add_by_vector(b + 1, 1)
             if b + 2 < B:
                 quantise_streams(b + 2)
-            y_by_vector(b, 3)
-            open_batch(b + 1)
-            y_by_scalar_and_gpsimd(b + 1, 0)
-            make_residual(b - 1)
-            if b + 2 < B:
-                finish_by_gpsimd(b - 1)
-        b = B - 1
-        y_by_vector(b, 1)
-        quantise_y(b - 1)
-        finish_by_gpsimd(b - 2)
-        y_by_vector(b, 2)
-        make_residual(b)
-        make_residual(b - 1)
-        y_by_vector(b, 3)
-        finish_by_vector(b - 1, 0, KINDS)
-        quantise_y(b, 0, PAIR)
-        quantise_y(b, PAIR, KINDS)
-        finish_by_vector(b, 0, PAIR)
-        finish_by_vector(b, PAIR, KINDS)
+                make_residual(b + 2)
+            finish(b - 1)
+        quantise_y(B - 1, 0, PAIR)
+        quantise_y(B - 1, PAIR, KINDS)
+        aggregate(B - 1, 0, PAIR)
+        aggregate(B - 1, PAIR, KINDS)
+        finish(B - 1, 0, PAIR)
+        finish(B - 1, PAIR, KINDS)

@@ -55,7 +55,7 @@ def tile_block_pb_kernel(
             )
 
         bias_raw = keep.tile([CHUNKS, KINDS, CHUNK], BF16)
-        streams = keep.tile([P, B, HALVES, C], BF16)
+        streams = keep.tile([P, HALVES, B, C], BF16)
         wg_rows = keep.tile([P, KINDS * KINDS * C], BF16)
         wp_rows = keep.tile([P, KINDS * C], BF16)
         adj_rows = keep.tile([P, KINDS, P], BF16)
@@ -64,14 +64,15 @@ def tile_block_pb_kernel(
         wg_dram = gcn2_w.rearrange("(k cb p) c -> cb p k c", k=KINDS, cb=KINDS)
         wg_blocks = wg_rows[:].rearrange("p (cb k c) -> p cb k c", cb=KINDS, k=KINDS)
 
-        def load_streams(b):
-            nc.sync.dma_start(
-                out=streams[JOINTS:P, b, :, :], in_=xg1[b].rearrange("(h i) c -> i h c", h=HALVES)
-            )
-            a_dram = attn_o[b].rearrange("n (h i) d -> h i n d", h=HALVES)
+        def load_streams(b0, b1):
+            a_dram = attn_o[b0:b1].rearrange("b n (h i) d -> h i (b n) d", h=HALVES)
+            g_dram = xg1[b0:b1].rearrange("b (h i) c -> h i b c", h=HALVES)
             for h in range(HALVES):
+                nc.sync.dma_start(out=streams[JOINTS:P, h, b0:b1, :], in_=g_dram[h])
                 nc.sync.dma_start(
-                    out=streams[0:JOINTS, b, h, :].rearrange("i (n d) -> i n d", d=HEAD_DIM),
+                    out=streams[0:JOINTS, h, b0:b1, :].rearrange(
+                        "i b (n d) -> i (b n) d", d=HEAD_DIM
+                    ),
                     in_=a_dram[h],
                 )
 
@@ -84,32 +85,32 @@ def tile_block_pb_kernel(
                 in_=x[b0 : b0 + PAIR].rearrange("b j c -> j b c"),
             )
 
-        load_streams(0)
-        nc.sync.dma_start(
+        nc.gpsimd.dma_start(
             out=bias_raw[:], in_=gcn2_b.rearrange("(k n c) -> n k c", k=KINDS, n=CHUNKS)
         )
-        nc.sync.dma_start(
+        nc.gpsimd.dma_start(
             out=bias_rows[CHUNKS : CHUNKS + PAIR, :],
             in_=proj_b.rearrange("(n c) -> n c", c=PAIR * P),
         )
-        for k in range(KINDS):
-            load_weights(0, k, k + 1)
-        load_streams(1)
-        for cb in range(1, KINDS):
-            load_weights(cb, 0, PAIR)
-            load_weights(cb, PAIR, KINDS)
-            if cb == 2:
-                load_residuals(0)
-        load_streams(2)
+        load_streams(0, 1)
+        load_weights(0, 0, PAIR)
+        load_weights(0, PAIR, KINDS)
+        load_streams(1, 2)
+        load_weights(1)
+        load_weights(2)
+        load_residuals(0)
+        load_weights(3)
+        load_streams(2, 4)
         nc.sync.dma_start(
             out=wp_rows[:].rearrange("p (ob c) -> p ob c", c=C),
             in_=proj_w.rearrange("(ob p) c -> p ob c", p=P),
         )
         nc.sync.dma_start(out=adj_rows[:], in_=adj.rearrange("k j w -> j k w"))
-        for b in range(PAIR + 1, B):
-            load_streams(b)
-            if b % PAIR == 1:
-                load_residuals(b - 1)
+        load_residuals(2)
+        load_streams(4, 6)
+        load_residuals(4)
+        load_streams(6, 8)
+        load_residuals(6)
 
         bias_g = keep.tile([P, KINDS, P, KINDS], BF16)
         bias_p = keep.tile([P, C], BF16)
@@ -173,7 +174,7 @@ def tile_block_pb_kernel(
                 first = half * (C // HALVES)
                 nc.tensor.matmul(
                     out=bank[:, t, :, :].rearrange("q s i -> q (s i)"),
-                    lhsT=streams[:, b, h, first + parity : first + C // HALVES : 2],
+                    lhsT=streams[:, h, b, first + parity : first + C // HALVES : 2],
                     rhs=mixer[:].rearrange("p s i -> p (s i)"),
                     start=True, stop=True,
                 )

@@ -10,6 +10,7 @@ U8 = mybir.dt.uint8
 FP8X4 = mybir.dt.float8_e4m3fn_x4
 ADD = mybir.AluOpType.add
 MULT = mybir.AluOpType.mult
+IDENTITY = mybir.ActivationFunctionType.Identity
 
 P = 128
 PACK = 4
@@ -23,6 +24,8 @@ PAIR = 2
 CHUNKS = 8
 CHUNK = C // CHUNKS
 BANKS = 8
+STRAIGHT = (4, 4, 2, 2)
+SPANS = {4: ((0, 4),), 2: ((0, 2), (2, 4)), 0: ((0, 4),)}
 STREAMS = 2
 U, V = 0, 1
 S_G2A = 0.5
@@ -46,6 +49,8 @@ def tile_block_pb_kernel(
         nc.vector.memset(bias_rows[:], 0.0)
         ident = keep.tile([P, P], F32)
         make_identity(nc, ident[:])
+        ident_bf16 = keep.tile([P, P], BF16)
+        nc.vector.tensor_copy(out=ident_bf16[:], in_=ident[:])
 
         mixer = keep.tile([P, STREAMS, JOINTS], BF16)
         for s, factor in ((U, G_IN_U), (V, S_G2A)):
@@ -55,10 +60,13 @@ def tile_block_pb_kernel(
             )
 
         bias_raw = keep.tile([CHUNKS, KINDS, CHUNK], BF16)
+        bias_natural = keep.tile([P, P], BF16)
+        nc.vector.memset(bias_natural[:], 0.0)
         streams = keep.tile([P, HALVES, B, C], BF16)
         wg_rows = keep.tile([P, KINDS * KINDS * C], BF16)
         wp_rows = keep.tile([P, KINDS * C], BF16)
         adj_rows = keep.tile([P, KINDS, P], BF16)
+        adj_pairs = keep.tile([P, PAIR, PAIR, P], BF16)
         x_rows = keep.tile([P, B, C], BF16)
 
         wg_dram = gcn2_w.rearrange("(k cb p) c -> cb p k c", k=KINDS, cb=KINDS)
@@ -85,31 +93,40 @@ def tile_block_pb_kernel(
                 in_=x[b0 : b0 + PAIR].rearrange("b j c -> j b c"),
             )
 
-        nc.gpsimd.dma_start(
+        load_streams(0, 1)
+        nc.sync.dma_start(
             out=bias_raw[:], in_=gcn2_b.rearrange("(k n c) -> n k c", k=KINDS, n=CHUNKS)
         )
-        nc.gpsimd.dma_start(
+        nc.sync.dma_start(
             out=bias_rows[CHUNKS : CHUNKS + PAIR, :],
             in_=proj_b.rearrange("(n c) -> n c", c=PAIR * P),
         )
-        load_streams(0, 1)
         load_weights(0, 0, PAIR)
         load_weights(0, PAIR, KINDS)
-        load_streams(1, 2)
-        load_weights(1)
-        load_weights(2)
+        for b in range(1, KINDS):
+            load_streams(b, b + 1)
+            load_weights(b)
         load_residuals(0)
-        load_weights(3)
-        load_streams(2, 4)
+        load_streams(4, 6)
+        load_residuals(2)
+        nc.sync.dma_start(out=adj_rows[:], in_=adj.rearrange("k j w -> j k w"))
+        adj_dram = adj.rearrange("(m kk) (jj e) w -> kk jj m (e w)", kk=PAIR, e=PAIR)
+        for kk in range(PAIR):
+            nc.sync.dma_start(
+                out=adj_pairs[kk * JOINTS : (kk + 1) * JOINTS, :, :, :].rearrange(
+                    "jj m e w -> jj m (e w)"
+                ),
+                in_=adj_dram[kk],
+            )
         nc.sync.dma_start(
             out=wp_rows[:].rearrange("p (ob c) -> p ob c", c=C),
             in_=proj_w.rearrange("(ob p) c -> p ob c", p=P),
         )
-        nc.sync.dma_start(out=adj_rows[:], in_=adj.rearrange("k j w -> j k w"))
-        load_residuals(2)
-        load_streams(4, 6)
-        load_residuals(4)
+        nc.sync.dma_start(
+            out=bias_natural[0 : KINDS * KINDS, :], in_=gcn2_b.rearrange("(r c) -> r c", c=P)
+        )
         load_streams(6, 8)
+        load_residuals(4)
         load_residuals(6)
 
         bias_g = keep.tile([P, KINDS, P, KINDS], BF16)
@@ -127,7 +144,16 @@ def tile_block_pb_kernel(
             nc.tensor.transpose(stood_up[:], bias_rows[:].bitcast(F32), ident[:])
             nc.scalar.copy(out=bias_cols[:], in_=stood_up[:])
 
-        def spread_rows(dst, row0, rows):
+        bias_parts = keep.tile([P, KINDS * KINDS], F32)
+
+        def lay_bias_on_partitions():
+            turned = psum.tile([P, P], BF16, tag="bank")
+            nc.tensor.transpose(turned[:], bias_natural[:], ident_bf16[:])
+            nc.scalar.copy(out=bias_parts[:], in_=turned[:, 0 : KINDS * KINDS])
+
+        spread_banks = {}
+
+        def spread_rows(row0, rows):
             spread = psum.tile([P, KINDS, P], F32, tag="bank")
             for n in range(rows):
                 nc.tensor.transpose(
@@ -135,25 +161,23 @@ def tile_block_pb_kernel(
                     bias_cols[:, row0 + n : row0 + n + 1].to_broadcast([P, P]),
                     ident[:],
                 )
+            spread_banks[row0] = spread[:, 0:rows, :].rearrange("p n w -> p (n w)")
+
+        def copy_graph_bias(cb0):
             nc.scalar.copy(
-                out=dst.bitcast(F32), in_=spread[:, 0:rows, :].rearrange("p n w -> p (n w)")
+                out=bias_g[:, cb0 : cb0 + PAIR, :, :].rearrange("p i c k -> p (i c k)").bitcast(F32),
+                in_=spread_banks[cb0 * PAIR],
             )
 
-        def spread_graph_bias(cb0):
-            spread_rows(
-                bias_g[:, cb0 : cb0 + PAIR, :, :].rearrange("p i c k -> p (i c k)"),
-                cb0 * PAIR, PAIR * PAIR,
-            )
-
-        def spread_projection_bias():
-            spread_rows(bias_p[:], CHUNKS, PAIR)
+        def copy_projection_bias():
+            nc.scalar.copy(out=bias_p[:].bitcast(F32), in_=spread_banks[CHUNKS])
 
         def quantise(values, codes, scales):
             nc.vector.quantize_mx(out=codes.bitcast(FP8X4), scales=scales, in_=values)
 
-        mixed = keep.tile([P, B, STREAMS, P, PACK], BF16, align_bytes=64)
-        mixed_codes = keep.tile([P, B, STREAMS, P], U32, align_bytes=64)
-        mixed_scales = keep.tile([P, B, STREAMS, P], U8, align_bytes=64)
+        mixed = keep.tile([P, STREAMS, B, P, PACK], BF16, align_bytes=64)
+        mixed_codes = keep.tile([P, STREAMS, B, P], U32, align_bytes=64)
+        mixed_scales = keep.tile([P, STREAMS, B, P], U8, align_bytes=64)
 
         def round_by_scalar(dst, product, factor):
             if factor == 1.0:
@@ -167,7 +191,9 @@ def tile_block_pb_kernel(
             else:
                 nc.vector.tensor_scalar(out=dst, in0=product, scalar1=factor, scalar2=None, op0=MULT)
 
-        def mix_half(b, h, rounder=round_by_scalar):
+        mixed_banks = {}
+
+        def mix(b, h):
             bank = psum.tile([P, PACK, STREAMS, JOINTS], F32, tag="bank")
             for t in range(PACK):
                 half, parity = divmod(t, PACK // HALVES)
@@ -178,20 +204,18 @@ def tile_block_pb_kernel(
                     rhs=mixer[:].rearrange("p s i -> p (s i)"),
                     start=True, stop=True,
                 )
+            mixed_banks[b, h] = bank[:].rearrange("q t s i -> q s i t")
+
+        def round_mixed(b, h, rounder=round_by_scalar):
             joints = slice(h * JOINTS, (h + 1) * JOINTS)
-            products = bank[:].rearrange("q t s i -> q s i t")
             for s, factor in ((U, S_A2G), (V, 1.0)):
-                rounder(mixed[:, b, s, joints, :], products[:, s, :, :], factor)
+                rounder(mixed[:, s, b, joints, :], mixed_banks[b, h][:, s, :, :], factor)
 
-        def mix_streams(b):
-            for h in range(HALVES):
-                mix_half(b, h)
-
-        def quantise_streams(b):
+        def quantise_stream(s, b0, b1):
             quantise(
-                mixed[:, b, :, :, :].rearrange("q s j t -> q (s j t)"),
-                mixed_codes[:, b, :, :].rearrange("q s r -> q (s r)"),
-                mixed_scales[:, b, :, :].rearrange("q s r -> q (s r)"),
+                mixed[:, s, b0:b1, :, :].rearrange("q b j t -> q (b j t)"),
+                mixed_codes[:, s, b0:b1, :].rearrange("q b r -> q (b r)"),
+                mixed_scales[:, s, b0:b1, :].rearrange("q b r -> q (b r)"),
             )
 
         wg_turned = keep.tile([P, KINDS * C * PACK], BF16, align_bytes=64)
@@ -200,26 +224,33 @@ def tile_block_pb_kernel(
         wp_turned = keep.tile([P, C * PACK], BF16, align_bytes=64)
         wp_codes = keep.tile([P, C], U32, align_bytes=64)
         wp_scales = keep.tile([P, C], U8, align_bytes=64)
-        adj_grouped = keep.tile([P, P, KINDS], BF16, align_bytes=64)
-        adj_codes = keep.tile([P, P], U32, align_bytes=64)
-        adj_scales = keep.tile([P, P], U8, align_bytes=64)
+        adj_grouped = keep.tile([P, PAIR, P, KINDS], BF16, align_bytes=64)
+        adj_codes = keep.tile([P, PAIR, P], U32, align_bytes=64)
+        adj_scales = keep.tile([P, PAIR, P], U8, align_bytes=64)
 
-        def turn_rows(rows, turned, first_block, copiers):
+        turned_banks = {}
+
+        def turn_rows(rows, n):
             row_words = rows[:].bitcast(F32).rearrange("p (n w) -> p n w", w=C // 2)
-            words = turned[:].bitcast(F32).rearrange("q (n r h) -> q n r h", r=P, h=HALVES)
-            for n, copier in zip(range(first_block, first_block + KINDS, PAIR), copiers):
-                bank = psum.tile([P, PAIR, HALVES, P], F32, tag="bank")
-                for i in range(PAIR):
-                    for h in range(HALVES):
-                        nc.tensor.transpose(
-                            bank[:, i, h, :], row_words[:, n + i, h * P : (h + 1) * P], ident[:]
-                        )
-                copier(
-                    out=words[:, n : n + PAIR, :, :], in_=bank[:].rearrange("q i h r -> q i r h")
-                )
+            bank = psum.tile([P, PAIR, HALVES, P], F32, tag="bank")
+            for i in range(PAIR):
+                for h in range(HALVES):
+                    nc.tensor.transpose(
+                        bank[:, i, h, :], row_words[:, n + i, h * P : (h + 1) * P], ident[:]
+                    )
+            return bank[:].rearrange("q i h r -> q i r h")
 
-        def turn_graph_weights(cb, *copiers):
-            turn_rows(wg_rows, wg_turned, cb * KINDS, copiers or (nc.scalar.copy, nc.scalar.copy))
+        def copy_rows(turned, n, bank, copier):
+            words = turned[:].bitcast(F32).rearrange("q (n r h) -> q n r h", r=P, h=HALVES)
+            copier(out=words[:, n : n + PAIR, :, :], in_=bank)
+
+        def turn_graph_weights(cb):
+            for n in (cb * KINDS, cb * KINDS + PAIR):
+                turned_banks[n] = turn_rows(wg_rows, n)
+
+        def copy_graph_weights(cb, *copiers):
+            for n, copier in zip((cb * KINDS, cb * KINDS + PAIR), copiers):
+                copy_rows(wg_turned, n, turned_banks[n], copier)
 
         def quantise_graph_weights(cb):
             quantise(
@@ -229,21 +260,34 @@ def tile_block_pb_kernel(
             )
 
         def turn_projection():
-            turn_rows(wp_rows, wp_turned, 0, (nc.scalar.copy, nc.scalar.copy))
-            nc.scalar.copy(out=adj_grouped[:], in_=adj_rows[:].rearrange("j k w -> j w k"))
+            for n in (0, PAIR):
+                copy_rows(wp_turned, n, turn_rows(wp_rows, n), nc.scalar.copy)
+
+        def group_adjacency(turned):
+            if turned:
+                values = adj_pairs[:].rearrange("p m e w -> p w (m e)")
+            else:
+                values = adj_rows[:].rearrange("j k w -> j w k")
+            nc.scalar.copy(out=adj_grouped[:, turned, :, :], in_=values)
 
         def quantise_projection():
             quantise(wp_turned[:], wp_codes[:], wp_scales[:])
-            quantise(adj_grouped[:].rearrange("j w k -> j (w k)"), adj_codes[:], adj_scales[:])
+
+        def quantise_adjacency():
+            quantise(
+                adj_grouped[:].rearrange("j m w k -> j (m w k)"),
+                adj_codes[:].rearrange("j m w -> j (m w)"),
+                adj_scales[:].rearrange("j m w -> j (m w)"),
+            )
 
         y_values = {}
         y_codes = {}
         y_scales = {}
 
-        def open_batch(b):
-            y_values[b] = flow.tile([P, KINDS, P, KINDS], BF16, align_bytes=64, name="y_values")
-            y_codes[b] = flow.tile([P, C], U32, align_bytes=64, name="y_codes")
-            y_scales[b] = flow.tile([P, C], U8, align_bytes=64, name="y_scales")
+        def open_pair(n):
+            y_values[n] = flow.tile([P, PAIR, KINDS, P, KINDS], BF16, align_bytes=64, name="y_values")
+            y_codes[n] = flow.tile([P, PAIR, C], U32, align_bytes=64, name="y_codes")
+            y_scales[n] = flow.tile([P, PAIR, C], U8, align_bytes=64, name="y_scales")
 
         products = {}
 
@@ -251,8 +295,8 @@ def tile_block_pb_kernel(
             bank = psum.tile([P, KINDS, P], F32, tag="bank")
             nc.tensor.matmul_mx(
                 out=bank[:].rearrange("j k c -> j (k c)"),
-                lhsT=mixed_codes[:, b, U, :].bitcast(FP8X4),
-                lhsT_scale=mixed_scales[:, b, U, :],
+                lhsT=mixed_codes[:, U, b, :].bitcast(FP8X4),
+                lhsT_scale=mixed_scales[:, U, b, :],
                 rhs=wg_codes[:, cb * C : (cb + 1) * C].bitcast(FP8X4),
                 rhs_scale=wg_scales[:, cb * C : (cb + 1) * C],
                 start=True,
@@ -261,147 +305,289 @@ def tile_block_pb_kernel(
             products[b, cb] = bank[:].rearrange("j k c -> j c k")
 
         def add_by_vector(b, cb):
+            n, i = divmod(b, PAIR)
             nc.vector.tensor_tensor(
-                out=y_values[b][:, cb, :, :], in0=products[b, cb], in1=bias_g[:, cb, :, :], op=ADD
+                out=y_values[n][:, i, cb, :, :], in0=products[b, cb], in1=bias_g[:, cb, :, :],
+                op=ADD,
             )
 
         def add_by_gpsimd(b, cb):
+            n, i = divmod(b, PAIR)
             copied = flow.tile([P, P, KINDS], F32, name="copied")
             nc.scalar.copy(out=copied[:], in_=products[b, cb])
             nc.gpsimd.tensor_tensor(
-                out=y_values[b][:, cb, :, :], in0=copied[:], in1=bias_g[:, cb, :, :], op=ADD
+                out=y_values[n][:, i, cb, :, :], in0=copied[:], in1=bias_g[:, cb, :, :], op=ADD
             )
+
+        column_banks = {}
+        column_values = {}
+        row_banks = {}
+
+        def multiply_columns(n, cb):
+            batches = slice(n * PAIR, (n + 1) * PAIR)
+            for m in range(PAIR):
+                bank = psum.tile([P, PAIR, PAIR, P], F32, tag="bank")
+                for kk in range(PAIR):
+                    first = (cb * KINDS + m * PAIR + kk) * P
+                    nc.tensor.matmul_mx(
+                        out=bank[:, kk, :, :].rearrange("c b j -> c (b j)"),
+                        lhsT=wg_codes[:, first : first + P].bitcast(FP8X4),
+                        lhsT_scale=wg_scales[:, first : first + P],
+                        rhs=mixed_codes[:, U, batches, :].rearrange("q b j -> q (b j)").bitcast(FP8X4),
+                        rhs_scale=mixed_scales[:, U, batches, :].rearrange("q b j -> q (b j)"),
+                        start=True,
+                        stop=True,
+                    )
+                column_banks[n, cb, m] = bank
+
+        def add_on_columns(n, cb):
+            values = flow.tile([P, PAIR, PAIR, PAIR, P], BF16, name="column_values")
+            for m in range(PAIR):
+                for kk in range(PAIR):
+                    k = m * PAIR + kk
+                    nc.scalar.activation(
+                        out=values[:, m, :, kk, :], in_=column_banks[n, cb, m][:, kk, :, :],
+                        func=IDENTITY,
+                        bias=bias_parts[:, k * KINDS + cb : k * KINDS + cb + 1], scale=1.0,
+                    )
+            column_values[n, cb] = values
+
+        def turn_columns(n, cb):
+            words = column_values[n, cb][:].rearrange("c m b kk j -> c m b (kk j)").bitcast(F32)
+            bank = psum.tile([P, PAIR, PAIR, P], F32, tag="bank")
+            for i in range(PAIR):
+                for m in range(PAIR):
+                    nc.tensor.transpose(bank[:, i, m, :], words[:, m, i, :], ident[:])
+            row_banks[n, cb] = bank[:].rearrange("p b m c -> p b c m")
+
+        def copy_columns(n, cb, copier):
+            copier(out=y_values[n][:, :, cb, :, :].bitcast(F32), in_=row_banks[n, cb])
 
         def quantise_y(b, cb0=0, cb1=KINDS):
+            n, i = divmod(b, PAIR)
             columns = slice(cb0 * P, cb1 * P)
             quantise(
-                y_values[b][:, cb0:cb1, :, :].rearrange("j cb c k -> j (cb c k)"),
-                y_codes[b][:, columns],
-                y_scales[b][:, columns],
+                y_values[n][:, i, cb0:cb1, :, :].rearrange("j cb c k -> j (cb c k)"),
+                y_codes[n][:, i, columns],
+                y_scales[n][:, i, columns],
             )
 
-        residuals = keep.tile([P, B, C], F32)
+        residuals = {}
 
         def make_residual(b):
+            residuals[b] = flow.tile([P, C], F32, name="residual")
             nc.gpsimd.tensor_tensor(
-                out=residuals[:, b, :], in0=x_rows[:, b, :], in1=bias_p[:], op=ADD
+                out=residuals[b][:], in0=x_rows[:, b, :], in1=bias_p[:], op=ADD
             )
 
         totals = {}
 
-        def aggregate(b, cb0=0, cb1=KINDS):
+        def open_total(b):
+            totals[b] = psum.tile([P, C], F32, tag="bank", name="total")
+
+        def aggregate(b, cb0, cb1, turned):
+            n, i = divmod(b, PAIR)
             columns = slice(cb0 * P, cb1 * P)
-            total = psum.tile([P, C], F32, tag="bank")
             nc.tensor.matmul_mx(
-                out=total[:, columns],
-                lhsT=mixed_codes[:, b, V, :].bitcast(FP8X4),
-                lhsT_scale=mixed_scales[:, b, V, :],
+                out=totals[b][:, columns],
+                lhsT=mixed_codes[:, V, b, :].bitcast(FP8X4),
+                lhsT_scale=mixed_scales[:, V, b, :],
                 rhs=wp_codes[:, columns].bitcast(FP8X4),
                 rhs_scale=wp_scales[:, columns],
                 start=True,
                 stop=False,
             )
             nc.tensor.matmul_mx(
-                out=total[:, columns],
-                lhsT=adj_codes[:].bitcast(FP8X4),
-                lhsT_scale=adj_scales[:],
-                rhs=y_codes[b][:, columns].bitcast(FP8X4),
-                rhs_scale=y_scales[b][:, columns],
+                out=totals[b][:, columns],
+                lhsT=adj_codes[:, turned, :].bitcast(FP8X4),
+                lhsT_scale=adj_scales[:, turned, :],
+                rhs=y_codes[n][:, i, columns].bitcast(FP8X4),
+                rhs_scale=y_scales[n][:, i, columns],
                 start=False,
                 stop=True,
             )
-            totals[b, cb0] = total
+
+        def aggregate_all(b):
+            open_total(b)
+            straight = STRAIGHT[b // PAIR]
+            for cb0, cb1 in SPANS[straight]:
+                aggregate(b, cb0, cb1, 0 if cb0 < straight else 1)
 
         def finish(b, cb0=0, cb1=KINDS):
             columns = slice(cb0 * P, cb1 * P)
-            result = flow.tile([P, C], F32, name="result")
+            result = flow.tile([P, C], F32, name="result", bufs=B)
             nc.vector.tensor_tensor(
-                out=result[:, columns], in0=totals[b, cb0][:, columns],
-                in1=residuals[:, b, columns], op=ADD,
+                out=result[:, columns], in0=totals[b][:, columns],
+                in1=residuals[b][:, columns], op=ADD,
             )
             nc.sync.dma_start(out=out[b][:, columns], in_=result[:, columns])
 
-        mix_half(0, 0)
-        mix_half(0, 1, round_by_vector)
+        VC, SC = nc.vector.tensor_copy, nc.scalar.copy
+        mix(0, 0)
+        mix(0, 1)
         interleave_graph_bias()
-        quantise_streams(0)
-        turn_graph_weights(0, nc.scalar.copy, nc.vector.tensor_copy)
+        round_mixed(0, 0)
+        round_mixed(0, 1, round_by_vector)
         stand_biases_up()
-        mix_half(1, 0)
-        mix_half(1, 1, round_by_vector)
-        spread_graph_bias(0)
+        turn_graph_weights(0)
+        quantise_stream(U, 0, 1)
+        copy_graph_weights(0, SC, VC)
+        spread_rows(0, 4)
         quantise_graph_weights(0)
-        turn_graph_weights(1, nc.scalar.copy, nc.vector.tensor_copy)
-        quantise_streams(1)
-        for b in range(PAIR):
-            open_batch(b)
+        copy_graph_bias(0)
+        mix(1, 0)
+        mix(1, 1)
+        round_mixed(1, 0)
+        round_mixed(1, 1, round_by_vector)
+        for n in (0, 1):
+            open_pair(n)
         multiply(0, 0)
-        spread_projection_bias()
-        turn_graph_weights(2)
+        turn_graph_weights(1)
+        copy_graph_weights(1, SC, SC)
+        quantise_stream(U, 1, 2)
         multiply(1, 0)
         add_by_vector(0, 0)
-        quantise_graph_weights(1)
-        make_residual(0)
-        make_residual(1)
+        mix(2, 0)
+        mix(2, 1)
+        round_mixed(2, 0)
+        round_mixed(2, 1)
         add_by_vector(1, 0)
+        quantise_graph_weights(1)
+        spread_rows(4, 4)
+        spread_rows(8, 2)
+        turn_graph_weights(2)
+        copy_graph_bias(2)
+        copy_graph_weights(2, SC, SC)
+        quantise_stream(U, 2, 3)
         multiply(0, 1)
-        turn_graph_weights(3)
         multiply(1, 1)
-        spread_graph_bias(2)
-        quantise_graph_weights(2)
-        add_by_vector(0, 1)
-        multiply(0, 2)
-        mix_streams(2)
-        add_by_vector(1, 1)
-        multiply(1, 2)
-        quantise_graph_weights(3)
-        add_by_gpsimd(0, 2)
-        multiply(0, 3)
-        multiply(1, 3)
-        add_by_vector(1, 2)
-        quantise_streams(2)
-        add_by_vector(0, 3)
-        turn_projection()
-        add_by_vector(1, 3)
-        open_batch(2)
         multiply(2, 0)
         multiply(2, 1)
-        add_by_gpsimd(2, 0)
-        mix_streams(3)
-        quantise_y(0)
-        multiply(2, 2)
-        multiply(2, 3)
-        quantise_projection()
+        add_by_vector(0, 1)
+        copy_projection_bias()
+        mix(3, 0)
+        mix(3, 1)
+        round_mixed(3, 0)
+        round_mixed(3, 1)
+        add_by_vector(1, 1)
+        quantise_graph_weights(2)
+        add_by_vector(2, 0)
+        turn_graph_weights(3)
+        copy_graph_weights(3, SC, SC)
         add_by_vector(2, 1)
-        aggregate(0)
+        multiply(0, 2)
+        multiply(1, 2)
+        quantise_stream(U, 3, 4)
+        multiply(2, 2)
+        add_by_vector(0, 2)
+        multiply(3, 0)
+        multiply(3, 1)
+        add_by_vector(1, 2)
+        mix(4, 0)
+        mix(4, 1)
+        quantise_graph_weights(3)
+        multiply(3, 2)
+        add_by_vector(2, 2)
+        multiply(0, 3)
+        round_mixed(4, 0)
+        round_mixed(4, 1)
+        add_by_vector(3, 0)
+        mix(5, 0)
+        mix(5, 1)
+        multiply(1, 3)
+        make_residual(0)
+        make_residual(1)
         make_residual(2)
-        quantise_streams(3)
         make_residual(3)
-        finish(0)
+        add_by_vector(3, 1)
+        multiply(2, 3)
+        round_mixed(5, 0)
+        round_mixed(5, 1)
+        add_by_vector(3, 2)
+        multiply(3, 3)
+        lay_bias_on_partitions()
+        group_adjacency(0)
+        turn_projection()
+        group_adjacency(1)
+        add_by_vector(0, 3)
+        quantise_stream(U, 4, 6)
+        add_by_vector(1, 3)
+        open_pair(2)
+        multiply_columns(2, 2)
+        add_by_vector(2, 3)
+        multiply_columns(2, 3)
+        add_by_vector(3, 3)
+        add_on_columns(2, 2)
+        multiply(4, 0)
+        add_on_columns(2, 3)
 
-        for b in range(PAIR, B):
-            add_by_vector(b, 2)
-            if b + 1 < B:
-                open_batch(b + 1)
-                multiply(b + 1, 0)
-                multiply(b + 1, 1)
-                add_by_gpsimd(b + 1, 0)
-            quantise_y(b - 1)
-            if b + 2 < B:
-                mix_streams(b + 2)
-            add_by_vector(b, 3)
-            aggregate(b - 1)
-            if b + 1 < B:
-                multiply(b + 1, 2)
-                multiply(b + 1, 3)
-                add_by_vector(b + 1, 1)
-            if b + 2 < B:
-                quantise_streams(b + 2)
-                make_residual(b + 2)
-            finish(b - 1)
-        quantise_y(B - 1, 0, PAIR)
-        quantise_y(B - 1, PAIR, KINDS)
-        aggregate(B - 1, 0, PAIR)
-        aggregate(B - 1, PAIR, KINDS)
-        finish(B - 1, 0, PAIR)
-        finish(B - 1, PAIR, KINDS)
+        quantise_stream(V, 0, 4)
+        mix(6, 0)
+        mix(6, 1)
+        quantise_y(0)
+        round_mixed(6, 0)
+        round_mixed(6, 1)
+        multiply(5, 0)
+        mix(7, 0)
+        mix(7, 1)
+        quantise_y(1)
+        round_mixed(7, 0)
+        round_mixed(7, 1)
+        turn_columns(2, 2)
+        turn_columns(2, 3)
+        quantise_y(2)
+        copy_columns(2, 2, SC)
+        copy_columns(2, 3, SC)
+        quantise_y(3)
+        multiply(4, 1)
+        quantise_projection()
+        quantise_adjacency()
+        multiply(5, 1)
+        aggregate_all(0)
+        aggregate_all(1)
+        add_by_vector(4, 0)
+        add_by_vector(5, 0)
+        aggregate_all(2)
+        add_by_vector(4, 1)
+        finish(0)
+        make_residual(4)
+        quantise_stream(U, 6, 8)
+        open_pair(3)
+        multiply_columns(3, 2)
+        finish(1)
+        aggregate_all(3)
+        make_residual(5)
+        add_by_vector(5, 1)
+        multiply_columns(3, 3)
+        add_on_columns(3, 2)
+        finish(2)
+        make_residual(6)
+        multiply(6, 0)
+        multiply(7, 0)
+        finish(3)
+        make_residual(7)
+        add_on_columns(3, 3)
+        quantise_y(4)
+        multiply(6, 1)
+        add_by_vector(6, 0)
+        multiply(7, 1)
+        add_by_vector(7, 0)
+        quantise_stream(V, 4, 8)
+        turn_columns(3, 2)
+        aggregate_all(4)
+        quantise_y(5)
+        turn_columns(3, 3)
+        copy_columns(3, 2, SC)
+        copy_columns(3, 3, SC)
+        add_by_vector(6, 1)
+        aggregate_all(5)
+        add_by_vector(7, 1)
+        finish(4)
+        quantise_y(6)
+        finish(5)
+        quantise_y(7)
+        aggregate_all(6)
+        aggregate_all(7)
+        finish(6)
+        finish(7, 0, PAIR)
+        finish(7, PAIR, KINDS)

@@ -24,8 +24,8 @@ PAIR = 2
 CHUNKS = 8
 CHUNK = C // CHUNKS
 BANKS = 8
-STRAIGHT = (4, 4, 2, 2)
-SPANS = {4: ((0, 4),), 2: ((0, 2), (2, 4)), 0: ((0, 4),)}
+STRAIGHT = (4, 4, 2, 1)
+SPANS = {4: ((0, 4),), 2: ((0, 2), (2, 4)), 1: ((0, 1), (1, 2), (2, 4))}
 STREAMS = 2
 U, V = 0, 1
 S_G2A = 0.5
@@ -106,9 +106,6 @@ def tile_block_pb_kernel(
         for b in range(1, KINDS):
             load_streams(b, b + 1)
             load_weights(b)
-        load_residuals(0)
-        load_streams(4, 6)
-        load_residuals(2)
         nc.sync.dma_start(out=adj_rows[:], in_=adj.rearrange("k j w -> j k w"))
         adj_dram = adj.rearrange("(m kk) (jj e) w -> kk jj m (e w)", kk=PAIR, e=PAIR)
         for kk in range(PAIR):
@@ -118,6 +115,9 @@ def tile_block_pb_kernel(
                 ),
                 in_=adj_dram[kk],
             )
+        load_residuals(0)
+        load_streams(4, 6)
+        load_residuals(2)
         nc.sync.dma_start(
             out=wp_rows[:].rearrange("p (ob c) -> p ob c", c=C),
             in_=proj_w.rearrange("(ob p) c -> p ob c", p=P),
@@ -268,7 +268,10 @@ def tile_block_pb_kernel(
                 values = adj_pairs[:].rearrange("p m e w -> p w (m e)")
             else:
                 values = adj_rows[:].rearrange("j k w -> j w k")
-            nc.scalar.copy(out=adj_grouped[:, turned, :, :], in_=values)
+            nc.gpsimd.tensor_scalar(
+                out=adj_grouped[:, turned, :, :], in0=values,
+                scalar1=1.0, scalar2=0.0, op0=MULT, op1=ADD,
+            )
 
         def quantise_projection():
             quantise(wp_turned[:], wp_codes[:], wp_scales[:])
@@ -453,17 +456,17 @@ def tile_block_pb_kernel(
         round_mixed(2, 1)
         add_by_vector(1, 0)
         quantise_graph_weights(1)
-        spread_rows(4, 4)
-        spread_rows(8, 2)
         turn_graph_weights(2)
-        copy_graph_bias(2)
         copy_graph_weights(2, SC, SC)
         quantise_stream(U, 2, 3)
         multiply(0, 1)
         multiply(1, 1)
         multiply(2, 0)
         multiply(2, 1)
+        spread_rows(4, 4)
+        spread_rows(8, 2)
         add_by_vector(0, 1)
+        copy_graph_bias(2)
         copy_projection_bias()
         mix(3, 0)
         mix(3, 1)
@@ -495,6 +498,8 @@ def tile_block_pb_kernel(
         mix(5, 0)
         mix(5, 1)
         multiply(1, 3)
+        group_adjacency(0)
+        group_adjacency(1)
         make_residual(0)
         make_residual(1)
         make_residual(2)
@@ -506,9 +511,7 @@ def tile_block_pb_kernel(
         add_by_vector(3, 2)
         multiply(3, 3)
         lay_bias_on_partitions()
-        group_adjacency(0)
         turn_projection()
-        group_adjacency(1)
         add_by_vector(0, 3)
         quantise_stream(U, 4, 6)
         add_by_vector(1, 3)
@@ -549,16 +552,18 @@ def tile_block_pb_kernel(
         add_by_vector(5, 0)
         aggregate_all(2)
         add_by_vector(4, 1)
-        finish(0)
-        make_residual(4)
         quantise_stream(U, 6, 8)
         open_pair(3)
-        multiply_columns(3, 2)
+        multiply_columns(3, 3)
+        finish(0)
+        make_residual(4)
+        quantise_stream(V, 4, 8)
         finish(1)
         aggregate_all(3)
         make_residual(5)
+        multiply_columns(3, 2)
+        add_on_columns(3, 3)
         add_by_vector(5, 1)
-        multiply_columns(3, 3)
         add_on_columns(3, 2)
         finish(2)
         make_residual(6)
@@ -566,28 +571,30 @@ def tile_block_pb_kernel(
         multiply(7, 0)
         finish(3)
         make_residual(7)
-        add_on_columns(3, 3)
         quantise_y(4)
-        multiply(6, 1)
+        multiply_columns(3, 1)
         add_by_vector(6, 0)
-        multiply(7, 1)
-        add_by_vector(7, 0)
-        quantise_stream(V, 4, 8)
+        turn_columns(3, 3)
         turn_columns(3, 2)
+        add_on_columns(3, 1)
         aggregate_all(4)
         quantise_y(5)
-        turn_columns(3, 3)
-        copy_columns(3, 2, SC)
+        add_by_vector(7, 0)
         copy_columns(3, 3, SC)
-        add_by_vector(6, 1)
+        turn_columns(3, 1)
         aggregate_all(5)
-        add_by_vector(7, 1)
         finish(4)
-        quantise_y(6)
-        finish(5)
-        quantise_y(7)
+        copy_columns(3, 2, VC)
+        copy_columns(3, 1, SC)
+        quantise_y(6, 0, 1)
+        quantise_y(7, 0, 1)
+        quantise_y(6, 2, 4)
+        quantise_y(7, 2, 4)
+        quantise_y(6, 1, 2)
         aggregate_all(6)
+        quantise_y(7, 1, 2)
         aggregate_all(7)
+        finish(5)
         finish(6)
         finish(7, 0, PAIR)
         finish(7, PAIR, KINDS)

@@ -72,17 +72,18 @@ def tile_block_pb_kernel(
         wg_dram = gcn2_w.rearrange("(k cb p) c -> cb p k c", k=KINDS, cb=KINDS)
         wg_blocks = wg_rows[:].rearrange("p (cb k c) -> p cb k c", cb=KINDS, k=KINDS)
 
-        def load_streams(b0, b1):
+        def load_graph_features(b, h0, h1, queue):
+            queue.dma_start(
+                out=streams[JOINTS:P, h0:h1, b, :],
+                in_=xg1[b].rearrange("(h i) c -> i h c", h=HALVES)[:, h0:h1, :],
+            )
+
+        def load_attention(b0, b1, h):
             a_dram = attn_o[b0:b1].rearrange("b n (h i) d -> h i (b n) d", h=HALVES)
-            g_dram = xg1[b0:b1].rearrange("b (h i) c -> h i b c", h=HALVES)
-            for h in range(HALVES):
-                nc.sync.dma_start(out=streams[JOINTS:P, h, b0:b1, :], in_=g_dram[h])
-                nc.sync.dma_start(
-                    out=streams[0:JOINTS, h, b0:b1, :].rearrange(
-                        "i b (n d) -> i (b n) d", d=HEAD_DIM
-                    ),
-                    in_=a_dram[h],
-                )
+            nc.sync.dma_start(
+                out=streams[0:JOINTS, h, b0:b1, :].rearrange("i b (n d) -> i (b n) d", d=HEAD_DIM),
+                in_=a_dram[h],
+            )
 
         def load_weights(cb, k0=0, k1=KINDS):
             nc.sync.dma_start(out=wg_blocks[:, cb, k0:k1, :], in_=wg_dram[cb][:, k0:k1, :])
@@ -93,7 +94,11 @@ def tile_block_pb_kernel(
                 in_=x[b0 : b0 + PAIR].rearrange("b j c -> j b c"),
             )
 
-        load_streams(0, 1)
+        for b in range(1, B):
+            load_graph_features(b, 0, HALVES, nc.gpsimd)
+        for h in range(HALVES):
+            load_graph_features(0, h, h + 1, nc.sync)
+            load_attention(0, 1, h)
         nc.sync.dma_start(
             out=bias_raw[:], in_=gcn2_b.rearrange("(k n c) -> n k c", k=KINDS, n=CHUNKS)
         )
@@ -103,9 +108,15 @@ def tile_block_pb_kernel(
         )
         load_weights(0, 0, PAIR)
         load_weights(0, PAIR, KINDS)
-        for b in range(1, KINDS):
-            load_streams(b, b + 1)
-            load_weights(b)
+        for h in range(HALVES):
+            load_attention(1, 2, h)
+        load_weights(1)
+        for h in range(HALVES):
+            load_attention(2, 3, h)
+        load_weights(2)
+        for h in range(HALVES):
+            load_attention(3, 4, h)
+        load_weights(3)
         nc.sync.dma_start(out=adj_rows[:], in_=adj.rearrange("k j w -> j k w"))
         adj_dram = adj.rearrange("(m kk) (jj e) w -> kk jj m (e w)", kk=PAIR, e=PAIR)
         for kk in range(PAIR):
@@ -116,7 +127,8 @@ def tile_block_pb_kernel(
                 in_=adj_dram[kk],
             )
         load_residuals(0)
-        load_streams(4, 6)
+        for h in range(HALVES):
+            load_attention(4, 6, h)
         load_residuals(2)
         nc.sync.dma_start(
             out=wp_rows[:].rearrange("p (ob c) -> p ob c", c=C),
@@ -125,7 +137,8 @@ def tile_block_pb_kernel(
         nc.sync.dma_start(
             out=bias_natural[0 : KINDS * KINDS, :], in_=gcn2_b.rearrange("(r c) -> r c", c=P)
         )
-        load_streams(6, 8)
+        for h in range(HALVES):
+            load_attention(6, 8, h)
         load_residuals(4)
         load_residuals(6)
 

@@ -62,7 +62,7 @@ def tile_block_pb_kernel(
         bias_raw = keep.tile([CHUNKS, KINDS, CHUNK], BF16)
         bias_natural = keep.tile([P, P], BF16)
         nc.vector.memset(bias_natural[:], 0.0)
-        streams = keep.tile([P, HALVES, B, C], BF16)
+        streams = keep.tile([P, B, HALVES, C], BF16)
         wg_rows = keep.tile([P, KINDS * KINDS * C], BF16)
         wp_rows = keep.tile([P, KINDS * C], BF16)
         adj_rows = keep.tile([P, KINDS, P], BF16)
@@ -74,15 +74,14 @@ def tile_block_pb_kernel(
 
         def load_graph_features(b, h0, h1, queue):
             queue.dma_start(
-                out=streams[JOINTS:P, h0:h1, b, :],
+                out=streams[JOINTS:P, b, h0:h1, :],
                 in_=xg1[b].rearrange("(h i) c -> i h c", h=HALVES)[:, h0:h1, :],
             )
 
-        def load_attention(b0, b1, h):
-            a_dram = attn_o[b0:b1].rearrange("b n (h i) d -> h i (b n) d", h=HALVES)
+        def load_attention(b, h):
             nc.sync.dma_start(
-                out=streams[0:JOINTS, h, b0:b1, :].rearrange("i b (n d) -> i (b n) d", d=HEAD_DIM),
-                in_=a_dram[h],
+                out=streams[0:JOINTS, b, h, :].rearrange("i (n d) -> i n d", d=HEAD_DIM),
+                in_=attn_o[b].rearrange("n (h i) d -> h i n d", h=HALVES)[h],
             )
 
         def load_weights(cb, k0=0, k1=KINDS):
@@ -98,7 +97,7 @@ def tile_block_pb_kernel(
             load_graph_features(b, 0, HALVES, nc.gpsimd)
         for h in range(HALVES):
             load_graph_features(0, h, h + 1, nc.sync)
-            load_attention(0, 1, h)
+            load_attention(0, h)
         nc.sync.dma_start(
             out=bias_raw[:], in_=gcn2_b.rearrange("(k n c) -> n k c", k=KINDS, n=CHUNKS)
         )
@@ -109,13 +108,13 @@ def tile_block_pb_kernel(
         load_weights(0, 0, PAIR)
         load_weights(0, PAIR, KINDS)
         for h in range(HALVES):
-            load_attention(1, 2, h)
+            load_attention(1, h)
         load_weights(1)
         for h in range(HALVES):
-            load_attention(2, 3, h)
+            load_attention(2, h)
         load_weights(2)
         for h in range(HALVES):
-            load_attention(3, 4, h)
+            load_attention(3, h)
         load_weights(3)
         nc.sync.dma_start(out=adj_rows[:], in_=adj.rearrange("k j w -> j k w"))
         adj_dram = adj.rearrange("(m kk) (jj e) w -> kk jj m (e w)", kk=PAIR, e=PAIR)
@@ -127,8 +126,9 @@ def tile_block_pb_kernel(
                 in_=adj_dram[kk],
             )
         load_residuals(0)
-        for h in range(HALVES):
-            load_attention(4, 6, h)
+        for b in range(4, 6):
+            for h in range(HALVES):
+                load_attention(b, h)
         load_residuals(2)
         nc.sync.dma_start(
             out=wp_rows[:].rearrange("p (ob c) -> p ob c", c=C),
@@ -137,8 +137,9 @@ def tile_block_pb_kernel(
         nc.sync.dma_start(
             out=bias_natural[0 : KINDS * KINDS, :], in_=gcn2_b.rearrange("(r c) -> r c", c=P)
         )
-        for h in range(HALVES):
-            load_attention(6, 8, h)
+        for b in range(6, 8):
+            for h in range(HALVES):
+                load_attention(b, h)
         load_residuals(4)
         load_residuals(6)
 
@@ -213,7 +214,7 @@ def tile_block_pb_kernel(
                 first = half * (C // HALVES)
                 nc.tensor.matmul(
                     out=bank[:, t, :, :].rearrange("q s i -> q (s i)"),
-                    lhsT=streams[:, h, b, first + parity : first + C // HALVES : 2],
+                    lhsT=streams[:, b, h, first + parity : first + C // HALVES : 2],
                     rhs=mixer[:].rearrange("p s i -> p (s i)"),
                     start=True, stop=True,
                 )
@@ -358,8 +359,8 @@ def tile_block_pb_kernel(
 
         def add_on_columns(n, cb):
             values = flow.tile([P, PAIR, PAIR, PAIR, P], BF16, name="column_values")
-            for m in range(PAIR):
-                for kk in range(PAIR):
+            for kk in range(PAIR):
+                for m in range(PAIR):
                     k = m * PAIR + kk
                     nc.scalar.activation(
                         out=values[:, m, :, kk, :], in_=column_banks[n, cb, m][:, kk, :, :],
@@ -377,7 +378,10 @@ def tile_block_pb_kernel(
             row_banks[n, cb] = bank[:].rearrange("p b m c -> p b c m")
 
         def copy_columns(n, cb, copier):
-            copier(out=y_values[n][:, :, cb, :, :].bitcast(F32), in_=row_banks[n, cb])
+            for i in range(PAIR):
+                copier(
+                    out=y_values[n][:, i, cb, :, :].bitcast(F32), in_=row_banks[n, cb][:, i, :, :]
+                )
 
         def quantise_y(b, cb0=0, cb1=KINDS):
             n, i = divmod(b, PAIR)

@@ -52,17 +52,24 @@ def tile_block_pb_kernel(
         ident_bf16 = keep.tile([P, P], BF16)
         nc.vector.tensor_copy(out=ident_bf16[:], in_=ident[:])
 
-        mixer = keep.tile([P, STREAMS, JOINTS], BF16)
-        for s, factor in ((U, G_IN_U), (V, S_G2A)):
-            nc.vector.scalar_tensor_tensor(
-                out=mixer[:, s, :], in0=ident[:, JOINTS:P], scalar=factor, in1=ident[:, 0:JOINTS],
-                op0=MULT, op1=ADD,
-            )
+        mixers = keep.tile([P, PAIR, STREAMS, JOINTS], BF16)
+        for m, a_columns, g_columns in (
+            (0, ident[:, 0:JOINTS], ident[:, JOINTS:P]), (1, ident[:, 0:P:2], ident[:, 1:P:2]),
+        ):
+            for s, factor in ((U, G_IN_U), (V, S_G2A)):
+                nc.vector.scalar_tensor_tensor(
+                    out=mixers[:, m, s, :], in0=g_columns, scalar=factor, in1=a_columns,
+                    op0=MULT, op1=ADD,
+                )
 
         bias_raw = keep.tile([CHUNKS, KINDS, CHUNK], BF16)
         bias_natural = keep.tile([P, P], BF16)
         nc.vector.memset(bias_natural[:], 0.0)
-        streams = keep.tile([P, B, HALVES, C], BF16)
+        streams = {}
+        for b in range(B):
+            streams[b] = keep.tile([P, HALVES, C], BF16, name="streams_%d" % b)
+        a_rows = {b: slice(0, JOINTS) if b == 0 else slice(0, P, 2) for b in range(B)}
+        g_rows = {b: slice(JOINTS, P) if b == 0 else slice(1, P, 2) for b in range(B)}
         wg_rows = keep.tile([P, KINDS * KINDS * C], BF16)
         wp_rows = keep.tile([P, KINDS * C], BF16)
         adj_rows = keep.tile([P, KINDS, P], BF16)
@@ -72,15 +79,15 @@ def tile_block_pb_kernel(
         wg_dram = gcn2_w.rearrange("(k cb p) c -> cb p k c", k=KINDS, cb=KINDS)
         wg_blocks = wg_rows[:].rearrange("p (cb k c) -> p cb k c", cb=KINDS, k=KINDS)
 
-        def load_graph_features(b, h0, h1, queue):
-            queue.dma_start(
-                out=streams[JOINTS:P, b, h0:h1, :],
+        def load_graph_features(b, h0=0, h1=HALVES):
+            nc.sync.dma_start(
+                out=streams[b][g_rows[b], h0:h1, :],
                 in_=xg1[b].rearrange("(h i) c -> i h c", h=HALVES)[:, h0:h1, :],
             )
 
         def load_attention(b, h):
             nc.sync.dma_start(
-                out=streams[0:JOINTS, b, h, :].rearrange("i (n d) -> i n d", d=HEAD_DIM),
+                out=streams[b][a_rows[b], h, :].rearrange("i (n d) -> i n d", d=HEAD_DIM),
                 in_=attn_o[b].rearrange("n (h i) d -> h i n d", h=HALVES)[h],
             )
 
@@ -93,29 +100,39 @@ def tile_block_pb_kernel(
                 in_=x[b0 : b0 + PAIR].rearrange("b j c -> j b c"),
             )
 
-        for b in range(1, B):
-            load_graph_features(b, 0, HALVES, nc.gpsimd)
         for h in range(HALVES):
-            load_graph_features(0, h, h + 1, nc.sync)
+            load_graph_features(0, h, h + 1)
             load_attention(0, h)
         nc.sync.dma_start(
             out=bias_raw[:], in_=gcn2_b.rearrange("(k n c) -> n k c", k=KINDS, n=CHUNKS)
         )
+        load_graph_features(1)
         nc.sync.dma_start(
             out=bias_rows[CHUNKS : CHUNKS + PAIR, :],
             in_=proj_b.rearrange("(n c) -> n c", c=PAIR * P),
         )
         load_weights(0, 0, PAIR)
         load_weights(0, PAIR, KINDS)
-        for h in range(HALVES):
-            load_attention(1, h)
+        load_graph_features(2)
+        load_attention(1, 0)
+        load_attention(1, 1)
         load_weights(1)
-        for h in range(HALVES):
-            load_attention(2, h)
+        load_graph_features(3)
+        load_attention(2, 0)
+        load_attention(2, 1)
         load_weights(2)
-        for h in range(HALVES):
-            load_attention(3, h)
+        load_graph_features(4)
+        load_attention(3, 0)
+        load_attention(3, 1)
         load_weights(3)
+        load_residuals(0)
+        load_graph_features(5)
+        load_attention(4, 0)
+        load_attention(4, 1)
+        load_residuals(2)
+        load_graph_features(6)
+        load_attention(5, 0)
+        load_attention(5, 1)
         nc.sync.dma_start(out=adj_rows[:], in_=adj.rearrange("k j w -> j k w"))
         adj_dram = adj.rearrange("(m kk) (jj e) w -> kk jj m (e w)", kk=PAIR, e=PAIR)
         for kk in range(PAIR):
@@ -125,11 +142,6 @@ def tile_block_pb_kernel(
                 ),
                 in_=adj_dram[kk],
             )
-        load_residuals(0)
-        for b in range(4, 6):
-            for h in range(HALVES):
-                load_attention(b, h)
-        load_residuals(2)
         nc.sync.dma_start(
             out=wp_rows[:].rearrange("p (ob c) -> p ob c", c=C),
             in_=proj_w.rearrange("(ob p) c -> p ob c", p=P),
@@ -137,9 +149,11 @@ def tile_block_pb_kernel(
         nc.sync.dma_start(
             out=bias_natural[0 : KINDS * KINDS, :], in_=gcn2_b.rearrange("(r c) -> r c", c=P)
         )
-        for b in range(6, 8):
-            for h in range(HALVES):
-                load_attention(b, h)
+        load_graph_features(7)
+        load_attention(6, 0)
+        load_attention(6, 1)
+        load_attention(7, 0)
+        load_attention(7, 1)
         load_residuals(4)
         load_residuals(6)
 
@@ -214,8 +228,8 @@ def tile_block_pb_kernel(
                 first = half * (C // HALVES)
                 nc.tensor.matmul(
                     out=bank[:, t, :, :].rearrange("q s i -> q (s i)"),
-                    lhsT=streams[:, b, h, first + parity : first + C // HALVES : 2],
-                    rhs=mixer[:].rearrange("p s i -> p (s i)"),
+                    lhsT=streams[b][:, h, first + parity : first + C // HALVES : 2],
+                    rhs=mixers[:, min(b, 1), :, :].rearrange("p s i -> p (s i)"),
                     start=True, stop=True,
                 )
             mixed_banks[b, h] = bank[:].rearrange("q t s i -> q s i t")
@@ -282,10 +296,7 @@ def tile_block_pb_kernel(
                 values = adj_pairs[:].rearrange("p m e w -> p w (m e)")
             else:
                 values = adj_rows[:].rearrange("j k w -> j w k")
-            nc.gpsimd.tensor_scalar(
-                out=adj_grouped[:, turned, :, :], in0=values,
-                scalar1=1.0, scalar2=0.0, op0=MULT, op1=ADD,
-            )
+            nc.scalar.copy(out=adj_grouped[:, turned, :, :], in_=values)
 
         def quantise_projection():
             quantise(wp_turned[:], wp_codes[:], wp_scales[:])
@@ -515,8 +526,6 @@ def tile_block_pb_kernel(
         mix(5, 0)
         mix(5, 1)
         multiply(1, 3)
-        group_adjacency(0)
-        group_adjacency(1)
         make_residual(0)
         make_residual(1)
         make_residual(2)
@@ -528,7 +537,9 @@ def tile_block_pb_kernel(
         add_by_vector(3, 2)
         multiply(3, 3)
         lay_bias_on_partitions()
+        group_adjacency(0)
         turn_projection()
+        group_adjacency(1)
         add_by_vector(0, 3)
         quantise_stream(U, 4, 6)
         add_by_vector(1, 3)

@@ -117,6 +117,9 @@ def tile_block_pb_kernel(
         load_attention(1, 0)
         load_attention(1, 1)
         load_weights(1)
+        nc.sync.dma_start(
+            out=bias_natural[0 : KINDS * KINDS, :], in_=gcn2_b.rearrange("(r c) -> r c", c=P)
+        )
         load_graph_features(3)
         load_attention(2, 0)
         load_attention(2, 1)
@@ -133,6 +136,10 @@ def tile_block_pb_kernel(
         load_graph_features(6)
         load_attention(5, 0)
         load_attention(5, 1)
+        nc.sync.dma_start(
+            out=wp_rows[:].rearrange("p (ob c) -> p ob c", c=C),
+            in_=proj_w.rearrange("(ob p) c -> p ob c", p=P),
+        )
         nc.sync.dma_start(out=adj_rows[:], in_=adj.rearrange("k j w -> j k w"))
         adj_dram = adj.rearrange("(m kk) (jj e) w -> kk jj m (e w)", kk=PAIR, e=PAIR)
         for kk in range(PAIR):
@@ -142,13 +149,6 @@ def tile_block_pb_kernel(
                 ),
                 in_=adj_dram[kk],
             )
-        nc.sync.dma_start(
-            out=wp_rows[:].rearrange("p (ob c) -> p ob c", c=C),
-            in_=proj_w.rearrange("(ob p) c -> p ob c", p=P),
-        )
-        nc.sync.dma_start(
-            out=bias_natural[0 : KINDS * KINDS, :], in_=gcn2_b.rearrange("(r c) -> r c", c=P)
-        )
         load_graph_features(7)
         load_attention(6, 0)
         load_attention(6, 1)
@@ -301,11 +301,10 @@ def tile_block_pb_kernel(
         def quantise_projection():
             quantise(wp_turned[:], wp_codes[:], wp_scales[:])
 
-        def quantise_adjacency():
+        def quantise_adjacency(turned):
             quantise(
-                adj_grouped[:].rearrange("j m w k -> j (m w k)"),
-                adj_codes[:].rearrange("j m w -> j (m w)"),
-                adj_scales[:].rearrange("j m w -> j (m w)"),
+                adj_grouped[:, turned, :, :].rearrange("j w k -> j (w k)"),
+                adj_codes[:, turned, :], adj_scales[:, turned, :],
             )
 
         y_values = {}
@@ -478,6 +477,7 @@ def tile_block_pb_kernel(
         quantise_stream(U, 1, 2)
         multiply(1, 0)
         add_by_vector(0, 0)
+        quantise_stream(V, 0, 2)
         mix(2, 0)
         mix(2, 1)
         round_mixed(2, 0)
@@ -493,9 +493,11 @@ def tile_block_pb_kernel(
         multiply(2, 1)
         spread_rows(4, 4)
         spread_rows(8, 2)
+        quantise_stream(V, 2, 3)
         add_by_vector(0, 1)
         copy_graph_bias(2)
         copy_projection_bias()
+        lay_bias_on_partitions()
         mix(3, 0)
         mix(3, 1)
         round_mixed(3, 0)
@@ -508,6 +510,7 @@ def tile_block_pb_kernel(
         add_by_vector(2, 1)
         multiply(0, 2)
         multiply(1, 2)
+        quantise_stream(V, 3, 4)
         quantise_stream(U, 3, 4)
         multiply(2, 2)
         add_by_vector(0, 2)
@@ -536,10 +539,8 @@ def tile_block_pb_kernel(
         round_mixed(5, 1)
         add_by_vector(3, 2)
         multiply(3, 3)
-        lay_bias_on_partitions()
         group_adjacency(0)
         turn_projection()
-        group_adjacency(1)
         add_by_vector(0, 3)
         quantise_stream(U, 4, 6)
         add_by_vector(1, 3)
@@ -551,8 +552,8 @@ def tile_block_pb_kernel(
         add_on_columns(2, 2)
         multiply(4, 0)
         add_on_columns(2, 3)
+        group_adjacency(1)
 
-        quantise_stream(V, 0, 4)
         mix(6, 0)
         mix(6, 1)
         quantise_y(0)
@@ -572,7 +573,8 @@ def tile_block_pb_kernel(
         quantise_y(3)
         multiply(4, 1)
         quantise_projection()
-        quantise_adjacency()
+        quantise_adjacency(0)
+        quantise_adjacency(1)
         multiply(5, 1)
         aggregate_all(0)
         aggregate_all(1)
@@ -612,16 +614,22 @@ def tile_block_pb_kernel(
         turn_columns(3, 1)
         aggregate_all(5)
         finish(4)
-        copy_columns(3, 2, VC)
+        copy_columns(3, 2, SC)
         copy_columns(3, 1, SC)
         quantise_y(6, 0, 1)
         quantise_y(7, 0, 1)
         quantise_y(6, 2, 4)
+        open_total(6)
+        aggregate(6, 0, 1, 0)
+        aggregate(6, 2, 4, 1)
         quantise_y(7, 2, 4)
+        open_total(7)
+        aggregate(7, 0, 1, 0)
+        aggregate(7, 2, 4, 1)
         quantise_y(6, 1, 2)
-        aggregate_all(6)
+        aggregate(6, 1, 2, 1)
         quantise_y(7, 1, 2)
-        aggregate_all(7)
+        aggregate(7, 1, 2, 1)
         finish(5)
         finish(6)
         finish(7, 0, PAIR)

from contextlib import ExitStack

import concourse.mybir as mybir
from concourse.masks import make_identity

F32 = mybir.dt.float32
BF16 = mybir.dt.bfloat16
U32 = mybir.dt.uint32
U8 = mybir.dt.uint8
FP8X4 = mybir.dt.float8_e4m3fn_x4
ADD = mybir.AluOpType.add
MULT = mybir.AluOpType.mult
IDENTITY = mybir.ActivationFunctionType.Identity

P = 128
PACK = 4
B = 8
C = 512
KINDS = 4
HEAD_DIM = 64
HALVES = 2
JOINTS = P // HALVES
PAIR = 2
CHUNKS = 8
CHUNK = C // CHUNKS
BANKS = 8
STRAIGHT = (4, 4, 2, 1)
SPANS = {4: ((0, 4),), 2: ((0, 2), (2, 4)), 1: ((0, 1), (1, 2), (2, 4))}
STREAMS = 2
U, V = 0, 1
S_G2A = 0.5
S_A2G = 0.8
G_IN_U = 1.25

FLOPS = 2 * B * P * C * (C + KINDS * C) + 2 * B * P * (KINDS * P) * C


def tile_block_pb_kernel(
    tc, attn_o, xg1, x, adj, proj_w, proj_b, gcn2_w, gcn2_b, out
):
    nc = tc.nc
    with ExitStack() as ctx:
        ctx.enter_context(tc.manual_schedule())
        keep = ctx.enter_context(tc.tile_pool(name="keep", bufs=1))
        flow = ctx.enter_context(tc.tile_pool(name="flow", bufs=4))
        psum = ctx.enter_context(tc.psum_pool(name="psum", bufs=BANKS))

        bias_rows = keep.tile([P, PAIR * P], BF16)
        nc.vector.memset(bias_rows[:], 0.0)
        ident = keep.tile([P, P], F32)
        make_identity(nc, ident[:])
        ident_bf16 = keep.tile([P, P], BF16)
        nc.vector.tensor_copy(out=ident_bf16[:], in_=ident[:])

        mixers = keep.tile([P, PAIR, STREAMS, JOINTS], BF16)
        for m, a_columns, g_columns in (
            (0, ident[:, 0:JOINTS], ident[:, JOINTS:P]), (1, ident[:, 0:P:2], ident[:, 1:P:2]),
        ):
            for s, factor in ((U, G_IN_U), (V, S_G2A)):
                nc.vector.scalar_tensor_tensor(
                    out=mixers[:, m, s, :], in0=g_columns, scalar=factor, in1=a_columns,
                    op0=MULT, op1=ADD,
                )

        bias_raw = keep.tile([CHUNKS, KINDS, CHUNK], BF16)
        bias_natural = keep.tile([P, P], BF16)
        nc.vector.memset(bias_natural[:], 0.0)
        streams = {}
        for b in range(B):
            streams[b] = keep.tile([P, HALVES, C], BF16, name="streams_%d" % b)
        a_rows = {b: slice(0, JOINTS) if b == 0 else slice(0, P, 2) for b in range(B)}
        g_rows = {b: slice(JOINTS, P) if b == 0 else slice(1, P, 2) for b in range(B)}
        wg_rows = keep.tile([P, KINDS * KINDS * C], BF16)
        wp_rows = keep.tile([P, KINDS * C], BF16)
        adj_rows = keep.tile([P, KINDS, P], BF16)
        adj_pairs = keep.tile([P, PAIR, PAIR, P], BF16)
        x_rows = keep.tile([P, B, C], BF16)

        wg_dram = gcn2_w.rearrange("(k cb p) c -> cb p k c", k=KINDS, cb=KINDS)
        wg_blocks = wg_rows[:].rearrange("p (cb k c) -> p cb k c", cb=KINDS, k=KINDS)

        def load_graph_features(b, h0=0, h1=HALVES):
            nc.sync.dma_start(
                out=streams[b][g_rows[b], h0:h1, :],
                in_=xg1[b].rearrange("(h i) c -> i h c", h=HALVES)[:, h0:h1, :],
            )

        def load_attention(b, h):
            nc.sync.dma_start(
                out=streams[b][a_rows[b], h, :].rearrange("i (n d) -> i n d", d=HEAD_DIM),
                in_=attn_o[b].rearrange("n (h i) d -> h i n d", h=HALVES)[h],
            )

        def load_weights(cb, k0=0, k1=KINDS):
            nc.sync.dma_start(out=wg_blocks[:, cb, k0:k1, :], in_=wg_dram[cb][:, k0:k1, :])

        def load_residuals(b0):
            nc.sync.dma_start(
                out=x_rows[:, b0 : b0 + PAIR, :],
                in_=x[b0 : b0 + PAIR].rearrange("b j c -> j b c"),
            )

        for h in range(HALVES):
            load_graph_features(0, h, h + 1)
            load_attention(0, h)
        nc.sync.dma_start(
            out=bias_raw[:], in_=gcn2_b.rearrange("(k n c) -> n k c", k=KINDS, n=CHUNKS)
        )
        load_graph_features(1)
        nc.sync.dma_start(
            out=bias_rows[CHUNKS : CHUNKS + PAIR, :],
            in_=proj_b.rearrange("(n c) -> n c", c=PAIR * P),
        )
        load_weights(0, 0, PAIR)
        load_weights(0, PAIR, KINDS)
        load_graph_features(2)
        load_attention(1, 0)
        load_attention(1, 1)
        load_weights(1)
        nc.sync.dma_start(
            out=bias_natural[0 : KINDS * KINDS, :], in_=gcn2_b.rearrange("(r c) -> r c", c=P)
        )
        load_graph_features(3)
        load_attention(2, 0)
        load_attention(2, 1)
        load_weights(2)
        load_graph_features(4)
        load_attention(3, 0)
        load_attention(3, 1)
        load_weights(3)
        load_residuals(0)
        load_graph_features(5)
        load_attention(4, 0)
        load_attention(4, 1)
        load_residuals(2)
        load_graph_features(6)
        load_attention(5, 0)
        load_attention(5, 1)
        nc.sync.dma_start(
            out=wp_rows[:].rearrange("p (ob c) -> p ob c", c=C),
            in_=proj_w.rearrange("(ob p) c -> p ob c", p=P),
        )
        nc.sync.dma_start(out=adj_rows[:], in_=adj.rearrange("k j w -> j k w"))
        adj_dram = adj.rearrange("(m kk) (jj e) w -> kk jj m (e w)", kk=PAIR, e=PAIR)
        for kk in range(PAIR):
            nc.sync.dma_start(
                out=adj_pairs[kk * JOINTS : (kk + 1) * JOINTS, :, :, :].rearrange(
                    "jj m e w -> jj m (e w)"
                ),
                in_=adj_dram[kk],
            )
        load_graph_features(7)
        load_attention(6, 0)
        load_attention(6, 1)
        load_attention(7, 0)
        load_attention(7, 1)
        load_residuals(4)
        load_residuals(6)

        bias_g = keep.tile([P, KINDS, P, KINDS], BF16)
        bias_p = keep.tile([P, C], BF16)
        bias_cols = keep.tile([P, P], F32)

        def interleave_graph_bias():
            nc.vector.tensor_copy(
                out=bias_rows[0:CHUNKS, :].rearrange("n (c k) -> n c k", k=KINDS),
                in_=bias_raw[:].rearrange("n k c -> n c k"),
            )

        def stand_biases_up():
            stood_up = psum.tile([P, P], F32, tag="bank")
            nc.tensor.transpose(stood_up[:], bias_rows[:].bitcast(F32), ident[:])
            nc.scalar.copy(out=bias_cols[:], in_=stood_up[:])

        bias_parts = keep.tile([P, KINDS * KINDS], F32)

        def lay_bias_on_partitions():
            turned = psum.tile([P, P], BF16, tag="bank")
            nc.tensor.transpose(turned[:], bias_natural[:], ident_bf16[:])
            nc.scalar.copy(out=bias_parts[:], in_=turned[:, 0 : KINDS * KINDS])

        spread_banks = {}

        def spread_rows(row0, rows):
            spread = psum.tile([P, KINDS, P], F32, tag="bank")
            for n in range(rows):
                nc.tensor.transpose(
                    spread[:, n, :],
                    bias_cols[:, row0 + n : row0 + n + 1].to_broadcast([P, P]),
                    ident[:],
                )
            spread_banks[row0] = spread[:, 0:rows, :].rearrange("p n w -> p (n w)")

        def copy_graph_bias(cb0):
            nc.scalar.copy(
                out=bias_g[:, cb0 : cb0 + PAIR, :, :].rearrange("p i c k -> p (i c k)").bitcast(F32),
                in_=spread_banks[cb0 * PAIR],
            )

        def copy_projection_bias():
            nc.scalar.copy(out=bias_p[:].bitcast(F32), in_=spread_banks[CHUNKS])

        def quantise(values, codes, scales):
            nc.vector.quantize_mx(out=codes.bitcast(FP8X4), scales=scales, in_=values)

        mixed = keep.tile([P, STREAMS, B, P, PACK], BF16, align_bytes=64)
        mixed_codes = keep.tile([P, STREAMS, B, P], U32, align_bytes=64)
        mixed_scales = keep.tile([P, STREAMS, B, P], U8, align_bytes=64)

        def round_by_scalar(dst, product, factor):
            if factor == 1.0:
                nc.scalar.copy(out=dst, in_=product)
            else:
                nc.scalar.mul(out=dst, in_=product, mul=factor)

        def round_by_vector(dst, product, factor):
            if factor == 1.0:
                nc.vector.tensor_copy(out=dst, in_=product)
            else:
                nc.vector.tensor_scalar(out=dst, in0=product, scalar1=factor, scalar2=None, op0=MULT)

        mixed_banks = {}

        def mix(b, h):
            bank = psum.tile([P, PACK, STREAMS, JOINTS], F32, tag="bank")
            for t in range(PACK):
                half, parity = divmod(t, PACK // HALVES)
                first = half * (C // HALVES)
                nc.tensor.matmul(
                    out=bank[:, t, :, :].rearrange("q s i -> q (s i)"),
                    lhsT=streams[b][:, h, first + parity : first + C // HALVES : 2],
                    rhs=mixers[:, min(b, 1), :, :].rearrange("p s i -> p (s i)"),
                    start=True, stop=True,
                )
            mixed_banks[b, h] = bank[:].rearrange("q t s i -> q s i t")

        def round_mixed(b, h, rounder=round_by_scalar):
            joints = slice(h * JOINTS, (h + 1) * JOINTS)
            for s, factor in ((U, S_A2G), (V, 1.0)):
                rounder(mixed[:, s, b, joints, :], mixed_banks[b, h][:, s, :, :], factor)

        def quantise_stream(s, b0, b1):
            quantise(
                mixed[:, s, b0:b1, :, :].rearrange("q b j t -> q (b j t)"),
                mixed_codes[:, s, b0:b1, :].rearrange("q b r -> q (b r)"),
                mixed_scales[:, s, b0:b1, :].rearrange("q b r -> q (b r)"),
            )

        wg_turned = keep.tile([P, KINDS * C * PACK], BF16, align_bytes=64)
        wg_codes = keep.tile([P, KINDS * C], U32, align_bytes=64)
        wg_scales = keep.tile([P, KINDS * C], U8, align_bytes=64)
        wp_turned = keep.tile([P, C * PACK], BF16, align_bytes=64)
        wp_codes = keep.tile([P, C], U32, align_bytes=64)
        wp_scales = keep.tile([P, C], U8, align_bytes=64)
        adj_grouped = keep.tile([P, PAIR, P, KINDS], BF16, align_bytes=64)
        adj_codes = keep.tile([P, PAIR, P], U32, align_bytes=64)
        adj_scales = keep.tile([P, PAIR, P], U8, align_bytes=64)

        turned_banks = {}

        def turn_rows(rows, n):
            row_words = rows[:].bitcast(F32).rearrange("p (n w) -> p n w", w=C // 2)
            bank = psum.tile([P, PAIR, HALVES, P], F32, tag="bank")
            for i in range(PAIR):
                for h in range(HALVES):
                    nc.tensor.transpose(
                        bank[:, i, h, :], row_words[:, n + i, h * P : (h + 1) * P], ident[:]
                    )
            return bank[:].rearrange("q i h r -> q i r h")

        def copy_rows(turned, n, bank, copier):
            words = turned[:].bitcast(F32).rearrange("q (n r h) -> q n r h", r=P, h=HALVES)
            copier(out=words[:, n : n + PAIR, :, :], in_=bank)

        def turn_graph_weights(cb):
            for n in (cb * KINDS, cb * KINDS + PAIR):
                turned_banks[n] = turn_rows(wg_rows, n)

        def copy_graph_weights(cb, *copiers):
            for n, copier in zip((cb * KINDS, cb * KINDS + PAIR), copiers):
                copy_rows(wg_turned, n, turned_banks[n], copier)

        def quantise_graph_weights(cb):
            quantise(
                wg_turned[:, cb * C * PACK : (cb + 1) * C * PACK],
                wg_codes[:, cb * C : (cb + 1) * C],
                wg_scales[:, cb * C : (cb + 1) * C],
            )

        def turn_projection():
            for n in (0, PAIR):
                copy_rows(wp_turned, n, turn_rows(wp_rows, n), nc.scalar.copy)

        def group_adjacency(turned):
            if turned:
                values = adj_pairs[:].rearrange("p m e w -> p w (m e)")
            else:
                values = adj_rows[:].rearrange("j k w -> j w k")
            nc.scalar.copy(out=adj_grouped[:, turned, :, :], in_=values)

        def quantise_projection():
            quantise(wp_turned[:], wp_codes[:], wp_scales[:])

        def quantise_adjacency(turned):
            quantise(
                adj_grouped[:, turned, :, :].rearrange("j w k -> j (w k)"),
                adj_codes[:, turned, :], adj_scales[:, turned, :],
            )

        y_values = {}
        y_codes = {}
        y_scales = {}

        def open_pair(n):
            y_values[n] = flow.tile([P, PAIR, KINDS, P, KINDS], BF16, align_bytes=64, name="y_values")
            y_codes[n] = flow.tile([P, PAIR, C], U32, align_bytes=64, name="y_codes")
            y_scales[n] = flow.tile([P, PAIR, C], U8, align_bytes=64, name="y_scales")

        products = {}

        def multiply(b, cb):
            bank = psum.tile([P, KINDS, P], F32, tag="bank")
            nc.tensor.matmul_mx(
                out=bank[:].rearrange("j k c -> j (k c)"),
                lhsT=mixed_codes[:, U, b, :].bitcast(FP8X4),
                lhsT_scale=mixed_scales[:, U, b, :],
                rhs=wg_codes[:, cb * C : (cb + 1) * C].bitcast(FP8X4),
                rhs_scale=wg_scales[:, cb * C : (cb + 1) * C],
                start=True,
                stop=True,
            )
            products[b, cb] = bank[:].rearrange("j k c -> j c k")

        def add_by_vector(b, cb):
            n, i = divmod(b, PAIR)
            nc.vector.tensor_tensor(
                out=y_values[n][:, i, cb, :, :], in0=products[b, cb], in1=bias_g[:, cb, :, :],
                op=ADD,
            )

        def add_by_gpsimd(b, cb):
            n, i = divmod(b, PAIR)
            copied = flow.tile([P, P, KINDS], F32, name="copied")
            nc.scalar.copy(out=copied[:], in_=products[b, cb])
            nc.gpsimd.tensor_tensor(
                out=y_values[n][:, i, cb, :, :], in0=copied[:], in1=bias_g[:, cb, :, :], op=ADD
            )

        column_banks = {}
        column_values = {}
        row_banks = {}

        def multiply_columns(n, cb):
            batches = slice(n * PAIR, (n + 1) * PAIR)
            for m in range(PAIR):
                bank = psum.tile([P, PAIR, PAIR, P], F32, tag="bank")
                for kk in range(PAIR):
                    first = (cb * KINDS + m * PAIR + kk) * P
                    nc.tensor.matmul_mx(
                        out=bank[:, kk, :, :].rearrange("c b j -> c (b j)"),
                        lhsT=wg_codes[:, first : first + P].bitcast(FP8X4),
                        lhsT_scale=wg_scales[:, first : first + P],
                        rhs=mixed_codes[:, U, batches, :].rearrange("q b j -> q (b j)").bitcast(FP8X4),
                        rhs_scale=mixed_scales[:, U, batches, :].rearrange("q b j -> q (b j)"),
                        start=True,
                        stop=True,
                    )
                column_banks[n, cb, m] = bank

        def add_on_columns(n, cb):
            values = flow.tile([P, PAIR, PAIR, PAIR, P], BF16, name="column_values")
            for kk in range(PAIR):
                for m in range(PAIR):
                    k = m * PAIR + kk
                    nc.scalar.activation(
                        out=values[:, m, :, kk, :], in_=column_banks[n, cb, m][:, kk, :, :],
                        func=IDENTITY,
                        bias=bias_parts[:, k * KINDS + cb : k * KINDS + cb + 1], scale=1.0,
                    )
            column_values[n, cb] = values

        def turn_columns(n, cb):
            words = column_values[n, cb][:].rearrange("c m b kk j -> c m b (kk j)").bitcast(F32)
            bank = psum.tile([P, PAIR, PAIR, P], F32, tag="bank")
            for i in range(PAIR):
                for m in range(PAIR):
                    nc.tensor.transpose(bank[:, i, m, :], words[:, m, i, :], ident[:])
            row_banks[n, cb] = bank[:].rearrange("p b m c -> p b c m")

        def copy_columns(n, cb, copier):
            for i in range(PAIR):
                copier(
                    out=y_values[n][:, i, cb, :, :].bitcast(F32), in_=row_banks[n, cb][:, i, :, :]
                )

        def quantise_y(b, cb0=0, cb1=KINDS):
            n, i = divmod(b, PAIR)
            columns = slice(cb0 * P, cb1 * P)
            quantise(
                y_values[n][:, i, cb0:cb1, :, :].rearrange("j cb c k -> j (cb c k)"),
                y_codes[n][:, i, columns],
                y_scales[n][:, i, columns],
            )

        residuals = {}

        def make_residual(b):
            residuals[b] = flow.tile([P, C], F32, name="residual")
            nc.gpsimd.tensor_tensor(
                out=residuals[b][:], in0=x_rows[:, b, :], in1=bias_p[:], op=ADD
            )

        totals = {}

        def open_total(b):
            totals[b] = psum.tile([P, C], F32, tag="bank", name="total")

        def aggregate(b, cb0, cb1, turned):
            n, i = divmod(b, PAIR)
            columns = slice(cb0 * P, cb1 * P)
            nc.tensor.matmul_mx(
                out=totals[b][:, columns],
                lhsT=mixed_codes[:, V, b, :].bitcast(FP8X4),
                lhsT_scale=mixed_scales[:, V, b, :],
                rhs=wp_codes[:, columns].bitcast(FP8X4),
                rhs_scale=wp_scales[:, columns],
                start=True,
                stop=False,
            )
            nc.tensor.matmul_mx(
                out=totals[b][:, columns],
                lhsT=adj_codes[:, turned, :].bitcast(FP8X4),
                lhsT_scale=adj_scales[:, turned, :],
                rhs=y_codes[n][:, i, columns].bitcast(FP8X4),
                rhs_scale=y_scales[n][:, i, columns],
                start=False,
                stop=True,
            )

        def aggregate_all(b):
            open_total(b)
            straight = STRAIGHT[b // PAIR]
            for cb0, cb1 in SPANS[straight]:
                aggregate(b, cb0, cb1, 0 if cb0 < straight else 1)

        def finish(b, cb0=0, cb1=KINDS):
            columns = slice(cb0 * P, cb1 * P)
            result = flow.tile([P, C], F32, name="result", bufs=B)
            nc.vector.tensor_tensor(
                out=result[:, columns], in0=totals[b][:, columns],
                in1=residuals[b][:, columns], op=ADD,
            )
            nc.sync.dma_start(out=out[b][:, columns], in_=result[:, columns])

        VC, SC = nc.vector.tensor_copy, nc.scalar.copy
        mix(0, 0)
        mix(0, 1)
        interleave_graph_bias()
        round_mixed(0, 0)
        round_mixed(0, 1, round_by_vector)
        stand_biases_up()
        turn_graph_weights(0)
        quantise_stream(U, 0, 1)
        copy_graph_weights(0, SC, VC)
        spread_rows(0, 4)
        quantise_graph_weights(0)
        copy_graph_bias(0)
        mix(1, 0)
        mix(1, 1)
        round_mixed(1, 0)
        round_mixed(1, 1, round_by_vector)
        for n in (0, 1):
            open_pair(n)
        multiply(0, 0)
        turn_graph_weights(1)
        copy_graph_weights(1, SC, SC)
        quantise_stream(U, 1, 2)
        multiply(1, 0)
        add_by_vector(0, 0)
        quantise_stream(V, 0, 2)
        mix(2, 0)
        mix(2, 1)
        round_mixed(2, 0)
        round_mixed(2, 1)
        add_by_vector(1, 0)
        quantise_graph_weights(1)
        turn_graph_weights(2)
        copy_graph_weights(2, SC, SC)
        quantise_stream(U, 2, 3)
        multiply(0, 1)
        multiply(1, 1)
        multiply(2, 0)
        multiply(2, 1)
        spread_rows(4, 4)
        spread_rows(8, 2)
        quantise_stream(V, 2, 3)
        add_by_vector(0, 1)
        copy_graph_bias(2)
        copy_projection_bias()
        lay_bias_on_partitions()
        mix(3, 0)
        mix(3, 1)
        round_mixed(3, 0)
        round_mixed(3, 1)
        add_by_vector(1, 1)
        quantise_graph_weights(2)
        add_by_vector(2, 0)
        turn_graph_weights(3)
        copy_graph_weights(3, SC, SC)
        add_by_vector(2, 1)
        multiply(0, 2)
        multiply(1, 2)
        quantise_stream(V, 3, 4)
        quantise_stream(U, 3, 4)
        multiply(2, 2)
        add_by_vector(0, 2)
        multiply(3, 0)
        multiply(3, 1)
        add_by_vector(1, 2)
        mix(4, 0)
        mix(4, 1)
        quantise_graph_weights(3)
        multiply(3, 2)
        add_by_vector(2, 2)
        multiply(0, 3)
        round_mixed(4, 0)
        round_mixed(4, 1)
        add_by_vector(3, 0)
        mix(5, 0)
        mix(5, 1)
        multiply(1, 3)
        make_residual(0)
        make_residual(1)
        make_residual(2)
        make_residual(3)
        add_by_vector(3, 1)
        multiply(2, 3)
        round_mixed(5, 0)
        round_mixed(5, 1)
        add_by_vector(3, 2)
        multiply(3, 3)
        group_adjacency(0)
        turn_projection()
        add_by_vector(0, 3)
        quantise_stream(U, 4, 6)
        add_by_vector(1, 3)
        open_pair(2)
        multiply_columns(2, 2)
        add_by_vector(2, 3)
        multiply_columns(2, 3)
        add_by_vector(3, 3)
        add_on_columns(2, 2)
        multiply(4, 0)
        add_on_columns(2, 3)
        group_adjacency(1)

        mix(6, 0)
        mix(6, 1)
        quantise_y(0)
        round_mixed(6, 0)
        round_mixed(6, 1)
        multiply(5, 0)
        mix(7, 0)
        mix(7, 1)
        quantise_y(1)
        round_mixed(7, 0)
        round_mixed(7, 1)
        turn_columns(2, 2)
        turn_columns(2, 3)
        quantise_y(2)
        copy_columns(2, 2, SC)
        copy_columns(2, 3, SC)
        quantise_y(3)
        multiply(4, 1)
        quantise_projection()
        quantise_adjacency(0)
        quantise_adjacency(1)
        multiply(5, 1)
        aggregate_all(0)
        aggregate_all(1)
        add_by_vector(4, 0)
        add_by_vector(5, 0)
        aggregate_all(2)
        add_by_vector(4, 1)
        quantise_stream(U, 6, 8)
        open_pair(3)
        multiply_columns(3, 3)
        finish(0)
        make_residual(4)
        quantise_stream(V, 4, 8)
        finish(1)
        aggregate_all(3)
        make_residual(5)
        multiply_columns(3, 2)
        add_on_columns(3, 3)
        add_by_vector(5, 1)
        add_on_columns(3, 2)
        finish(2)
        make_residual(6)
        multiply(6, 0)
        multiply(7, 0)
        finish(3)
        make_residual(7)
        quantise_y(4)
        multiply_columns(3, 1)
        add_by_vector(6, 0)
        turn_columns(3, 3)
        turn_columns(3, 2)
        add_on_columns(3, 1)
        aggregate_all(4)
        quantise_y(5)
        add_by_vector(7, 0)
        copy_columns(3, 3, SC)
        turn_columns(3, 1)
        aggregate_all(5)
        finish(4)
        copy_columns(3, 2, SC)
        copy_columns(3, 1, SC)
        quantise_y(6, 0, 1)
        quantise_y(7, 0, 1)
        quantise_y(6, 2, 4)
        open_total(6)
        aggregate(6, 0, 1, 0)
        aggregate(6, 2, 4, 1)
        quantise_y(7, 2, 4)
        open_total(7)
        aggregate(7, 0, 1, 0)
        aggregate(7, 2, 4, 1)
        quantise_y(6, 1, 2)
        aggregate(6, 1, 2, 1)
        quantise_y(7, 1, 2)
        aggregate(7, 1, 2, 1)
        finish(5)
        finish(6)
        finish(7, 0, PAIR)
        finish(7, PAIR, KINDS)
